import numpy as np
import ml_dtypes


def mxq(x, axis, fmt="e4m3"):
    dtype, down = {"e4m3": (ml_dtypes.float8_e4m3fn, 7), "e5m2": (ml_dtypes.float8_e5m2, 14)}[fmt]
    v = np.moveaxis(np.asarray(x, np.float32).astype(ml_dtypes.bfloat16).astype(np.float64), axis, -1)
    blocks = v.reshape(v.shape[:-1] + (-1, 32))
    amax = np.abs(blocks).max(-1, keepdims=True)
    byte = np.maximum(np.where(amax > 0, np.frexp(amax)[1] - 1 + 127, 0) - down, 1)
    scale = np.exp2(byte - 127.0)
    codes = (blocks / scale).astype(np.float32).astype(dtype).astype(np.float64)
    return np.moveaxis((codes * scale).reshape(v.shape), -1, axis)


WIDE = False


def mx_kscale(k):
    if not WIDE:
        return np.ones(k)
    levels = np.array([10, -10, 5, -5, 0])
    if k % 512:
        return np.exp2(np.random.permutation(np.resize(levels, k // 32))).repeat(32)
    a = np.empty((k // 512, 16))
    for p in range(k // 512):
        a[p, :8] = np.random.permutation(np.resize(levels, 8))
        for g in range(8):
            far = levels[np.abs(levels - a[p, g]) >= 10]
            a[p, g + 8] = far[np.random.randint(len(far))]
    return np.exp2(a.ravel()).repeat(32)


BF16 = ml_dtypes.bfloat16


def bf(x):
    return np.asarray(x, np.float32).astype(BF16)


def f64(x):
    return np.asarray(x).astype(np.float64)


B, C, H, W, O, KH, KW, PH, PW, T, R = 4, 1024, 7, 7, 512, 2, 2, 1, 1, 8, 64
HO, WO = H + PH + PH - KH + 1, W + PW + PW - KW + 1
N = B * HO * WO
D = C * KH * KW
R2 = R * KH * KW
K1, K2 = T * R, T * R2


def draw0():
    s, t1, t2 = mx_kscale(D), mx_kscale(K1).reshape(T, R), mx_kscale(K2).reshape(T, R2)
    return {"xw": bf(np.random.standard_normal((N, D)) * s),
            "S1s": bf(np.random.standard_normal((T, D, R)) / np.sqrt(D) / s[None, :, None] * t1[:, None, :]),
            "U1s": bf(np.random.standard_normal((T, R, O)) * T / np.sqrt(K1) / t1[:, :, None]),
            "U2s": bf(np.random.standard_normal((T, R2, D)) / np.sqrt(D) / s[None, None, :] * t2[:, :, None]),
            "S2s": bf(np.random.standard_normal((T, R2, O)) * T / np.sqrt(K2) / t2[:, :, None]),
            "bias": bf(np.random.standard_normal(O) * 0.3)}


def core(xw, S1s, U1s, U2s, S2s, bias):
    xq = mxq(f64(xw), 1, "e4m3")
    s1 = f64(S1s).transpose(1, 0, 2).reshape(D, K1)
    h1 = xq @ mxq(s1, 0, "e4m3")
    out1 = (mxq(h1, 1, "e4m3") @ mxq(f64(U1s).reshape(K1, O), 0, "e4m3")) / T + f64(bias)
    u2 = f64(U2s).reshape(K2, D)
    h2 = xq @ mxq(u2, 1, "e4m3").T
    out2 = (mxq(h2, 1, "e4m3") @ mxq(f64(S2s).reshape(K2, O), 0, "e4m3")) / T
    out = out1 + out2 + f64(bias)
    return out.reshape(B, HO, WO, O).transpose(0, 3, 1, 2)


def e4m3fn_bytes(y):
    return np.clip(np.asarray(y, np.float64), -448.0, 448.0).astype(np.float32).astype(ml_dtypes.float8_e4m3fn).view(np.uint8)


def e4m3fn_values(b):
    return np.asarray(b, np.uint8).view(ml_dtypes.float8_e4m3fn).astype(np.float64)


def setup_inputs():
    d = draw0()
    x0 = np.asarray(d['xw']).astype(np.float64)
    s = (np.max(np.abs(x0), axis=(0,), keepdims=True) / 448.0).astype(np.float32)
    out = {}
    for k, v in d.items():
        if k == 'xw':
            out['xw_bytes'] = e4m3fn_bytes(x0 / s.astype(np.float64))
            out['xw_scale'] = s
        else:
            out[k] = v
    return out


def reference(xw_bytes, xw_scale, S1s, U1s, U2s, S2s, bias):
    return core(e4m3fn_values(xw_bytes) * xw_scale.astype(np.float64), S1s, U1s, U2s, S2s, bias)

@@ -1,0 +1,320 @@
+from contextlib import ExitStack
+
+import concourse.mybir as mybir
+from concourse.masks import make_identity
+
+F32 = mybir.dt.float32
+BF16 = mybir.dt.bfloat16
+U32 = mybir.dt.uint32
+U8 = mybir.dt.uint8
+FP8 = mybir.dt.float8_e4m3fn
+FP8X4 = mybir.dt.float8_e4m3fn_x4
+MULT = mybir.AluOpType.mult
+ADD = mybir.AluOpType.add
+IDENTITY = mybir.ActivationFunctionType.Identity
+
+P = 128
+N = 256
+D = 4096
+O = 512
+K1 = 512
+K2 = 2048
+GD = D // 512
+G2 = K2 // 512
+TILES = K2 // P
+SEQ = [0, 2, 4, 1, 3, 5] + list(range(6, 16))
+
+FLOPS = 2 * N * D * (K1 + K2) + 2 * N * (K1 + K2) * O
+
+
+def tile_skconv2d_pa_kernel(tc, xw_bytes, xw_scale, S1s, U1s, U2s, S2s, bias, out):
+    nc = tc.nc
+
+    with ExitStack() as ctx:
+        const = ctx.enter_context(tc.tile_pool(name="const", bufs=1))
+        keep = ctx.enter_context(tc.tile_pool(name="keep", bufs=1))
+        pool = ctx.enter_context(tc.tile_pool(name="pool", bufs=2))
+        psum = ctx.enter_context(tc.psum_pool(name="psum", bufs=2))
+        ctx.enter_context(tc.manual_schedule())
+
+        u2_rows = U2s.rearrange("t r d -> (t r) d").rearrange("(g p t) d -> g t p d", p=P, t=4)
+        s1_rows = S1s.rearrange("t (g p j) r -> g p t (j r)", p=P, j=4)
+        s2_rows = S2s.rearrange("t r o -> (t r) o").rearrange("(g p j) o -> g p (j o)", p=P, j=4)
+        u1_rows = U1s.rearrange("t r o -> (t r) o").rearrange("(g p j) o -> g p (j o)", p=P, j=4)
+
+        ident = const.tile([P, P], F32, name="ident", align_bytes=64)
+        make_identity(nc, ident[:])
+        x_scale = const.tile([P, GD, 4], F32, name="x_scale", align_bytes=64)
+        bias_in = const.tile([P, 4], BF16, name="bias_in", align_bytes=64)
+
+        u2_raw = {}
+
+        def load_u2(i, pieces=1):
+            raw = pool.tile([P, D], BF16, name="u2_raw", bufs=5, align_bytes=64)
+            w = D // pieces
+            for c in range(pieces):
+                nc.sync.dma_start(out=raw[:, c * w : (c + 1) * w], in_=u2_rows[i // 4, i % 4][:, c * w : (c + 1) * w])
+            u2_raw[i] = raw
+
+        w_raw = {}
+
+        def load_w(c):
+            raw = pool.tile([P, 2048], BF16, name="w_raw", bufs=3, align_bytes=64)
+            if c < 8:
+                nc.sync.dma_start(out=raw[:].rearrange("p (t x) -> p t x", t=8), in_=s1_rows[c])
+            elif c < 12:
+                nc.sync.dma_start(out=raw[:], in_=s2_rows[c - 8])
+            else:
+                nc.sync.dma_start(out=raw[:], in_=u1_rows[0])
+            w_raw[c] = raw
+
+        load_u2(SEQ[0], 4)
+        x_in = []
+        for h in range(2):
+            xi = keep.tile([P, D], U8, name="x_in%d" % h, align_bytes=64)
+            nc.sync.dma_start(out=xi[:], in_=xw_bytes[h * P : (h + 1) * P, :])
+            x_in.append(xi)
+        nc.sync.dma_start(out=x_scale[:], in_=xw_scale.rearrange("o (g p t) -> p (o g) t", p=P, t=4))
+        load_u2(SEQ[1], 2)
+        for i in range(2, 5):
+            load_u2(SEQ[i])
+        nc.sync.dma_start(out=bias_in[:], in_=bias.rearrange("(p m) -> p m", m=4))
+
+        x_bf = [keep.tile([P, D], BF16, name="x_bf%d" % h, align_bytes=64) for h in range(2)]
+        x_codes = keep.tile([P, GD, N], U32, name="x_codes", align_bytes=64)
+        x_scales = keep.tile([P, GD, N], U8, name="x_scales", align_bytes=64)
+        for q, h in [(0, 0), (0, 1), (1, 0), (1, 1), (2, 0), (2, 1), (3, 0), (3, 1)]:
+            cols = slice(q * 1024, (q + 1) * 1024)
+            nc.vector.tensor_copy(out=x_bf[h][:, cols], in_=x_in[h][:, cols].bitcast(FP8))
+
+        x_grp = {}
+
+        def turn_x(g):
+            xt = psum.tile([P, 2, N], F32, name="tp", bufs=5)
+            for h in range(2):
+                words = x_bf[h][:].bitcast(F32)
+                for u in range(2):
+                    nc.tensor.transpose(
+                        xt[:, u, h * P : (h + 1) * P], words[:, 256 * g + u : 256 * (g + 1) : 2], ident[:]
+                    )
+            if g % 2 == 0:
+                x_grp[g // 2] = pool.tile([P, 2, N, 4], BF16, name="x_grp", bufs=2, align_bytes=64)
+            grp = x_grp[g // 2]
+            sc = x_scale[:, g : g + 1, :].rearrange("p o (u e) -> p o u e", u=2)
+            nc.vector.tensor_tensor(
+                out=grp[:, g % 2].rearrange("p n (u e) -> p n u e", u=2),
+                in0=xt[:].rearrange("p u n -> p (u n)").bitcast(BF16).rearrange("p (u n e) -> p n u e", u=2, e=2),
+                in1=sc.to_broadcast([P, N, 2, 2]),
+                op=MULT,
+            )
+
+        def quant_x(b):
+            nc.vector.quantize_mx(
+                out=x_codes[:, 2 * b : 2 * b + 2, :].rearrange("p g n -> p (g n)").bitcast(FP8X4),
+                scales=x_scales[:, 2 * b : 2 * b + 2, :].rearrange("p g n -> p (g n)"),
+                in_=x_grp[b][:].rearrange("p g n t -> p (g n t)"),
+            )
+
+        u2_grp = {}
+        u2_codes = {}
+
+        def turn_u2(i, b):
+            if b == 0:
+                u2_grp[i] = pool.tile([P, GD, P, 4], BF16, name="u2_grp", bufs=4, align_bytes=64)
+            words = u2_raw[i][:].bitcast(F32)
+            ut = psum.tile([P, 2, 2, P], F32, name="tp", bufs=5)
+            for s in range(2):
+                g = 2 * b + s
+                for u in range(2):
+                    nc.tensor.transpose(ut[:, s, u, :], words[:, 256 * g + u : 256 * (g + 1) : 2], ident[:])
+            nc.scalar.copy(
+                out=u2_grp[i][:, 2 * b : 2 * b + 2].rearrange("p g n t -> p (g n t)").bitcast(F32)
+                .rearrange("p (g n u) -> p g n u", g=2, u=2),
+                in_=ut[:].rearrange("p g u n -> p g n u"),
+            )
+
+        def quant_u2(i):
+            codes = pool.tile([P, GD, P], U32, name="u2_codes", bufs=5, align_bytes=64)
+            scales = pool.tile([P, GD, P], U8, name="u2_scales", bufs=5, align_bytes=64)
+            nc.vector.quantize_mx(
+                out=codes[:].rearrange("p g n -> p (g n)").bitcast(FP8X4),
+                scales=scales[:].rearrange("p g n -> p (g n)"),
+                in_=u2_grp[i][:].rearrange("p g n t -> p (g n t)"),
+            )
+            u2_codes[i] = (codes, scales)
+
+        w_codes = [keep.tile([P, 512], U32, name="w_codes%d" % c, align_bytes=64) for c in range(13)]
+        w_scales = [keep.tile([P, 512], U8, name="w_scales%d" % c, align_bytes=64) for c in range(13)]
+        w_grp = {}
+
+        def copy_w(c):
+            grp = pool.tile([P, 2048], BF16, name="w_grp", bufs=2, align_bytes=64)
+            if c < 8:
+                nc.vector.tensor_copy(
+                    out=grp[:].rearrange("p (q t r j) -> p q t r j", q=4, t=8, j=4),
+                    in_=w_raw[c][:].rearrange("p (t j r q) -> p q t r j", t=8, j=4, q=4),
+                )
+            else:
+                nc.scalar.copy(
+                    out=grp[:].rearrange("p (q m j) -> p q m j", q=4, j=4),
+                    in_=w_raw[c][:].rearrange("p (j m q) -> p q m j", j=4, q=4),
+                )
+            w_grp[c] = grp
+
+        def quant_w(c):
+            nc.vector.quantize_mx(out=w_codes[c][:].bitcast(FP8X4), scales=w_scales[c][:], in_=w_grp[c][:])
+
+        h_bank = {}
+        h_grp = {}
+        h_codes = [keep.tile([P, N], U32, name="h_codes%d" % g, align_bytes=64) for g in range(5)]
+        h_scales = [keep.tile([P, N], U8, name="h_scales%d" % g, align_bytes=64) for g in range(5)]
+
+        def multiply(group, t, lhs, passes=range(GD)):
+            if (group, t // 2) not in h_bank:
+                h_bank[group, t // 2] = psum.tile([P, 2, N], F32, name="hp", bufs=3)
+            bank = h_bank[group, t // 2]
+            for g in passes:
+                codes, scales = lhs(g)
+                nc.tensor.matmul_mx(
+                    out=bank[:, t % 2, :],
+                    lhsT=codes.bitcast(FP8X4),
+                    lhsT_scale=scales,
+                    rhs=x_codes[:, g, :].bitcast(FP8X4),
+                    rhs_scale=x_scales[:, g, :],
+                    start=(g == 0),
+                    stop=(g == GD - 1),
+                )
+
+        def multiply_u2(i, passes=range(GD)):
+            codes, scales = u2_codes[i]
+            multiply(i // 4, i % 4, lambda g: (codes[:, g, :], scales[:, g, :]), passes)
+
+        def multiply_s1(t):
+            cols = slice(t * P, (t + 1) * P)
+            multiply(4, t, lambda g: (w_codes[g][:, cols], w_scales[g][:, cols]))
+
+        def empty_h(group, half):
+            if half == 0:
+                h_grp[group] = pool.tile([P, N, 4], BF16, name="h_grp", bufs=2, align_bytes=64)
+            nc.scalar.copy(
+                out=h_grp[group][:, :, 2 * half : 2 * half + 2],
+                in_=h_bank[group, half][:].rearrange("p t n -> p n t"),
+            )
+
+        def quant_h(group):
+            nc.vector.quantize_mx(
+                out=h_codes[group][:].bitcast(FP8X4),
+                scales=h_scales[group][:],
+                in_=h_grp[group][:].rearrange("p n t -> p (n t)"),
+            )
+
+        a, b_, c_ = SEQ[:3]
+        banks = [(SEQ[n // 4], n % 4) for n in range(4, 20)]
+        for b in range(4):
+            turn_u2(a, b)
+
+        def head(g):
+            turn_x(g)
+            for i, b in banks[2 * g : 2 * g + 2]:
+                turn_u2(i, b)
+
+        head(0)
+        head(1)
+        head(2)
+        quant_x(0)
+        head(3)
+        quant_u2(a)
+        quant_x(1)
+        multiply_u2(a, range(0, 2))
+        head(4)
+        multiply_u2(a, range(2, 4))
+        head(5)
+        quant_u2(b_)
+        quant_x(2)
+        load_u2(SEQ[5])
+        head(6)
+        multiply_u2(b_, range(0, 4))
+        head(7)
+        quant_u2(c_)
+        quant_x(3)
+        multiply_u2(a, range(4, 6))
+        multiply_u2(b_, range(4, 6))
+        multiply_u2(c_, range(0, 6))
+        load_u2(SEQ[6])
+        load_w(0)
+        load_w(8)
+        quant_u2(SEQ[3])
+        for i in (a, b_, c_):
+            multiply_u2(i, range(6, 8))
+        copy_w(0)
+
+        chunks = [0, 8, 1, 2, 9, 3, 4, 10, 5, 6, 11, 7, 12]
+        at = 1
+        copied = [0]
+        group_done = []
+        for s in range(3, TILES):
+            load_w(chunks[at + 1]) if at + 1 < 13 else None
+            if s + 4 < TILES:
+                load_u2(SEQ[s + 4])
+            if s + 2 < TILES:
+                for b in range(4):
+                    turn_u2(SEQ[s + 2], b)
+            if s + 1 < TILES:
+                quant_u2(SEQ[s + 1])
+            if copied:
+                quant_w(copied.pop())
+            while group_done:
+                quant_h(group_done.pop())
+            if at < 13:
+                copy_w(chunks[at])
+                copied.append(chunks[at])
+                at += 1
+            if s == 15:
+                for t in range(4):
+                    multiply_s1(t)
+                    if t % 2 == 1:
+                        empty_h(4, t // 2)
+            i = SEQ[s]
+            multiply_u2(i)
+            if i % 2 == 1:
+                empty_h(i // 4, (i % 4) // 2)
+                if i % 4 == 3:
+                    group_done.append(i // 4)
+        quant_h(4)
+        quant_h(3)
+
+        bias2 = const.tile([P, 4], F32, name="bias2", align_bytes=64)
+        nc.vector.tensor_scalar(out=bias2[:], in0=bias_in[:], scalar1=2.0, scalar2=None, op0=MULT)
+        order = [(4, 12), (0, 8), (1, 9), (2, 10), (3, 11)]
+        acc = [psum.tile([P, 512], F32, name="tp", bufs=5) for m in range(4)]
+
+        def second(m, n):
+            group, w = order[n]
+            nc.tensor.matmul_mx(
+                out=acc[m][:, :N],
+                lhsT=w_codes[w][:, m * P : (m + 1) * P].bitcast(FP8X4),
+                lhsT_scale=w_scales[w][:, m * P : (m + 1) * P],
+                rhs=h_codes[group][:].bitcast(FP8X4),
+                rhs_scale=h_scales[group][:],
+                start=(n == 0),
+                stop=(n == 4),
+            )
+
+        for m in range(4):
+            for n in range(4):
+                second(m, n)
+        result = keep.tile([P, 4, 4, 64], F32, name="result", align_bytes=64)
+        out_view = out.rearrange("b (p m) i j -> p b m (i j)", m=4)
+        for m in range(4):
+            second(m, 4)
+        for m in range(4):
+            src = acc[m][:, :N].rearrange("p (b s) -> p b s", b=4)
+            if m % 2 == 0:
+                nc.scalar.activation(
+                    out=result[:, :, m, :], in_=src, func=IDENTITY, bias=bias2[:, m : m + 1], scale=0.125
+                )
+            else:
+                nc.vector.tensor_scalar(
+                    out=result[:, :, m, :], in0=src, scalar1=0.125, scalar2=bias2[:, m : m + 1], op0=MULT, op1=ADD
+                )
+                nc.sync.dma_start(out=out_view[:, :, m - 1 : m + 1, :], in_=result[:, :, m - 1 : m + 1, :])

@@ -20,9 +20,13 @@ O = 512
 K1 = 512
 K2 = 2048
 GD = D // 512
-G2 = K2 // 512
-TILES = K2 // P
-SEQ = [0, 2, 4, 1, 3, 5] + list(range(6, 16))
+UNITS = 16
+HEAD = 4
+SORTED = 2
+X_MM = 2
+X_PAR = 2
+SORT_ON_SCALAR = ()
+S1_FIRST = 4
 
 FLOPS = 2 * N * D * (K1 + K2) + 2 * N * (K1 + K2) * O
 
@@ -37,29 +41,45 @@ def tile_skconv2d_pa_kernel(tc, xw_bytes, xw_scale, S1s, U1s, U2s, S2s, bias, ou
         psum = ctx.enter_context(tc.psum_pool(name="psum", bufs=2))
         ctx.enter_context(tc.manual_schedule())
 
-        u2_rows = U2s.rearrange("t r d -> (t r) d").rearrange("(g p t) d -> g t p d", p=P, t=4)
+        u2_rows = U2s.rearrange("t r d -> (t r) d").rearrange("(g p t) d -> g p t d", p=P, t=4)
         s1_rows = S1s.rearrange("t (g p j) r -> g p t (j r)", p=P, j=4)
         s2_rows = S2s.rearrange("t r o -> (t r) o").rearrange("(g p j) o -> g p (j o)", p=P, j=4)
         u1_rows = U1s.rearrange("t r o -> (t r) o").rearrange("(g p j) o -> g p (j o)", p=P, j=4)
+        x_rows = xw_bytes.rearrange("(h p) d -> p h d", p=P)
 
         ident = const.tile([P, P], F32, name="ident", align_bytes=64)
         make_identity(nc, ident[:])
+        ident_bf = const.tile([P, P], BF16, name="ident_bf", align_bytes=64)
+        make_identity(nc, ident_bf[:])
+        ones = const.tile([P, 1], F32, name="ones", align_bytes=64)
+        nc.vector.memset(ones[:], 1.0)
         x_scale = const.tile([P, GD, 4], F32, name="x_scale", align_bytes=64)
         bias_in = const.tile([P, 4], BF16, name="bias_in", align_bytes=64)
 
         u2_raw = {}
-
-        def load_u2(i, pieces=1):
-            raw = pool.tile([P, D], BF16, name="u2_raw", bufs=5, align_bytes=64)
-            w = D // pieces
-            for c in range(pieces):
-                nc.sync.dma_start(out=raw[:, c * w : (c + 1) * w], in_=u2_rows[i // 4, i % 4][:, c * w : (c + 1) * w])
-            u2_raw[i] = raw
-
+        x_in = {}
         w_raw = {}
 
+        def load_u2(i, pieces=1):
+            raw = pool.tile([P, D], BF16, name="u2_raw", bufs=6, align_bytes=64)
+            if i < HEAD:
+                k = 4 // pieces
+                for c in range(pieces):
+                    nc.sync.dma_start(
+                        out=raw[:, c * k * 1024 : (c + 1) * k * 1024].rearrange("p (t d) -> p t d", t=k),
+                        in_=u2_rows[0][:, c * k : (c + 1) * k, i * 1024 : (i + 1) * 1024],
+                    )
+            else:
+                nc.sync.dma_start(out=raw[:], in_=u2_rows[i // 4][:, i % 4, :])
+            u2_raw[i] = raw
+
+        def load_x(b):
+            xi = keep.tile([P, 2, 1024], U8, name="x_in%d" % b, align_bytes=64)
+            nc.sync.dma_start(out=xi[:], in_=x_rows[:, :, b * 1024 : (b + 1) * 1024])
+            x_in[b] = xi
+
         def load_w(c):
-            raw = pool.tile([P, 2048], BF16, name="w_raw", bufs=3, align_bytes=64)
+            raw = pool.tile([P, 2048], BF16, name="w_raw", bufs=4, align_bytes=64)
             if c < 8:
                 nc.sync.dma_start(out=raw[:].rearrange("p (t x) -> p t x", t=8), in_=s1_rows[c])
             elif c < 12:
@@ -68,45 +88,77 @@ def tile_skconv2d_pa_kernel(tc, xw_bytes, xw_scale, S1s, U1s, U2s, S2s, bias, ou
                 nc.sync.dma_start(out=raw[:], in_=u1_rows[0])
             w_raw[c] = raw
 
-        load_u2(SEQ[0], 4)
-        x_in = []
-        for h in range(2):
-            xi = keep.tile([P, D], U8, name="x_in%d" % h, align_bytes=64)
-            nc.sync.dma_start(out=xi[:], in_=xw_bytes[h * P : (h + 1) * P, :])
-            x_in.append(xi)
-        nc.sync.dma_start(out=x_scale[:], in_=xw_scale.rearrange("o (g p t) -> p (o g) t", p=P, t=4))
-        load_u2(SEQ[1], 2)
-        for i in range(2, 5):
-            load_u2(SEQ[i])
-        nc.sync.dma_start(out=bias_in[:], in_=bias.rearrange("(p m) -> p m", m=4))
-
-        x_bf = [keep.tile([P, D], BF16, name="x_bf%d" % h, align_bytes=64) for h in range(2)]
         x_codes = keep.tile([P, GD, N], U32, name="x_codes", align_bytes=64)
         x_scales = keep.tile([P, GD, N], U8, name="x_scales", align_bytes=64)
-        for q, h in [(0, 0), (0, 1), (1, 0), (1, 1), (2, 0), (2, 1), (3, 0), (3, 1)]:
-            cols = slice(q * 1024, (q + 1) * 1024)
-            nc.vector.tensor_copy(out=x_bf[h][:, cols], in_=x_in[h][:, cols].bitcast(FP8))
-
+        x_bf = {}
         x_grp = {}
+        x_bank = {}
 
-        def turn_x(g):
-            xt = psum.tile([P, 2, N], F32, name="tp", bufs=5)
-            for h in range(2):
-                words = x_bf[h][:].bitcast(F32)
-                for u in range(2):
-                    nc.tensor.transpose(
-                        xt[:, u, h * P : (h + 1) * P], words[:, 256 * g + u : 256 * (g + 1) : 2], ident[:]
+        def widen_x(b, h):
+            wide = pool.tile([P, 1024], BF16, name="x_bf", bufs=8, align_bytes=64)
+            src = x_in[b][:, h, :].bitcast(FP8)
+            if b < X_MM:
+                nc.vector.tensor_scalar(
+                    out=wide[:].rearrange("p (s t m) -> p s m t", s=2, t=4),
+                    in0=src.rearrange("p (s m t) -> p s m t", s=2, t=4),
+                    scalar1=ones[:],
+                    scalar2=None,
+                    op0=MULT,
+                )
+            elif b < X_PAR:
+                nc.vector.tensor_scalar(
+                    out=wide[:].rearrange("p (s u m e) -> p s m u e", s=2, u=2, e=2),
+                    in0=src.rearrange("p (s m u e) -> p s m u e", s=2, u=2, e=2),
+                    scalar1=ones[:],
+                    scalar2=None,
+                    op0=MULT,
+                )
+            else:
+                nc.scalar.copy(out=wide[:], in_=src)
+            x_bf[b, h] = wide
+
+        def turn_x(b, s):
+            if b < X_MM:
+                for h in range(2):
+                    xt = psum.tile([P, 4, P], F32, name="tp", bufs=5)
+                    for t in range(4):
+                        c = (4 * s + t) * P
+                        nc.tensor.matmul(xt[:, t, :], x_bf[b, h][:, c : c + P], ident_bf[:], start=True, stop=True)
+                    x_bank[b, s, h] = xt
+            else:
+                xt = psum.tile([P, 2, N], F32, name="tp", bufs=5)
+                for h in range(2):
+                    words = x_bf[b, h][:].bitcast(F32)
+                    for u in range(2):
+                        if b < X_PAR:
+                            src = words[:, 256 * s + P * u : 256 * s + P * (u + 1)]
+                        else:
+                            src = words[:, 256 * s + u : 256 * (s + 1) : 2]
+                        nc.tensor.transpose(xt[:, u, h * P : (h + 1) * P], src, ident[:])
+                x_bank[b, s] = xt
+
+        def scale_x(b, s):
+            if s == 0:
+                x_grp[b] = pool.tile([P, 2, N, 4], BF16, name="x_grp", bufs=2, align_bytes=64)
+            grp = x_grp[b]
+            g = 2 * b + s
+            if b < X_MM:
+                for h in range(2):
+                    nc.vector.tensor_tensor(
+                        out=grp[:, s, h * P : (h + 1) * P, :],
+                        in0=x_bank[b, s, h][:].rearrange("p t n -> p n t"),
+                        in1=x_scale[:, g : g + 1, :].to_broadcast([P, P, 4]),
+                        op=MULT,
                     )
-            if g % 2 == 0:
-                x_grp[g // 2] = pool.tile([P, 2, N, 4], BF16, name="x_grp", bufs=2, align_bytes=64)
-            grp = x_grp[g // 2]
-            sc = x_scale[:, g : g + 1, :].rearrange("p o (u e) -> p o u e", u=2)
-            nc.vector.tensor_tensor(
-                out=grp[:, g % 2].rearrange("p n (u e) -> p n u e", u=2),
-                in0=xt[:].rearrange("p u n -> p (u n)").bitcast(BF16).rearrange("p (u n e) -> p n u e", u=2, e=2),
-                in1=sc.to_broadcast([P, N, 2, 2]),
-                op=MULT,
-            )
+            else:
+                sc = x_scale[:, g : g + 1, :].rearrange("p o (u e) -> p o u e", u=2)
+                nc.vector.tensor_tensor(
+                    out=grp[:, s].rearrange("p n (u e) -> p n u e", u=2),
+                    in0=x_bank[b, s][:].rearrange("p u n -> p (u n)").bitcast(BF16)
+                    .rearrange("p (u n e) -> p n u e", u=2, e=2),
+                    in1=sc.to_broadcast([P, N, 2, 2]),
+                    op=MULT,
+                )
 
         def quant_x(b):
             nc.vector.quantize_mx(
@@ -115,51 +167,68 @@ def tile_skconv2d_pa_kernel(tc, xw_bytes, xw_scale, S1s, U1s, U2s, S2s, bias, ou
                 in_=x_grp[b][:].rearrange("p g n t -> p (g n t)"),
             )
 
+        u2_sorted = {}
+        sorted_banks = []
         u2_grp = {}
         u2_codes = {}
 
+        def sort_u2(i, lo, hi):
+            if i not in u2_sorted:
+                u2_sorted[i] = pool.tile([P, GD, 2, P], F32, name="u2_sorted", bufs=3, align_bytes=64)
+            words = u2_raw[i][:].bitcast(F32)[:, lo * 512 : hi * 512]
+            nc.vector.tensor_copy(
+                out=u2_sorted[i][:, 2 * lo : 2 * hi], in_=words.rearrange("p (g w u) -> p g u w", w=P, u=2)
+            )
+            sorted_banks.extend((i, b) for b in range(lo, hi))
+
         def turn_u2(i, b):
             if b == 0:
-                u2_grp[i] = pool.tile([P, GD, P, 4], BF16, name="u2_grp", bufs=4, align_bytes=64)
+                u2_grp[i] = pool.tile([P, GD, P, 4], BF16, name="u2_grp", bufs=3, align_bytes=64)
             words = u2_raw[i][:].bitcast(F32)
             ut = psum.tile([P, 2, 2, P], F32, name="tp", bufs=5)
             for s in range(2):
                 g = 2 * b + s
                 for u in range(2):
-                    nc.tensor.transpose(ut[:, s, u, :], words[:, 256 * g + u : 256 * (g + 1) : 2], ident[:])
+                    if (i, b) in sorted_banks:
+                        src = u2_sorted[i][:, g, u, :]
+                    else:
+                        src = words[:, 256 * g + u : 256 * (g + 1) : 2]
+                    nc.tensor.transpose(ut[:, s, u, :], src, ident[:])
             nc.scalar.copy(
                 out=u2_grp[i][:, 2 * b : 2 * b + 2].rearrange("p g n t -> p (g n t)").bitcast(F32)
                 .rearrange("p (g n u) -> p g n u", g=2, u=2),
                 in_=ut[:].rearrange("p g u n -> p g n u"),
             )
 
-        def quant_u2(i):
-            codes = pool.tile([P, GD, P], U32, name="u2_codes", bufs=5, align_bytes=64)
-            scales = pool.tile([P, GD, P], U8, name="u2_scales", bufs=5, align_bytes=64)
+        def quant_u2(i, lo=0, hi=GD):
+            if lo == 0:
+                codes = pool.tile([P, GD, P], U32, name="u2_codes", bufs=3, align_bytes=64)
+                scales = pool.tile([P, GD, P], U8, name="u2_scales", bufs=3, align_bytes=64)
+                u2_codes[i] = (codes, scales)
+            codes, scales = u2_codes[i]
             nc.vector.quantize_mx(
-                out=codes[:].rearrange("p g n -> p (g n)").bitcast(FP8X4),
-                scales=scales[:].rearrange("p g n -> p (g n)"),
-                in_=u2_grp[i][:].rearrange("p g n t -> p (g n t)"),
+                out=codes[:, lo:hi].rearrange("p g n -> p (g n)").bitcast(FP8X4),
+                scales=scales[:, lo:hi].rearrange("p g n -> p (g n)"),
+                in_=u2_grp[i][:, lo:hi].rearrange("p g n t -> p (g n t)"),
             )
-            u2_codes[i] = (codes, scales)
 
         w_codes = [keep.tile([P, 512], U32, name="w_codes%d" % c, align_bytes=64) for c in range(13)]
         w_scales = [keep.tile([P, 512], U8, name="w_scales%d" % c, align_bytes=64) for c in range(13)]
         w_grp = {}
 
-        def copy_w(c):
-            grp = pool.tile([P, 2048], BF16, name="w_grp", bufs=2, align_bytes=64)
+        def copy_w(c, engine, lo, hi):
+            if c not in w_grp:
+                w_grp[c] = pool.tile([P, 2048], BF16, name="w_grp", bufs=3, align_bytes=64)
             if c < 8:
-                nc.vector.tensor_copy(
-                    out=grp[:].rearrange("p (q t r j) -> p q t r j", q=4, t=8, j=4),
-                    in_=w_raw[c][:].rearrange("p (t j r q) -> p q t r j", t=8, j=4, q=4),
-                )
+                dst = w_grp[c][:].rearrange("p (q t r j) -> p t r j q", q=4, t=8, j=4)[:, lo:hi]
+                src = w_raw[c][:].rearrange("p (t j r q) -> p t r j q", t=8, j=4, q=4)[:, lo:hi]
             else:
-                nc.scalar.copy(
-                    out=grp[:].rearrange("p (q m j) -> p q m j", q=4, j=4),
-                    in_=w_raw[c][:].rearrange("p (j m q) -> p q m j", j=4, q=4),
-                )
-            w_grp[c] = grp
+                dst = w_grp[c][:].rearrange("p (q m j) -> p m j q", q=4, j=4)[:, 16 * lo : 16 * hi]
+                src = w_raw[c][:].rearrange("p (j m q) -> p m j q", j=4, q=4)[:, 16 * lo : 16 * hi]
+            if engine == "vector":
+                nc.vector.tensor_copy(out=dst, in_=src)
+            else:
+                nc.scalar.copy(out=dst, in_=src)
 
         def quant_w(c):
             nc.vector.quantize_mx(out=w_codes[c][:].bitcast(FP8X4), scales=w_scales[c][:], in_=w_grp[c][:])
@@ -169,37 +238,44 @@ def tile_skconv2d_pa_kernel(tc, xw_bytes, xw_scale, S1s, U1s, U2s, S2s, bias, ou
         h_codes = [keep.tile([P, N], U32, name="h_codes%d" % g, align_bytes=64) for g in range(5)]
         h_scales = [keep.tile([P, N], U8, name="h_scales%d" % g, align_bytes=64) for g in range(5)]
 
-        def multiply(group, t, lhs, passes=range(GD)):
+        def multiply(group, t, g, codes, scales, start, stop):
             if (group, t // 2) not in h_bank:
                 h_bank[group, t // 2] = psum.tile([P, 2, N], F32, name="hp", bufs=3)
-            bank = h_bank[group, t // 2]
-            for g in passes:
-                codes, scales = lhs(g)
-                nc.tensor.matmul_mx(
-                    out=bank[:, t % 2, :],
-                    lhsT=codes.bitcast(FP8X4),
-                    lhsT_scale=scales,
-                    rhs=x_codes[:, g, :].bitcast(FP8X4),
-                    rhs_scale=x_scales[:, g, :],
-                    start=(g == 0),
-                    stop=(g == GD - 1),
-                )
+            nc.tensor.matmul_mx(
+                out=h_bank[group, t // 2][:, t % 2, :],
+                lhsT=codes.bitcast(FP8X4),
+                lhsT_scale=scales,
+                rhs=x_codes[:, g, :].bitcast(FP8X4),
+                rhs_scale=x_scales[:, g, :],
+                start=start,
+                stop=stop,
+            )
 
         def multiply_u2(i, passes=range(GD)):
             codes, scales = u2_codes[i]
-            multiply(i // 4, i % 4, lambda g: (codes[:, g, :], scales[:, g, :]), passes)
+            for c in passes:
+                if i < HEAD:
+                    t, s = divmod(c, 2)
+                    first = i == 0 and c % 4 == 0
+                    last = i == HEAD - 1 and c % 4 == 3
+                    multiply(0, t, 2 * i + s, codes[:, c, :], scales[:, c, :], first, last)
+                else:
+                    multiply(i // 4, i % 4, c, codes[:, c, :], scales[:, c, :], c == 0, c == GD - 1)
 
         def multiply_s1(t):
             cols = slice(t * P, (t + 1) * P)
-            multiply(4, t, lambda g: (w_codes[g][:, cols], w_scales[g][:, cols]))
+            for g in range(GD):
+                multiply(4, t, g, w_codes[g][:, cols], w_scales[g][:, cols], g == 0, g == GD - 1)
 
-        def empty_h(group, half):
-            if half == 0:
+        def empty_h(group, half, engine="scalar"):
+            if group not in h_grp:
                 h_grp[group] = pool.tile([P, N, 4], BF16, name="h_grp", bufs=2, align_bytes=64)
-            nc.scalar.copy(
-                out=h_grp[group][:, :, 2 * half : 2 * half + 2],
-                in_=h_bank[group, half][:].rearrange("p t n -> p n t"),
-            )
+            dst = h_grp[group][:, :, 2 * half : 2 * half + 2]
+            src = h_bank[group, half][:].rearrange("p t n -> p n t")
+            if engine == "vector":
+                nc.vector.tensor_copy(out=dst, in_=src)
+            else:
+                nc.scalar.copy(out=dst, in_=src)
 
         def quant_h(group):
             nc.vector.quantize_mx(
@@ -208,88 +284,130 @@ def tile_skconv2d_pa_kernel(tc, xw_bytes, xw_scale, S1s, U1s, U2s, S2s, bias, ou
                 in_=h_grp[group][:].rearrange("p n t -> p (n t)"),
             )
 
-        a, b_, c_ = SEQ[:3]
-        banks = [(SEQ[n // 4], n % 4) for n in range(4, 20)]
-        for b in range(4):
-            turn_u2(a, b)
-
-        def head(g):
-            turn_x(g)
-            for i, b in banks[2 * g : 2 * g + 2]:
-                turn_u2(i, b)
-
-        head(0)
-        head(1)
-        head(2)
-        quant_x(0)
-        head(3)
-        quant_u2(a)
-        quant_x(1)
-        multiply_u2(a, range(0, 2))
-        head(4)
-        multiply_u2(a, range(2, 4))
-        head(5)
-        quant_u2(b_)
-        quant_x(2)
-        load_u2(SEQ[5])
-        head(6)
-        multiply_u2(b_, range(0, 4))
-        head(7)
-        quant_u2(c_)
-        quant_x(3)
-        multiply_u2(a, range(4, 6))
-        multiply_u2(b_, range(4, 6))
-        multiply_u2(c_, range(0, 6))
-        load_u2(SEQ[6])
+        load_x(0)
+        nc.scalar.dma_start(out=x_scale[:], in_=xw_scale.rearrange("o (g p t) -> p (o g) t", p=P, t=4))
+        load_x(1)
+        load_x(2)
+        load_u2(0, 2)
+        load_u2(1)
+        load_x(3)
+        load_u2(2)
         load_w(0)
-        load_w(8)
-        quant_u2(SEQ[3])
-        for i in (a, b_, c_):
-            multiply_u2(i, range(6, 8))
-        copy_w(0)
+        load_u2(3)
+        load_w(1)
+        load_u2(4)
+        load_u2(5)
+        nc.sync.dma_start(out=bias_in[:], in_=bias.rearrange("(p m) -> p m", m=4))
+        load_w(2)
 
-        chunks = [0, 8, 1, 2, 9, 3, 4, 10, 5, 6, 11, 7, 12]
-        at = 1
-        copied = [0]
-        group_done = []
-        for s in range(3, TILES):
-            load_w(chunks[at + 1]) if at + 1 < 13 else None
-            if s + 4 < TILES:
-                load_u2(SEQ[s + 4])
-            if s + 2 < TILES:
-                for b in range(4):
-                    turn_u2(SEQ[s + 2], b)
-            if s + 1 < TILES:
-                quant_u2(SEQ[s + 1])
-            if copied:
-                quant_w(copied.pop())
-            while group_done:
-                quant_h(group_done.pop())
-            if at < 13:
-                copy_w(chunks[at])
-                copied.append(chunks[at])
-                at += 1
-            if s == 15:
-                for t in range(4):
-                    multiply_s1(t)
-                    if t % 2 == 1:
-                        empty_h(4, t // 2)
-            i = SEQ[s]
-            multiply_u2(i)
-            if i % 2 == 1:
-                empty_h(i // 4, (i % 4) // 2)
-                if i % 4 == 3:
-                    group_done.append(i // 4)
-        quant_h(4)
-        quant_h(3)
+        done = [0, 0, 3]
 
+        def turn_half(n):
+            turn_u2(n // 2, 2 * (n % 2))
+            turn_u2(n // 2, 2 * (n % 2) + 1)
+
+        def interleave(engine, n):
+            while n and done[0] < 8 * 13:
+                c, lo = divmod(done[0], 8)
+                k = min(n, 8 - lo)
+                copy_w(c, engine, lo, lo + k)
+                done[0] += k
+                n -= k
+                if lo + k == 8 and done[2] < 13:
+                    load_w(done[2])
+                    done[2] += 1
+
+        def quant_ready():
+            while done[1] < done[0] // 8:
+                quant_w(done[1])
+                done[1] += 1
+
+        for b in range(3):
+            for h in range(2):
+                widen_x(b, h)
+        for g in range(2):
+            turn_x(0, g)
+            scale_x(0, g)
+        turn_half(0)
+        turn_x(1, 0)
+        scale_x(1, 0)
+        turn_half(1)
+        load_u2(6)
+        quant_x(0)
+        quant_u2(0, 0, 4)
+        turned = 2
+        for j in range(2 * HEAD):
+            g = j + 3
+            if g < GD:
+                turn_x(g // 2, g % 2)
+            for n in range(2 if j in (5, 6) else 1):
+                turn_half(turned)
+                turned += 1
+                if turned % 2 == 0 and turned // 2 + 5 < UNITS:
+                    load_u2(turned // 2 + 5)
+            if j < 2:
+                widen_x(3, j)
+            if j % 2 == 1 and j < 6:
+                quant_x((j + 1) // 2)
+            quant_u2((j + 1) // 2, 4 * ((j + 1) % 2), 4 * ((j + 1) % 2) + 4)
+            if g < GD:
+                scale_x(g // 2, g % 2)
+            quant_ready()
+            if j in (2, 3, 4):
+                interleave("scalar", 4)
+            if j < 4:
+                sort_u2(turned // 2, 2 * (turned % 2) + 1, 2 * (turned % 2) + 2)
+            elif j < 6:
+                sort_u2(j, 4 - SORTED, 4)
+            elif j == 7:
+                sort_u2(6, 4 - SORTED, 4)
+            multiply_u2(j // 2, range(4 * (j % 2), 4 * (j % 2) + 4))
+        quant_u2(HEAD, 4, 8)
         bias2 = const.tile([P, 4], F32, name="bias2", align_bytes=64)
         nc.vector.tensor_scalar(out=bias2[:], in0=bias_in[:], scalar1=2.0, scalar2=None, op0=MULT)
-        order = [(4, 12), (0, 8), (1, 9), (2, 10), (3, 11)]
+        for i in range(HEAD, UNITS):
+            if i + 2 < UNITS:
+                for b in range(4):
+                    turn_u2(i + 2, b)
+                    if i == HEAD and b % 2 == 1:
+                        empty_h(0, b // 2)
+                    if b == 1 and i % 2 == 0 and i > HEAD:
+                        empty_h((i - 1) // 4, ((i - 1) % 4) // 2)
+            if i + 8 < UNITS:
+                load_u2(i + 8)
+            if i + 1 < UNITS:
+                quant_u2(i + 1)
+            quant_ready()
+            if i + 3 < UNITS:
+                sort_u2(i + 3, 4 - SORTED, 4)
+            if i % 4 == 1:
+                quant_h(i // 4 - 1)
+            if i == 14:
+                empty_h(3, 0)
+            interleave("vector", 5 if i < 13 else 8)
+            interleave("scalar", 1 if i < 14 else 6)
+            if i == 15:
+                multiply_s1(0)
+                multiply_s1(1)
+                empty_h(4, 0)
+            multiply_u2(i)
+        quant_ready()
+        empty_h(3, 1)
+        interleave("vector", 8)
+        interleave("scalar", 4)
+        multiply_s1(2)
+        multiply_s1(3)
+        quant_h(3)
+        quant_ready()
+        interleave("vector", 99)
+        empty_h(4, 1)
+        quant_ready()
+        quant_h(4)
+
         acc = [psum.tile([P, 512], F32, name="tp", bufs=5) for m in range(4)]
 
-        def second(m, n):
-            group, w = order[n]
+        def second(m, n, group):
+            w = 12 if group == 4 else 8 + group
             nc.tensor.matmul_mx(
                 out=acc[m][:, :N],
                 lhsT=w_codes[w][:, m * P : (m + 1) * P].bitcast(FP8X4),
@@ -300,21 +418,17 @@ def tile_skconv2d_pa_kernel(tc, xw_bytes, xw_scale, S1s, U1s, U2s, S2s, bias, ou
                 stop=(n == 4),
             )
 
-        for m in range(4):
-            for n in range(4):
-                second(m, n)
-        result = keep.tile([P, 4, 4, 64], F32, name="result", align_bytes=64)
-        out_view = out.rearrange("b (p m) i j -> p b m (i j)", m=4)
-        for m in range(4):
-            second(m, 4)
+        for n, group in enumerate([0, 1, 2, 3, 4]):
+            for m in range(4):
+                second(m, n, group)
+        result = [keep.tile([P, 4, 2, 64], F32, name="result%d" % m, align_bytes=64) for m in range(2)]
+        out_view = out.rearrange("b (p a m) i j -> a p b (m i j)", a=2, m=2)
         for m in range(4):
             src = acc[m][:, :N].rearrange("p (b s) -> p b s", b=4)
             if m % 2 == 0:
-                nc.scalar.activation(
-                    out=result[:, :, m, :], in_=src, func=IDENTITY, bias=bias2[:, m : m + 1], scale=0.125
-                )
+                nc.scalar.activation(out=result[m // 2][:, :, m % 2, :], in_=src, func=IDENTITY, bias=bias2[:, m : m + 1], scale=0.125)
             else:
                 nc.vector.tensor_scalar(
-                    out=result[:, :, m, :], in0=src, scalar1=0.125, scalar2=bias2[:, m : m + 1], op0=MULT, op1=ADD
+                    out=result[m // 2][:, :, m % 2, :], in0=src, scalar1=0.125, scalar2=bias2[:, m : m + 1], op0=MULT, op1=ADD
                 )
-                nc.sync.dma_start(out=out_view[:, :, m - 1 : m + 1, :], in_=result[:, :, m - 1 : m + 1, :])
+                nc.sync.dma_start(out=out_view[m // 2], in_=result[m // 2][:].rearrange("p b m s -> p b (m s)"))

@@ -61,7 +61,7 @@ def tile_skconv2d_pa_kernel(tc, xw_bytes, xw_scale, S1s, U1s, U2s, S2s, bias, ou
         w_raw = {}
 
         def load_u2(i, pieces=1):
-            raw = pool.tile([P, D], BF16, name="u2_raw", bufs=6, align_bytes=64)
+            raw = pool.tile([P, D], BF16, name="u2_raw", bufs=7, align_bytes=64)
             if i < HEAD:
                 k = 4 // pieces
                 for c in range(pieces):
@@ -79,7 +79,7 @@ def tile_skconv2d_pa_kernel(tc, xw_bytes, xw_scale, S1s, U1s, U2s, S2s, bias, ou
             x_in[b] = xi
 
         def load_w(c):
-            raw = pool.tile([P, 2048], BF16, name="w_raw", bufs=4, align_bytes=64)
+            raw = pool.tile([P, 2048], BF16, name="w_raw", bufs=6, align_bytes=64)
             if c < 8:
                 nc.sync.dma_start(out=raw[:].rearrange("p (t x) -> p t x", t=8), in_=s1_rows[c])
             elif c < 12:
@@ -172,12 +172,16 @@ def tile_skconv2d_pa_kernel(tc, xw_bytes, xw_scale, S1s, U1s, U2s, S2s, bias, ou
         u2_grp = {}
         u2_codes = {}
 
+        def slot(i, b):
+            return b // 2 if i < HEAD else b - 2
+
         def sort_u2(i, lo, hi):
             if i not in u2_sorted:
-                u2_sorted[i] = pool.tile([P, GD, 2, P], F32, name="u2_sorted", bufs=3, align_bytes=64)
+                u2_sorted[i] = pool.tile([P, 2, 2, 2, P], F32, name="u2_sorted", bufs=3, align_bytes=64)
             words = u2_raw[i][:].bitcast(F32)[:, lo * 512 : hi * 512]
             nc.vector.tensor_copy(
-                out=u2_sorted[i][:, 2 * lo : 2 * hi], in_=words.rearrange("p (g w u) -> p g u w", w=P, u=2)
+                out=u2_sorted[i][:, slot(i, lo) : slot(i, lo) + hi - lo].rearrange("p b s u w -> p (b s) u w"),
+                in_=words.rearrange("p (g w u) -> p g u w", w=P, u=2),
             )
             sorted_banks.extend((i, b) for b in range(lo, hi))
 
@@ -190,7 +194,7 @@ def tile_skconv2d_pa_kernel(tc, xw_bytes, xw_scale, S1s, U1s, U2s, S2s, bias, ou
                 g = 2 * b + s
                 for u in range(2):
                     if (i, b) in sorted_banks:
-                        src = u2_sorted[i][:, g, u, :]
+                        src = u2_sorted[i][:, slot(i, b), s, u, :]
                     else:
                         src = words[:, 256 * g + u : 256 * (g + 1) : 2]
                     nc.tensor.transpose(ut[:, s, u, :], src, ident[:])
@@ -220,15 +224,18 @@ def tile_skconv2d_pa_kernel(tc, xw_bytes, xw_scale, S1s, U1s, U2s, S2s, bias, ou
             if c not in w_grp:
                 w_grp[c] = pool.tile([P, 2048], BF16, name="w_grp", bufs=3, align_bytes=64)
             if c < 8:
-                dst = w_grp[c][:].rearrange("p (q t r j) -> p t r j q", q=4, t=8, j=4)[:, lo:hi]
-                src = w_raw[c][:].rearrange("p (t j r q) -> p t r j q", t=8, j=4, q=4)[:, lo:hi]
+                dst = w_grp[c][:].rearrange("p (q t m r j) -> p t m q r j", q=4, t=8, r=2, j=4)
+                src = w_raw[c][:].rearrange("p (t j m r q) -> p t m q r j", t=8, j=4, r=2, q=4)
+                parts = [(dst[:, t], src[:, t]) for t in range(lo, hi)]
             else:
-                dst = w_grp[c][:].rearrange("p (q m j) -> p m j q", q=4, j=4)[:, 16 * lo : 16 * hi]
-                src = w_raw[c][:].rearrange("p (j m q) -> p m j q", j=4, q=4)[:, 16 * lo : 16 * hi]
-            if engine == "vector":
-                nc.vector.tensor_copy(out=dst, in_=src)
-            else:
-                nc.scalar.copy(out=dst, in_=src)
+                dst = w_grp[c][:].rearrange("p (q m r j) -> p m q r j", q=4, r=2, j=4)
+                src = w_raw[c][:].rearrange("p (j m r q) -> p m q r j", j=4, r=2, q=4)
+                parts = [(dst[:, 8 * lo : 8 * hi], src[:, 8 * lo : 8 * hi])]
+            for dst, src in parts:
+                if engine == "vector":
+                    nc.vector.tensor_copy(out=dst, in_=src)
+                else:
+                    nc.scalar.copy(out=dst, in_=src)
 
         def quant_w(c):
             nc.vector.quantize_mx(out=w_codes[c][:].bitcast(FP8X4), scales=w_scales[c][:], in_=w_grp[c][:])
@@ -299,6 +306,7 @@ def tile_skconv2d_pa_kernel(tc, xw_bytes, xw_scale, S1s, U1s, U2s, S2s, bias, ou
         load_u2(5)
         nc.sync.dma_start(out=bias_in[:], in_=bias.rearrange("(p m) -> p m", m=4))
         load_w(2)
+        load_u2(6)
 
         done = [0, 0, 3]
 
@@ -313,9 +321,18 @@ def tile_skconv2d_pa_kernel(tc, xw_bytes, xw_scale, S1s, U1s, U2s, S2s, bias, ou
                 copy_w(c, engine, lo, lo + k)
                 done[0] += k
                 n -= k
-                if lo + k == 8 and done[2] < 13:
-                    load_w(done[2])
-                    done[2] += 1
+                if UNITS - 1 in u2_raw:
+                    load_weights(13)
+
+        def load_weights(n):
+            while n and done[2] < min(13, done[0] // 8 + 6):
+                load_w(done[2])
+                done[2] += 1
+                n -= 1
+
+        def load_next(i):
+            load_u2(i)
+            load_weights(1)
 
         def quant_ready():
             while done[1] < done[0] // 8:
@@ -332,7 +349,7 @@ def tile_skconv2d_pa_kernel(tc, xw_bytes, xw_scale, S1s, U1s, U2s, S2s, bias, ou
         turn_x(1, 0)
         scale_x(1, 0)
         turn_half(1)
-        load_u2(6)
+        load_next(7)
         quant_x(0)
         quant_u2(0, 0, 4)
         turned = 2
@@ -343,8 +360,8 @@ def tile_skconv2d_pa_kernel(tc, xw_bytes, xw_scale, S1s, U1s, U2s, S2s, bias, ou
             for n in range(2 if j in (5, 6) else 1):
                 turn_half(turned)
                 turned += 1
-                if turned % 2 == 0 and turned // 2 + 5 < UNITS:
-                    load_u2(turned // 2 + 5)
+                if turned % 2 == 0 and turned // 2 + 6 < UNITS:
+                    load_next(turned // 2 + 6)
             if j < 2:
                 widen_x(3, j)
             if j % 2 == 1 and j < 6:
@@ -373,8 +390,8 @@ def tile_skconv2d_pa_kernel(tc, xw_bytes, xw_scale, S1s, U1s, U2s, S2s, bias, ou
                         empty_h(0, b // 2)
                     if b == 1 and i % 2 == 0 and i > HEAD:
                         empty_h((i - 1) // 4, ((i - 1) % 4) // 2)
-            if i + 8 < UNITS:
-                load_u2(i + 8)
+            if i + 9 < UNITS:
+                load_next(i + 9)
             if i + 1 < UNITS:
                 quant_u2(i + 1)
             quant_ready()

@@ -75,7 +75,9 @@ def tile_skconv2d_pa_kernel(tc, xw_bytes, xw_scale, S1s, U1s, U2s, S2s, bias, ou
 
         def load_x(b):
             xi = keep.tile([P, 2, 1024], U8, name="x_in%d" % b, align_bytes=64)
-            nc.sync.dma_start(out=xi[:], in_=x_rows[:, :, b * 1024 : (b + 1) * 1024])
+            k = 1 if b == 0 else 2
+            for h in range(0, 2, k):
+                nc.sync.dma_start(out=xi[:, h : h + k], in_=x_rows[:, h : h + k, b * 1024 : (b + 1) * 1024])
             x_in[b] = xi
 
         def load_w(c):
@@ -173,13 +175,13 @@ def tile_skconv2d_pa_kernel(tc, xw_bytes, xw_scale, S1s, U1s, U2s, S2s, bias, ou
         u2_codes = {}
 
         def slot(i, b):
-            return b // 2 if i < HEAD else b - 2
+            return b // 2 if i < HEAD else b - (4 - SORTED)
 
-        def sort_u2(i, lo, hi):
+        def sort_u2(i, lo, hi, copy=nc.vector.tensor_copy):
             if i not in u2_sorted:
-                u2_sorted[i] = pool.tile([P, 2, 2, 2, P], F32, name="u2_sorted", bufs=3, align_bytes=64)
+                u2_sorted[i] = pool.tile([P, max(SORTED, 2), 2, 2, P], F32, name="u2_sorted", bufs=2, align_bytes=64)
             words = u2_raw[i][:].bitcast(F32)[:, lo * 512 : hi * 512]
-            nc.vector.tensor_copy(
+            copy(
                 out=u2_sorted[i][:, slot(i, lo) : slot(i, lo) + hi - lo].rearrange("p b s u w -> p (b s) u w"),
                 in_=words.rearrange("p (g w u) -> p g u w", w=P, u=2),
             )
@@ -228,9 +230,9 @@ def tile_skconv2d_pa_kernel(tc, xw_bytes, xw_scale, S1s, U1s, U2s, S2s, bias, ou
                 src = w_raw[c][:].rearrange("p (t j m r q) -> p t m q r j", t=8, j=4, r=2, q=4)
                 parts = [(dst[:, t], src[:, t]) for t in range(lo, hi)]
             else:
-                dst = w_grp[c][:].rearrange("p (q m r j) -> p m q r j", q=4, r=2, j=4)
-                src = w_raw[c][:].rearrange("p (j m r q) -> p m q r j", j=4, r=2, q=4)
-                parts = [(dst[:, 8 * lo : 8 * hi], src[:, 8 * lo : 8 * hi])]
+                dst = w_grp[c][:].rearrange("p (q m r j) -> p m j r q", q=2, r=2, j=4)
+                src = w_raw[c][:].rearrange("p (j m r q) -> p m j r q", j=4, r=2, q=2)
+                parts = [(dst[:, 16 * lo : 16 * hi], src[:, 16 * lo : 16 * hi])]
             for dst, src in parts:
                 if engine == "vector":
                     nc.vector.tensor_copy(out=dst, in_=src)
@@ -296,17 +298,19 @@ def tile_skconv2d_pa_kernel(tc, xw_bytes, xw_scale, S1s, U1s, U2s, S2s, bias, ou
         load_x(1)
         load_x(2)
         load_u2(0, 2)
-        load_u2(1)
         load_x(3)
-        load_u2(2)
+        load_u2(1)
         load_w(0)
-        load_u2(3)
+        load_u2(2)
         load_w(1)
+        load_u2(3)
         load_u2(4)
-        load_u2(5)
-        nc.sync.dma_start(out=bias_in[:], in_=bias.rearrange("(p m) -> p m", m=4))
         load_w(2)
+        load_u2(5)
         load_u2(6)
+        nc.sync.dma_start(
+            out=bias_in[:].rearrange("p (a m) -> p a m", a=2), in_=bias.rearrange("(a p m) -> p a m", a=2, m=2)
+        )
 
         done = [0, 0, 3]
 
@@ -332,7 +336,8 @@ def tile_skconv2d_pa_kernel(tc, xw_bytes, xw_scale, S1s, U1s, U2s, S2s, bias, ou
 
         def load_next(i):
             load_u2(i)
-            load_weights(1)
+            if i % 3:
+                load_weights(1)
 
         def quant_ready():
             while done[1] < done[0] // 8:
@@ -346,15 +351,20 @@ def tile_skconv2d_pa_kernel(tc, xw_bytes, xw_scale, S1s, U1s, U2s, S2s, bias, ou
             turn_x(0, g)
             scale_x(0, g)
         turn_half(0)
+        widen_x(3, 0)
         turn_x(1, 0)
         scale_x(1, 0)
         turn_half(1)
+        widen_x(3, 1)
         load_next(7)
         quant_x(0)
         quant_u2(0, 0, 4)
         turned = 2
         for j in range(2 * HEAD):
             g = j + 3
+            if j % 2 == 1 and j < 6:
+                quant_x((j + 1) // 2)
+            quant_u2((j + 1) // 2, 4 * ((j + 1) % 2), 4 * ((j + 1) % 2) + 4)
             if g < GD:
                 turn_x(g // 2, g % 2)
             for n in range(2 if j in (5, 6) else 1):
@@ -362,24 +372,18 @@ def tile_skconv2d_pa_kernel(tc, xw_bytes, xw_scale, S1s, U1s, U2s, S2s, bias, ou
                 turned += 1
                 if turned % 2 == 0 and turned // 2 + 6 < UNITS:
                     load_next(turned // 2 + 6)
-            if j < 2:
-                widen_x(3, j)
-            if j % 2 == 1 and j < 6:
-                quant_x((j + 1) // 2)
-            quant_u2((j + 1) // 2, 4 * ((j + 1) % 2), 4 * ((j + 1) % 2) + 4)
             if g < GD:
                 scale_x(g // 2, g % 2)
             quant_ready()
-            if j in (2, 3, 4):
+            if j in (0, 1, 2, 3, 4):
                 interleave("scalar", 4)
-            if j < 4:
-                sort_u2(turned // 2, 2 * (turned % 2) + 1, 2 * (turned % 2) + 2)
-            elif j < 6:
+            if 4 <= j < 6:
                 sort_u2(j, 4 - SORTED, 4)
             elif j == 7:
                 sort_u2(6, 4 - SORTED, 4)
             multiply_u2(j // 2, range(4 * (j % 2), 4 * (j % 2) + 4))
         quant_u2(HEAD, 4, 8)
+        interleave("vector", 4)
         bias2 = const.tile([P, 4], F32, name="bias2", align_bytes=64)
         nc.vector.tensor_scalar(out=bias2[:], in0=bias_in[:], scalar1=2.0, scalar2=None, op0=MULT)
         for i in range(HEAD, UNITS):
@@ -392,16 +396,17 @@ def tile_skconv2d_pa_kernel(tc, xw_bytes, xw_scale, S1s, U1s, U2s, S2s, bias, ou
                         empty_h((i - 1) // 4, ((i - 1) % 4) // 2)
             if i + 9 < UNITS:
                 load_next(i + 9)
-            if i + 1 < UNITS:
-                quant_u2(i + 1)
-            quant_ready()
             if i + 3 < UNITS:
                 sort_u2(i + 3, 4 - SORTED, 4)
-            if i % 4 == 1:
-                quant_h(i // 4 - 1)
+            quant_ready()
             if i == 14:
                 empty_h(3, 0)
-            interleave("vector", 5 if i < 13 else 8)
+            interleave("vector", 4 if i < 13 else 0)
+            if i + 1 < UNITS:
+                quant_u2(i + 1)
+            if i % 4 == 1:
+                quant_h(i // 4 - 1)
+            interleave("vector", 0 if i < 13 else 8)
             interleave("scalar", 1 if i < 14 else 6)
             if i == 15:
                 multiply_s1(0)
@@ -424,22 +429,26 @@ def tile_skconv2d_pa_kernel(tc, xw_bytes, xw_scale, S1s, U1s, U2s, S2s, bias, ou
         acc = [psum.tile([P, 512], F32, name="tp", bufs=5) for m in range(4)]
 
         def second(m, n, group):
+            cols = slice((2 * (m % 2) + m // 2) * P, (2 * (m % 2) + m // 2 + 1) * P)
             w = 12 if group == 4 else 8 + group
             nc.tensor.matmul_mx(
                 out=acc[m][:, :N],
-                lhsT=w_codes[w][:, m * P : (m + 1) * P].bitcast(FP8X4),
-                lhsT_scale=w_scales[w][:, m * P : (m + 1) * P],
+                lhsT=w_codes[w][:, cols].bitcast(FP8X4),
+                lhsT_scale=w_scales[w][:, cols],
                 rhs=h_codes[group][:].bitcast(FP8X4),
                 rhs_scale=h_scales[group][:],
                 start=(n == 0),
                 stop=(n == 4),
             )
 
-        for n, group in enumerate([0, 1, 2, 3, 4]):
-            for m in range(4):
-                second(m, n, group)
+        order = [0, 1, 2, 3, 4]
+        for part in (range(0, 3), range(3, 5)):
+            for pair in range(2):
+                for n in part:
+                    for m in range(2 * pair, 2 * pair + 2):
+                        second(m, n, order[n])
         result = [keep.tile([P, 4, 2, 64], F32, name="result%d" % m, align_bytes=64) for m in range(2)]
-        out_view = out.rearrange("b (p a m) i j -> a p b (m i j)", a=2, m=2)
+        out_view = out.rearrange("b (a p m) i j -> a p b (m i j)", a=2, m=2)
         for m in range(4):
             src = acc[m][:, :N].rearrange("p (b s) -> p b s", b=4)
             if m % 2 == 0:

@@ -182,8 +182,8 @@ def tile_skconv2d_pa_kernel(tc, xw_bytes, xw_scale, S1s, U1s, U2s, S2s, bias, ou
                 u2_sorted[i] = pool.tile([P, max(SORTED, 2), 2, 2, P], F32, name="u2_sorted", bufs=2, align_bytes=64)
             words = u2_raw[i][:].bitcast(F32)[:, lo * 512 : hi * 512]
             copy(
-                out=u2_sorted[i][:, slot(i, lo) : slot(i, lo) + hi - lo].rearrange("p b s u w -> p (b s) u w"),
-                in_=words.rearrange("p (g w u) -> p g u w", w=P, u=2),
+                out=u2_sorted[i][:, slot(i, lo) : slot(i, lo) + hi - lo].rearrange("p b s u w -> p (b s) w u"),
+                in_=words.rearrange("p (g w u) -> p g w u", w=P, u=2),
             )
             sorted_banks.extend((i, b) for b in range(lo, hi))
 

@@ -19,14 +19,25 @@ D = 4096
 O = 512
 K1 = 512
 K2 = 2048
-GD = D // 512
+PASSES = D // 512
 UNITS = 16
 HEAD = 4
+S1_CHUNKS = 8
+CHUNKS = 13
+H1_GROUP = 4
+U1_CHUNK = 12
+RAW_UNITS = 7
+RAW_CHUNKS = 6
+TURN_BANKS = 5
+
+X_BY_MATMUL = 2
 SORTED = 2
-X_MM = 2
-X_PAR = 2
-SORT_ON_SCALAR = ()
-S1_FIRST = 4
+SCALAR_HEAD_SHARE = 4
+VECTOR_GAP_SHARE = 2
+VECTOR_SHARE = 5
+SCALAR_SHARE = 2
+VECTOR_END_SHARE = 8
+SCALAR_END_SHARE = 6
 
 FLOPS = 2 * N * D * (K1 + K2) + 2 * N * (K1 + K2) * O
 
@@ -44,7 +55,7 @@ def tile_skconv2d_pa_kernel(tc, xw_bytes, xw_scale, S1s, U1s, U2s, S2s, bias, ou
         u2_rows = U2s.rearrange("t r d -> (t r) d").rearrange("(g p t) d -> g p t d", p=P, t=4)
         s1_rows = S1s.rearrange("t (g p j) r -> g p t (j r)", p=P, j=4)
         s2_rows = S2s.rearrange("t r o -> (t r) o").rearrange("(g p j) o -> g p (j o)", p=P, j=4)
-        u1_rows = U1s.rearrange("t r o -> (t r) o").rearrange("(g p j) o -> g p (j o)", p=P, j=4)
+        u1_rows = U1s.rearrange("t r o -> (t r) o").rearrange("(p j) o -> p (j o)", j=4)
         x_rows = xw_bytes.rearrange("(h p) d -> p h d", p=P)
 
         ident = const.tile([P, P], F32, name="ident", align_bytes=64)
@@ -53,64 +64,75 @@ def tile_skconv2d_pa_kernel(tc, xw_bytes, xw_scale, S1s, U1s, U2s, S2s, bias, ou
         make_identity(nc, ident_bf[:])
         ones = const.tile([P, 1], F32, name="ones", align_bytes=64)
         nc.vector.memset(ones[:], 1.0)
-        x_scale = const.tile([P, GD, 4], F32, name="x_scale", align_bytes=64)
+        x_scale = const.tile([P, PASSES, 4], F32, name="x_scale", align_bytes=64)
         bias_in = const.tile([P, 4], BF16, name="bias_in", align_bytes=64)
 
         u2_raw = {}
         x_in = {}
         w_raw = {}
 
-        def load_u2(i, pieces=1):
-            raw = pool.tile([P, D], BF16, name="u2_raw", bufs=7, align_bytes=64)
+        def load_x(b):
+            x_in[b] = keep.tile([P, 2, 1024], U8, name="x_in%d" % b, align_bytes=64)
+            k = 1 if b == 0 else 2
+            for h in range(0, 2, k):
+                nc.sync.dma_start(out=x_in[b][:, h : h + k], in_=x_rows[:, h : h + k, b * 1024 : (b + 1) * 1024])
+
+        def load_u2(i):
+            raw = pool.tile([P, D], BF16, name="u2_raw", bufs=RAW_UNITS, align_bytes=64)
             if i < HEAD:
-                k = 4 // pieces
-                for c in range(pieces):
+                k = 2 if i == 0 else 4
+                for t in range(0, 4, k):
                     nc.sync.dma_start(
-                        out=raw[:, c * k * 1024 : (c + 1) * k * 1024].rearrange("p (t d) -> p t d", t=k),
-                        in_=u2_rows[0][:, c * k : (c + 1) * k, i * 1024 : (i + 1) * 1024],
+                        out=raw[:, t * 1024 : (t + k) * 1024].rearrange("p (t d) -> p t d", t=k),
+                        in_=u2_rows[0][:, t : t + k, i * 1024 : (i + 1) * 1024],
                     )
             else:
                 nc.sync.dma_start(out=raw[:], in_=u2_rows[i // 4][:, i % 4, :])
             u2_raw[i] = raw
 
-        def load_x(b):
-            xi = keep.tile([P, 2, 1024], U8, name="x_in%d" % b, align_bytes=64)
-            k = 1 if b == 0 else 2
-            for h in range(0, 2, k):
-                nc.sync.dma_start(out=xi[:, h : h + k], in_=x_rows[:, h : h + k, b * 1024 : (b + 1) * 1024])
-            x_in[b] = xi
-
         def load_w(c):
-            raw = pool.tile([P, 2048], BF16, name="w_raw", bufs=6, align_bytes=64)
-            if c < 8:
+            raw = pool.tile([P, 2048], BF16, name="w_raw", bufs=RAW_CHUNKS, align_bytes=64)
+            if c < S1_CHUNKS:
                 nc.sync.dma_start(out=raw[:].rearrange("p (t x) -> p t x", t=8), in_=s1_rows[c])
-            elif c < 12:
-                nc.sync.dma_start(out=raw[:], in_=s2_rows[c - 8])
+            elif c < U1_CHUNK:
+                nc.sync.dma_start(out=raw[:], in_=s2_rows[c - S1_CHUNKS])
             else:
-                nc.sync.dma_start(out=raw[:], in_=u1_rows[0])
+                nc.sync.dma_start(out=raw[:], in_=u1_rows)
             w_raw[c] = raw
 
-        x_codes = keep.tile([P, GD, N], U32, name="x_codes", align_bytes=64)
-        x_scales = keep.tile([P, GD, N], U8, name="x_scales", align_bytes=64)
+        queue = []
+        for i in range(2, UNITS):
+            queue.append(("unit", i))
+            queue.extend(("chunk", c) for c in range(S1_CHUNKS) if 2 + (UNITS - 2) * c // S1_CHUNKS == i)
+        queue.extend(("chunk", c) for c in range(S1_CHUNKS, CHUNKS))
+        units_turned = []
+        eighths_done = []
+        chunks_quantised = []
+
+        def load_more():
+            while queue:
+                kind, n = queue[0]
+                if kind == "unit" and n < len(units_turned) + RAW_UNITS:
+                    load_u2(n)
+                elif kind == "chunk" and n < len(eighths_done) // 8 + RAW_CHUNKS:
+                    load_w(n)
+                else:
+                    return
+                queue.pop(0)
+
+        x_codes = keep.tile([P, PASSES, N], U32, name="x_codes", align_bytes=64)
+        x_scales = keep.tile([P, PASSES, N], U8, name="x_scales", align_bytes=64)
         x_bf = {}
-        x_grp = {}
         x_bank = {}
+        x_grp = {}
 
         def widen_x(b, h):
-            wide = pool.tile([P, 1024], BF16, name="x_bf", bufs=8, align_bytes=64)
+            wide = pool.tile([P, 1024], BF16, name="x_bf", bufs=2 * HEAD, align_bytes=64)
             src = x_in[b][:, h, :].bitcast(FP8)
-            if b < X_MM:
+            if b < X_BY_MATMUL:
                 nc.vector.tensor_scalar(
                     out=wide[:].rearrange("p (s t m) -> p s m t", s=2, t=4),
                     in0=src.rearrange("p (s m t) -> p s m t", s=2, t=4),
-                    scalar1=ones[:],
-                    scalar2=None,
-                    op0=MULT,
-                )
-            elif b < X_PAR:
-                nc.vector.tensor_scalar(
-                    out=wide[:].rearrange("p (s u m e) -> p s m u e", s=2, u=2, e=2),
-                    in0=src.rearrange("p (s m u e) -> p s m u e", s=2, u=2, e=2),
                     scalar1=ones[:],
                     scalar2=None,
                     op0=MULT,
@@ -119,46 +141,43 @@ def tile_skconv2d_pa_kernel(tc, xw_bytes, xw_scale, S1s, U1s, U2s, S2s, bias, ou
                 nc.scalar.copy(out=wide[:], in_=src)
             x_bf[b, h] = wide
 
-        def turn_x(b, s):
-            if b < X_MM:
+        def turn_x(g):
+            b, s = divmod(g, 2)
+            if b < X_BY_MATMUL:
                 for h in range(2):
-                    xt = psum.tile([P, 4, P], F32, name="tp", bufs=5)
+                    xt = psum.tile([P, 4, P], F32, name="turn", bufs=TURN_BANKS)
                     for t in range(4):
                         c = (4 * s + t) * P
                         nc.tensor.matmul(xt[:, t, :], x_bf[b, h][:, c : c + P], ident_bf[:], start=True, stop=True)
-                    x_bank[b, s, h] = xt
+                    x_bank[g, h] = xt
             else:
-                xt = psum.tile([P, 2, N], F32, name="tp", bufs=5)
+                xt = psum.tile([P, 2, N], F32, name="turn", bufs=TURN_BANKS)
                 for h in range(2):
                     words = x_bf[b, h][:].bitcast(F32)
                     for u in range(2):
-                        if b < X_PAR:
-                            src = words[:, 256 * s + P * u : 256 * s + P * (u + 1)]
-                        else:
-                            src = words[:, 256 * s + u : 256 * (s + 1) : 2]
+                        src = words[:, 256 * s + u : 256 * (s + 1) : 2]
                         nc.tensor.transpose(xt[:, u, h * P : (h + 1) * P], src, ident[:])
-                x_bank[b, s] = xt
+                x_bank[g] = xt
 
-        def scale_x(b, s):
+        def scale_x(g):
+            b, s = divmod(g, 2)
             if s == 0:
                 x_grp[b] = pool.tile([P, 2, N, 4], BF16, name="x_grp", bufs=2, align_bytes=64)
-            grp = x_grp[b]
-            g = 2 * b + s
-            if b < X_MM:
+            factor = x_scale[:, g : g + 1, :]
+            if b < X_BY_MATMUL:
                 for h in range(2):
                     nc.vector.tensor_tensor(
-                        out=grp[:, s, h * P : (h + 1) * P, :],
-                        in0=x_bank[b, s, h][:].rearrange("p t n -> p n t"),
-                        in1=x_scale[:, g : g + 1, :].to_broadcast([P, P, 4]),
+                        out=x_grp[b][:, s, h * P : (h + 1) * P, :],
+                        in0=x_bank[g, h][:].rearrange("p t n -> p n t"),
+                        in1=factor.to_broadcast([P, P, 4]),
                         op=MULT,
                     )
             else:
-                sc = x_scale[:, g : g + 1, :].rearrange("p o (u e) -> p o u e", u=2)
+                values = x_bank[g][:].rearrange("p u n -> p (u n)").bitcast(BF16)
                 nc.vector.tensor_tensor(
-                    out=grp[:, s].rearrange("p n (u e) -> p n u e", u=2),
-                    in0=x_bank[b, s][:].rearrange("p u n -> p (u n)").bitcast(BF16)
-                    .rearrange("p (u n e) -> p n u e", u=2, e=2),
-                    in1=sc.to_broadcast([P, N, 2, 2]),
+                    out=x_grp[b][:, s].rearrange("p n (u e) -> p n u e", u=2),
+                    in0=values.rearrange("p (u n e) -> p n u e", u=2, e=2),
+                    in1=factor.rearrange("p o (u e) -> p o u e", u=2).to_broadcast([P, N, 2, 2]),
                     op=MULT,
                 )
 
@@ -170,77 +189,88 @@ def tile_skconv2d_pa_kernel(tc, xw_bytes, xw_scale, S1s, U1s, U2s, S2s, bias, ou
             )
 
         u2_sorted = {}
-        sorted_banks = []
         u2_grp = {}
         u2_codes = {}
 
-        def slot(i, b):
-            return b // 2 if i < HEAD else b - (4 - SORTED)
-
-        def sort_u2(i, lo, hi, copy=nc.vector.tensor_copy):
-            if i not in u2_sorted:
-                u2_sorted[i] = pool.tile([P, max(SORTED, 2), 2, 2, P], F32, name="u2_sorted", bufs=2, align_bytes=64)
-            words = u2_raw[i][:].bitcast(F32)[:, lo * 512 : hi * 512]
-            copy(
-                out=u2_sorted[i][:, slot(i, lo) : slot(i, lo) + hi - lo].rearrange("p b s u w -> p (b s) w u"),
-                in_=words.rearrange("p (g w u) -> p g w u", w=P, u=2),
+        def sort_u2(i):
+            srt = pool.tile([P, 2 * SORTED, 2, P], F32, name="u2_sorted", bufs=2, align_bytes=64)
+            words = u2_raw[i][:].bitcast(F32)[:, (4 - SORTED) * 512 :]
+            nc.vector.tensor_copy(
+                out=srt[:].rearrange("p c u w -> p c w u"), in_=words.rearrange("p (c w u) -> p c w u", w=P, u=2)
             )
-            sorted_banks.extend((i, b) for b in range(lo, hi))
+            u2_sorted[i] = srt
 
         def turn_u2(i, b):
             if b == 0:
-                u2_grp[i] = pool.tile([P, GD, P, 4], BF16, name="u2_grp", bufs=3, align_bytes=64)
+                u2_grp[i] = pool.tile([P, 8, P, 4], BF16, name="u2_grp", bufs=3, align_bytes=64)
             words = u2_raw[i][:].bitcast(F32)
-            ut = psum.tile([P, 2, 2, P], F32, name="tp", bufs=5)
+            ut = psum.tile([P, 2, 2, P], F32, name="turn", bufs=TURN_BANKS)
             for s in range(2):
-                g = 2 * b + s
+                c = 2 * b + s
                 for u in range(2):
-                    if (i, b) in sorted_banks:
-                        src = u2_sorted[i][:, slot(i, b), s, u, :]
+                    if i >= HEAD and b >= 4 - SORTED:
+                        src = u2_sorted[i][:, c - 2 * (4 - SORTED), u, :]
                     else:
-                        src = words[:, 256 * g + u : 256 * (g + 1) : 2]
+                        src = words[:, 256 * c + u : 256 * (c + 1) : 2]
                     nc.tensor.transpose(ut[:, s, u, :], src, ident[:])
+            dst = u2_grp[i][:, 2 * b : 2 * b + 2].rearrange("p s n t -> p (s n t)").bitcast(F32)
             nc.scalar.copy(
-                out=u2_grp[i][:, 2 * b : 2 * b + 2].rearrange("p g n t -> p (g n t)").bitcast(F32)
-                .rearrange("p (g n u) -> p g n u", g=2, u=2),
-                in_=ut[:].rearrange("p g u n -> p g n u"),
+                out=dst.rearrange("p (s n u) -> p s n u", s=2, u=2), in_=ut[:].rearrange("p s u n -> p s n u")
             )
+            if b == 3:
+                units_turned.append(i)
+                load_more()
 
-        def quant_u2(i, lo=0, hi=GD):
+        def turn_half(n):
+            for b in range(2 * (n % 2), 2 * (n % 2) + 2):
+                turn_u2(n // 2, b)
+
+        def quant_u2(i, lo=0, hi=8):
             if lo == 0:
-                codes = pool.tile([P, GD, P], U32, name="u2_codes", bufs=3, align_bytes=64)
-                scales = pool.tile([P, GD, P], U8, name="u2_scales", bufs=3, align_bytes=64)
+                codes = pool.tile([P, 8, P], U32, name="u2_codes", bufs=3, align_bytes=64)
+                scales = pool.tile([P, 8, P], U8, name="u2_scales", bufs=3, align_bytes=64)
                 u2_codes[i] = (codes, scales)
             codes, scales = u2_codes[i]
             nc.vector.quantize_mx(
-                out=codes[:, lo:hi].rearrange("p g n -> p (g n)").bitcast(FP8X4),
-                scales=scales[:, lo:hi].rearrange("p g n -> p (g n)"),
-                in_=u2_grp[i][:, lo:hi].rearrange("p g n t -> p (g n t)"),
+                out=codes[:, lo:hi].rearrange("p c n -> p (c n)").bitcast(FP8X4),
+                scales=scales[:, lo:hi].rearrange("p c n -> p (c n)"),
+                in_=u2_grp[i][:, lo:hi].rearrange("p c n t -> p (c n t)"),
             )
 
-        w_codes = [keep.tile([P, 512], U32, name="w_codes%d" % c, align_bytes=64) for c in range(13)]
-        w_scales = [keep.tile([P, 512], U8, name="w_scales%d" % c, align_bytes=64) for c in range(13)]
+        def quant_half(n):
+            quant_u2(n // 2, 4 * (n % 2), 4 * (n % 2) + 4)
+
+        w_codes = [keep.tile([P, 512], U32, name="w_codes%d" % c, align_bytes=64) for c in range(CHUNKS)]
+        w_scales = [keep.tile([P, 512], U8, name="w_scales%d" % c, align_bytes=64) for c in range(CHUNKS)]
         w_grp = {}
 
-        def copy_w(c, engine, lo, hi):
-            if c not in w_grp:
+        def interleave_part(copy, c, lo, hi):
+            if lo == 0:
                 w_grp[c] = pool.tile([P, 2048], BF16, name="w_grp", bufs=3, align_bytes=64)
-            if c < 8:
+            if c < S1_CHUNKS:
                 dst = w_grp[c][:].rearrange("p (q t m r j) -> p t m q r j", q=4, t=8, r=2, j=4)
                 src = w_raw[c][:].rearrange("p (t j m r q) -> p t m q r j", t=8, j=4, r=2, q=4)
-                parts = [(dst[:, t], src[:, t]) for t in range(lo, hi)]
+                for t in range(lo, hi):
+                    copy(out=dst[:, t], in_=src[:, t])
             else:
-                dst = w_grp[c][:].rearrange("p (q m r j) -> p m j r q", q=2, r=2, j=4)
-                src = w_raw[c][:].rearrange("p (j m r q) -> p m j r q", j=4, r=2, q=2)
-                parts = [(dst[:, 16 * lo : 16 * hi], src[:, 16 * lo : 16 * hi])]
-            for dst, src in parts:
-                if engine == "vector":
-                    nc.vector.tensor_copy(out=dst, in_=src)
-                else:
-                    nc.scalar.copy(out=dst, in_=src)
+                dst = w_grp[c][:].rearrange("p (e m r j) -> p m j r e", e=2, r=2, j=4)
+                src = w_raw[c][:].rearrange("p (j m r e) -> p m j r e", j=4, r=2, e=2)
+                copy(out=dst[:, 16 * lo : 16 * hi], in_=src[:, 16 * lo : 16 * hi])
 
-        def quant_w(c):
-            nc.vector.quantize_mx(out=w_codes[c][:].bitcast(FP8X4), scales=w_scales[c][:], in_=w_grp[c][:])
+        def interleave(copy, n):
+            n = min(n, 8 * CHUNKS - len(eighths_done))
+            while n:
+                c, lo = divmod(len(eighths_done), 8)
+                hi = min(lo + n, 8)
+                interleave_part(copy, c, lo, hi)
+                eighths_done.extend(range(lo, hi))
+                n -= hi - lo
+                load_more()
+
+        def quant_chunks():
+            for c in range(len(chunks_quantised), len(eighths_done) // 8):
+                nc.vector.quantize_mx(out=w_codes[c][:].bitcast(FP8X4), scales=w_scales[c][:], in_=w_grp[c][:])
+                chunks_quantised.append(c)
 
         h_bank = {}
         h_grp = {}
@@ -249,7 +279,7 @@ def tile_skconv2d_pa_kernel(tc, xw_bytes, xw_scale, S1s, U1s, U2s, S2s, bias, ou
 
         def multiply(group, t, g, codes, scales, start, stop):
             if (group, t // 2) not in h_bank:
-                h_bank[group, t // 2] = psum.tile([P, 2, N], F32, name="hp", bufs=3)
+                h_bank[group, t // 2] = psum.tile([P, 2, N], F32, name="sums", bufs=8 - TURN_BANKS)
             nc.tensor.matmul_mx(
                 out=h_bank[group, t // 2][:, t % 2, :],
                 lhsT=codes.bitcast(FP8X4),
@@ -260,31 +290,32 @@ def tile_skconv2d_pa_kernel(tc, xw_bytes, xw_scale, S1s, U1s, U2s, S2s, bias, ou
                 stop=stop,
             )
 
-        def multiply_u2(i, passes=range(GD)):
+        def multiply_half(n):
+            i, pair = divmod(n, 2)
             codes, scales = u2_codes[i]
-            for c in passes:
-                if i < HEAD:
-                    t, s = divmod(c, 2)
-                    first = i == 0 and c % 4 == 0
-                    last = i == HEAD - 1 and c % 4 == 3
-                    multiply(0, t, 2 * i + s, codes[:, c, :], scales[:, c, :], first, last)
-                else:
-                    multiply(i // 4, i % 4, c, codes[:, c, :], scales[:, c, :], c == 0, c == GD - 1)
+            for c in range(4 * pair, 4 * pair + 4):
+                t, s = divmod(c, 2)
+                first = i == 0 and c % 4 == 0
+                last = i == HEAD - 1 and c % 4 == 3
+                multiply(0, t, 2 * i + s, codes[:, c, :], scales[:, c, :], first, last)
+
+        def multiply_u2(i):
+            codes, scales = u2_codes[i]
+            for g in range(PASSES):
+                multiply(i // 4, i % 4, g, codes[:, g, :], scales[:, g, :], g == 0, g == PASSES - 1)
 
         def multiply_s1(t):
             cols = slice(t * P, (t + 1) * P)
-            for g in range(GD):
-                multiply(4, t, g, w_codes[g][:, cols], w_scales[g][:, cols], g == 0, g == GD - 1)
+            for g in range(PASSES):
+                multiply(H1_GROUP, t, g, w_codes[g][:, cols], w_scales[g][:, cols], g == 0, g == PASSES - 1)
 
-        def empty_h(group, half, engine="scalar"):
-            if group not in h_grp:
+        def empty_h(group, pair):
+            if pair == 0:
                 h_grp[group] = pool.tile([P, N, 4], BF16, name="h_grp", bufs=2, align_bytes=64)
-            dst = h_grp[group][:, :, 2 * half : 2 * half + 2]
-            src = h_bank[group, half][:].rearrange("p t n -> p n t")
-            if engine == "vector":
-                nc.vector.tensor_copy(out=dst, in_=src)
-            else:
-                nc.scalar.copy(out=dst, in_=src)
+            nc.scalar.copy(
+                out=h_grp[group][:, :, 2 * pair : 2 * pair + 2],
+                in_=h_bank[group, pair][:].rearrange("p t n -> p n t"),
+            )
 
         def quant_h(group):
             nc.vector.quantize_mx(
@@ -297,164 +328,124 @@ def tile_skconv2d_pa_kernel(tc, xw_bytes, xw_scale, S1s, U1s, U2s, S2s, bias, ou
         nc.scalar.dma_start(out=x_scale[:], in_=xw_scale.rearrange("o (g p t) -> p (o g) t", p=P, t=4))
         load_x(1)
         load_x(2)
-        load_u2(0, 2)
-        load_x(3)
+        load_u2(0)
         load_u2(1)
-        load_w(0)
-        load_u2(2)
-        load_w(1)
-        load_u2(3)
-        load_u2(4)
-        load_w(2)
-        load_u2(5)
-        load_u2(6)
-        nc.sync.dma_start(
-            out=bias_in[:].rearrange("p (a m) -> p a m", a=2), in_=bias.rearrange("(a p m) -> p a m", a=2, m=2)
-        )
+        load_x(3)
+        load_more()
 
-        done = [0, 0, 3]
-
-        def turn_half(n):
-            turn_u2(n // 2, 2 * (n % 2))
-            turn_u2(n // 2, 2 * (n % 2) + 1)
-
-        def interleave(engine, n):
-            while n and done[0] < 8 * 13:
-                c, lo = divmod(done[0], 8)
-                k = min(n, 8 - lo)
-                copy_w(c, engine, lo, lo + k)
-                done[0] += k
-                n -= k
-                if UNITS - 1 in u2_raw:
-                    load_weights(13)
-
-        def load_weights(n):
-            while n and done[2] < min(13, done[0] // 8 + 6):
-                load_w(done[2])
-                done[2] += 1
-                n -= 1
-
-        def load_next(i):
-            load_u2(i)
-            if i % 3:
-                load_weights(1)
-
-        def quant_ready():
-            while done[1] < done[0] // 8:
-                quant_w(done[1])
-                done[1] += 1
-
-        for b in range(3):
+        for b in range(HEAD - 1):
             for h in range(2):
                 widen_x(b, h)
         for g in range(2):
-            turn_x(0, g)
-            scale_x(0, g)
+            turn_x(g)
+            scale_x(g)
         turn_half(0)
-        widen_x(3, 0)
-        turn_x(1, 0)
-        scale_x(1, 0)
+        turn_x(2)
+        scale_x(2)
         turn_half(1)
-        widen_x(3, 1)
-        load_next(7)
         quant_x(0)
-        quant_u2(0, 0, 4)
-        turned = 2
+        quant_half(0)
+        x_steps = PASSES - 3
+        next_half = 2
         for j in range(2 * HEAD):
-            g = j + 3
-            if j % 2 == 1 and j < 6:
+            quant_half(j + 1)
+            if j % 2 == 1 and j <= x_steps:
                 quant_x((j + 1) // 2)
-            quant_u2((j + 1) // 2, 4 * ((j + 1) % 2), 4 * ((j + 1) % 2) + 4)
-            if g < GD:
-                turn_x(g // 2, g % 2)
-            for n in range(2 if j in (5, 6) else 1):
-                turn_half(turned)
-                turned += 1
-                if turned % 2 == 0 and turned // 2 + 6 < UNITS:
-                    load_next(turned // 2 + 6)
-            if g < GD:
-                scale_x(g // 2, g % 2)
-            quant_ready()
-            if j in (0, 1, 2, 3, 4):
-                interleave("scalar", 4)
-            if 4 <= j < 6:
-                sort_u2(j, 4 - SORTED, 4)
-            elif j == 7:
-                sort_u2(6, 4 - SORTED, 4)
-            multiply_u2(j // 2, range(4 * (j % 2), 4 * (j % 2) + 4))
-        quant_u2(HEAD, 4, 8)
-        interleave("vector", 4)
-        bias2 = const.tile([P, 4], F32, name="bias2", align_bytes=64)
-        nc.vector.tensor_scalar(out=bias2[:], in0=bias_in[:], scalar1=2.0, scalar2=None, op0=MULT)
+            if j < x_steps:
+                turn_x(j + 3)
+            for n in range(2 if j in (x_steps, x_steps + 1) else 1):
+                turn_half(next_half)
+                next_half += 1
+            if j < 2:
+                widen_x(HEAD - 1, j)
+            if j < x_steps:
+                scale_x(j + 3)
+            quant_chunks()
+            if 2 <= j < x_steps:
+                interleave(nc.scalar.copy, SCALAR_HEAD_SHARE)
+            if j in (HEAD, HEAD + 1):
+                sort_u2(j)
+            elif j == 2 * HEAD - 1:
+                sort_u2(HEAD + 2)
+            multiply_half(j)
+        quant_half(2 * HEAD + 1)
+        interleave(nc.vector.tensor_copy, VECTOR_GAP_SHARE)
+
         for i in range(HEAD, UNITS):
-            if i + 2 < UNITS:
+            turning = i + 2 < UNITS
+            sorting = i + 3 < UNITS
+            pair_closed = i % 2 == 0 and i > HEAD
+            if turning:
                 for b in range(4):
                     turn_u2(i + 2, b)
                     if i == HEAD and b % 2 == 1:
                         empty_h(0, b // 2)
-                    if b == 1 and i % 2 == 0 and i > HEAD:
-                        empty_h((i - 1) // 4, ((i - 1) % 4) // 2)
-            if i + 9 < UNITS:
-                load_next(i + 9)
-            if i + 3 < UNITS:
-                sort_u2(i + 3, 4 - SORTED, 4)
-            quant_ready()
-            if i == 14:
-                empty_h(3, 0)
-            interleave("vector", 4 if i < 13 else 0)
+                    if pair_closed and b == 1:
+                        empty_h((i - 1) // 4, (i - 1) % 4 // 2)
+            elif pair_closed:
+                empty_h((i - 1) // 4, (i - 1) % 4 // 2)
+            quant_chunks()
+            if sorting:
+                interleave(nc.vector.tensor_copy, VECTOR_SHARE)
+                sort_u2(i + 3)
             if i + 1 < UNITS:
                 quant_u2(i + 1)
             if i % 4 == 1:
                 quant_h(i // 4 - 1)
-            interleave("vector", 0 if i < 13 else 8)
-            interleave("scalar", 1 if i < 14 else 6)
-            if i == 15:
+            if not sorting:
+                interleave(nc.vector.tensor_copy, VECTOR_END_SHARE)
+            if not turning:
+                interleave(nc.scalar.copy, SCALAR_END_SHARE)
+            elif i % 2 == 1:
+                interleave(nc.scalar.copy, SCALAR_SHARE)
+            if i == UNITS - 1:
                 multiply_s1(0)
                 multiply_s1(1)
-                empty_h(4, 0)
+                empty_h(H1_GROUP, 0)
             multiply_u2(i)
-        quant_ready()
+        nc.sync.dma_start(
+            out=bias_in[:].rearrange("p (a e) -> p a e", a=2), in_=bias.rearrange("(a p e) -> p a e", a=2, e=2)
+        )
+        quant_chunks()
+        bias2 = const.tile([P, 4], F32, name="bias2", align_bytes=64)
+        nc.vector.tensor_scalar(out=bias2[:], in0=bias_in[:], scalar1=2.0, scalar2=None, op0=MULT)
         empty_h(3, 1)
-        interleave("vector", 8)
-        interleave("scalar", 4)
         multiply_s1(2)
         multiply_s1(3)
         quant_h(3)
-        quant_ready()
-        interleave("vector", 99)
-        empty_h(4, 1)
-        quant_ready()
-        quant_h(4)
+        empty_h(H1_GROUP, 1)
+        quant_h(H1_GROUP)
 
-        acc = [psum.tile([P, 512], F32, name="tp", bufs=5) for m in range(4)]
+        acc = [psum.tile([P, 512], F32, name="turn", bufs=TURN_BANKS) for m in range(4)]
+        for groups in (range(0, 3), range(3, 5)):
+            for a in range(2):
+                for group in groups:
+                    c = S1_CHUNKS + group
+                    for e in range(2):
+                        cols = slice(256 * e + P * a, 256 * e + P * (a + 1))
+                        nc.tensor.matmul_mx(
+                            out=acc[2 * a + e][:, :N],
+                            lhsT=w_codes[c][:, cols].bitcast(FP8X4),
+                            lhsT_scale=w_scales[c][:, cols],
+                            rhs=h_codes[group][:].bitcast(FP8X4),
+                            rhs_scale=h_scales[group][:],
+                            start=(group == 0),
+                            stop=(group == H1_GROUP),
+                        )
 
-        def second(m, n, group):
-            cols = slice((2 * (m % 2) + m // 2) * P, (2 * (m % 2) + m // 2 + 1) * P)
-            w = 12 if group == 4 else 8 + group
-            nc.tensor.matmul_mx(
-                out=acc[m][:, :N],
-                lhsT=w_codes[w][:, cols].bitcast(FP8X4),
-                lhsT_scale=w_scales[w][:, cols],
-                rhs=h_codes[group][:].bitcast(FP8X4),
-                rhs_scale=h_scales[group][:],
-                start=(n == 0),
-                stop=(n == 4),
+        result = [keep.tile([P, 4, 2, 64], F32, name="result%d" % a, align_bytes=64) for a in range(2)]
+        out_view = out.rearrange("b (a p e) i j -> a p b (e i j)", a=2, e=2)
+        for a in range(2):
+            even, odd = (acc[2 * a + e][:, :N].rearrange("p (b s) -> p b s", b=4) for e in range(2))
+            nc.scalar.activation(
+                out=result[a][:, :, 0, :], in_=even, func=IDENTITY, bias=bias2[:, 2 * a : 2 * a + 1], scale=0.125
             )
-
-        order = [0, 1, 2, 3, 4]
-        for part in (range(0, 3), range(3, 5)):
-            for pair in range(2):
-                for n in part:
-                    for m in range(2 * pair, 2 * pair + 2):
-                        second(m, n, order[n])
-        result = [keep.tile([P, 4, 2, 64], F32, name="result%d" % m, align_bytes=64) for m in range(2)]
-        out_view = out.rearrange("b (a p m) i j -> a p b (m i j)", a=2, m=2)
-        for m in range(4):
-            src = acc[m][:, :N].rearrange("p (b s) -> p b s", b=4)
-            if m % 2 == 0:
-                nc.scalar.activation(out=result[m // 2][:, :, m % 2, :], in_=src, func=IDENTITY, bias=bias2[:, m : m + 1], scale=0.125)
-            else:
-                nc.vector.tensor_scalar(
-                    out=result[m // 2][:, :, m % 2, :], in0=src, scalar1=0.125, scalar2=bias2[:, m : m + 1], op0=MULT, op1=ADD
-                )
-                nc.sync.dma_start(out=out_view[m // 2], in_=result[m // 2][:].rearrange("p b m s -> p b (m s)"))
+            nc.vector.tensor_scalar(
+                out=result[a][:, :, 1, :],
+                in0=odd,
+                scalar1=0.125,
+                scalar2=bias2[:, 2 * a + 1 : 2 * a + 2],
+                op0=MULT,
+                op1=ADD,
+            )
+            nc.sync.dma_start(out=out_view[a], in_=result[a][:].rearrange("p b e s -> p b (e s)"))

@@ -22,22 +22,44 @@ K2 = 2048
 PASSES = D // 512
 UNITS = 16
 HEAD = 4
+PIECES = 8
 S1_CHUNKS = 8
 CHUNKS = 13
 H1_GROUP = 4
 U1_CHUNK = 12
 RAW_UNITS = 7
 RAW_CHUNKS = 6
-TURN_BANKS = 5
+GRP_CHUNKS = 4
+GRP_UNITS = 5
+CODE_UNITS = 4
+TURN_BANKS = 4
 
-X_BY_MATMUL = 2
-SORTED = 2
-SCALAR_HEAD_SHARE = 4
-VECTOR_GAP_SHARE = 2
-VECTOR_SHARE = 5
-SCALAR_SHARE = 2
-VECTOR_END_SHARE = 8
-SCALAR_END_SHARE = 6
+V_EVERY = 4
+SORT_EVEN = 3
+SORT_ODD = 3
+SORT_FROM = 4
+SORT_LATE = 15
+SORT_END = 2
+DOUBLE = 1
+H1_STEP = 13
+FIRST = 4
+LAST = 15
+G_EARLY = 1
+CLAG = 0
+Q0 = 2
+Q1 = 5
+S2_EARLY = 2
+V_EVEN = 3
+V_ODD = 3
+S_EVEN = 1
+S_ODD = 1
+S_EXTRA = 2
+S_GAP = 0
+S_STOP = 15
+V_LATE = 4
+V_END = 0
+V_END2 = 4
+S_END = 2
 
 FLOPS = 2 * N * D * (K1 + K2) + 2 * N * (K1 + K2) * O
 
@@ -55,13 +77,13 @@ def tile_skconv2d_pa_kernel(tc, xw_bytes, xw_scale, S1s, U1s, U2s, S2s, bias, ou
         u2_rows = U2s.rearrange("t r d -> (t r) d").rearrange("(g p t) d -> g p t d", p=P, t=4)
         s1_rows = S1s.rearrange("t (g p j) r -> g p t (j r)", p=P, j=4)
         s2_rows = S2s.rearrange("t r o -> (t r) o").rearrange("(g p j) o -> g p (j o)", p=P, j=4)
-        u1_rows = U1s.rearrange("t r o -> (t r) o").rearrange("(p j) o -> p (j o)", j=4)
-        x_rows = xw_bytes.rearrange("(h p) d -> p h d", p=P)
+        u1_rows = U1s.rearrange("t r o -> (t r) o").rearrange("(a q i) o -> i a q o", q=4, i=4)
+        x_rows = xw_bytes.rearrange("(h p) d -> h p d", p=P)
 
-        ident = const.tile([P, P], F32, name="ident", align_bytes=64)
-        make_identity(nc, ident[:])
         ident_bf = const.tile([P, P], BF16, name="ident_bf", align_bytes=64)
         make_identity(nc, ident_bf[:])
+        ident = const.tile([P, P], F32, name="ident", align_bytes=64)
+        make_identity(nc, ident[:])
         ones = const.tile([P, 1], F32, name="ones", align_bytes=64)
         nc.vector.memset(ones[:], 1.0)
         x_scale = const.tile([P, PASSES, 4], F32, name="x_scale", align_bytes=64)
@@ -71,24 +93,18 @@ def tile_skconv2d_pa_kernel(tc, xw_bytes, xw_scale, S1s, U1s, U2s, S2s, bias, ou
         x_in = {}
         w_raw = {}
 
-        def load_x(b):
-            x_in[b] = keep.tile([P, 2, 1024], U8, name="x_in%d" % b, align_bytes=64)
-            k = 1 if b == 0 else 2
-            for h in range(0, 2, k):
-                nc.sync.dma_start(out=x_in[b][:, h : h + k], in_=x_rows[:, h : h + k, b * 1024 : (b + 1) * 1024])
+        def load_x(lo, hi):
+            t = keep.tile([P, (hi - lo) * 1024], U8, name="x_in%d" % lo, align_bytes=64)
+            c = lo % 4 * 1024
+            nc.sync.dma_start(out=t[:], in_=x_rows[lo // 4][:, c : c + (hi - lo) * 1024])
+            for a in range(lo, hi):
+                x_in[a] = t[:, (a - lo) * 1024 : (a - lo + 1) * 1024]
 
-        def load_u2(i):
-            raw = pool.tile([P, D], BF16, name="u2_raw", bufs=RAW_UNITS, align_bytes=64)
-            if i < HEAD:
-                k = 2 if i == 0 else 4
-                for t in range(0, 4, k):
-                    nc.sync.dma_start(
-                        out=raw[:, t * 1024 : (t + k) * 1024].rearrange("p (t d) -> p t d", t=k),
-                        in_=u2_rows[0][:, t : t + k, i * 1024 : (i + 1) * 1024],
-                    )
-            else:
-                nc.sync.dma_start(out=raw[:], in_=u2_rows[i // 4][:, i % 4, :])
-            u2_raw[i] = raw
+        def load_u2(i, lo=0, hi=4):
+            if lo == 0:
+                u2_raw[i] = pool.tile([P, D], BF16, name="u2_raw", bufs=RAW_UNITS, align_bytes=64)
+            cols = slice(lo * 1024, hi * 1024)
+            nc.sync.dma_start(out=u2_raw[i][:, cols], in_=u2_rows[i // 4][:, i % 4, cols])
 
         def load_w(c):
             raw = pool.tile([P, 2048], BF16, name="w_raw", bufs=RAW_CHUNKS, align_bytes=64)
@@ -97,123 +113,119 @@ def tile_skconv2d_pa_kernel(tc, xw_bytes, xw_scale, S1s, U1s, U2s, S2s, bias, ou
             elif c < U1_CHUNK:
                 nc.sync.dma_start(out=raw[:], in_=s2_rows[c - S1_CHUNKS])
             else:
-                nc.sync.dma_start(out=raw[:], in_=u1_rows)
+                for i in range(4):
+                    nc.sync.dma_start(out=raw[i:P:4, :].rearrange("p (q o) -> p q o", q=4), in_=u1_rows[i])
             w_raw[c] = raw
 
+        order = list(range(S1_CHUNKS)) + [8, 9, 10, U1_CHUNK, 11]
+        behind = [min(FIRST + n, LAST) for n in range(CHUNKS)]
         queue = []
         for i in range(2, UNITS):
             queue.append(("unit", i))
-            queue.extend(("chunk", c) for c in range(S1_CHUNKS) if 2 + (UNITS - 2) * c // S1_CHUNKS == i)
-        queue.extend(("chunk", c) for c in range(S1_CHUNKS, CHUNKS))
+            queue.extend(("chunk", n) for n in range(CHUNKS) if behind[n] == i)
         units_turned = []
-        eighths_done = []
+        quarters_done = []
         chunks_quantised = []
+        x_quantised = []
 
         def load_more():
             while queue:
                 kind, n = queue[0]
                 if kind == "unit" and n < len(units_turned) + RAW_UNITS:
                     load_u2(n)
-                elif kind == "chunk" and n < len(eighths_done) // 8 + RAW_CHUNKS:
-                    load_w(n)
+                elif kind == "chunk" and n + 4 < len(x_quantised) + len(quarters_done) // 4 + RAW_CHUNKS:
+                    load_w(order[n])
                 else:
                     return
                 queue.pop(0)
 
-        x_codes = keep.tile([P, PASSES, N], U32, name="x_codes", align_bytes=64)
-        x_scales = keep.tile([P, PASSES, N], U8, name="x_scales", align_bytes=64)
+        x_codes = keep.tile([P, PASSES * N], U32, name="x_codes", align_bytes=64)
+        x_scales = keep.tile([P, PASSES * N], U8, name="x_scales", align_bytes=64)
         x_bf = {}
         x_bank = {}
-        x_grp = {}
+        x_grp = [pool.tile([P, 2048], BF16, name="w_raw", bufs=RAW_CHUNKS, align_bytes=64) for b in range(4)]
 
-        def widen_x(b, h):
-            wide = pool.tile([P, 1024], BF16, name="x_bf", bufs=2 * HEAD, align_bytes=64)
-            src = x_in[b][:, h, :].bitcast(FP8)
-            if b < X_BY_MATMUL:
+        def widen_x(a):
+            if a % 2 == 0:
+                x_bf[a // 2] = pool.tile([P, 2048], BF16, name="w_grp", bufs=GRP_CHUNKS, align_bytes=64)
+            wide = x_bf[a // 2][:, a % 2 * 1024 : (a % 2 + 1) * 1024]
+            src = x_in[a].bitcast(FP8)
+            if a % V_EVERY == 0:
                 nc.vector.tensor_scalar(
-                    out=wide[:].rearrange("p (s t m) -> p s m t", s=2, t=4),
+                    out=wide.rearrange("p (s t m) -> p s m t", s=2, t=4),
                     in0=src.rearrange("p (s m t) -> p s m t", s=2, t=4),
                     scalar1=ones[:],
                     scalar2=None,
                     op0=MULT,
                 )
             else:
-                nc.scalar.copy(out=wide[:], in_=src)
-            x_bf[b, h] = wide
+                nc.scalar.copy(out=wide, in_=src)
 
-        def turn_x(g):
-            b, s = divmod(g, 2)
-            if b < X_BY_MATMUL:
-                for h in range(2):
-                    xt = psum.tile([P, 4, P], F32, name="turn", bufs=TURN_BANKS)
-                    for t in range(4):
-                        c = (4 * s + t) * P
-                        nc.tensor.matmul(xt[:, t, :], x_bf[b, h][:, c : c + P], ident_bf[:], start=True, stop=True)
-                    x_bank[g, h] = xt
-            else:
-                xt = psum.tile([P, 2, N], F32, name="turn", bufs=TURN_BANKS)
-                for h in range(2):
-                    words = x_bf[b, h][:].bitcast(F32)
-                    for u in range(2):
-                        src = words[:, 256 * s + u : 256 * (s + 1) : 2]
-                        nc.tensor.transpose(xt[:, u, h * P : (h + 1) * P], src, ident[:])
-                x_bank[g] = xt
-
-        def scale_x(g):
-            b, s = divmod(g, 2)
-            if s == 0:
-                x_grp[b] = pool.tile([P, 2, N, 4], BF16, name="x_grp", bufs=2, align_bytes=64)
-            factor = x_scale[:, g : g + 1, :]
-            if b < X_BY_MATMUL:
-                for h in range(2):
-                    nc.vector.tensor_tensor(
-                        out=x_grp[b][:, s, h * P : (h + 1) * P, :],
-                        in0=x_bank[g, h][:].rearrange("p t n -> p n t"),
-                        in1=factor.to_broadcast([P, P, 4]),
-                        op=MULT,
-                    )
-            else:
-                values = x_bank[g][:].rearrange("p u n -> p (u n)").bitcast(BF16)
+        def turn_x(a):
+            wide = x_bf[a // 2][:, a % 2 * 1024 : (a % 2 + 1) * 1024]
+            for s in range(2):
+                xt = psum.tile([P, 4, P], F32, name="long" if s else "sums", bufs=2)
+                for t in range(4):
+                    if a % V_EVERY == 0:
+                        src = wide[:, (4 * s + t) * P : (4 * s + t + 1) * P]
+                    else:
+                        src = wide[:, 512 * s + t : 512 * (s + 1) : 4]
+                    nc.tensor.matmul(xt[:, t, :], src, ident_bf[:], start=True, stop=True)
+                x_bank[a, s] = xt
+                h, b = divmod(a, 4)
+                g = 2 * b + s
+                c = s * 1024 + h * 512
                 nc.vector.tensor_tensor(
-                    out=x_grp[b][:, s].rearrange("p n (u e) -> p n u e", u=2),
-                    in0=values.rearrange("p (u n e) -> p n u e", u=2, e=2),
-                    in1=factor.rearrange("p o (u e) -> p o u e", u=2).to_broadcast([P, N, 2, 2]),
+                    out=x_grp[b][:, c : c + 512].rearrange("p (n t) -> p n t", t=4),
+                    in0=xt[:].rearrange("p t n -> p n t"),
+                    in1=x_scale[:, g : g + 1, :].to_broadcast([P, P, 4]),
                     op=MULT,
                 )
 
         def quant_x(b):
-            nc.vector.quantize_mx(
-                out=x_codes[:, 2 * b : 2 * b + 2, :].rearrange("p g n -> p (g n)").bitcast(FP8X4),
-                scales=x_scales[:, 2 * b : 2 * b + 2, :].rearrange("p g n -> p (g n)"),
-                in_=x_grp[b][:].rearrange("p g n t -> p (g n t)"),
-            )
+            cols = slice(2 * b * N, (2 * b + 2) * N)
+            nc.vector.quantize_mx(out=x_codes[:, cols].bitcast(FP8X4), scales=x_scales[:, cols], in_=x_grp[b][:])
+            x_quantised.append(b)
+            load_more()
 
         u2_sorted = {}
         u2_grp = {}
         u2_codes = {}
 
+        def sorted_banks(i):
+            if i < SORT_FROM:
+                return 0
+            if i >= SORT_LATE:
+                return SORT_END
+            return SORT_ODD if i % 2 else SORT_EVEN
+
         def sort_u2(i):
-            srt = pool.tile([P, 2 * SORTED, 2, P], F32, name="u2_sorted", bufs=2, align_bytes=64)
-            words = u2_raw[i][:].bitcast(F32)[:, (4 - SORTED) * 512 :]
-            nc.vector.tensor_copy(
-                out=srt[:].rearrange("p c u w -> p c w u"), in_=words.rearrange("p (c w u) -> p c w u", w=P, u=2)
-            )
-            u2_sorted[i] = srt
+            k = sorted_banks(i)
+            if k:
+                srt = pool.tile([P, 512 * k], F32, name="u2_sorted", bufs=2, align_bytes=64)
+                words = u2_raw[i][:].bitcast(F32)[:, (4 - k) * 512 :]
+                nc.vector.tensor_copy(
+                    out=srt[:].rearrange("p (c u w) -> p c w u", u=2, w=P),
+                    in_=words.rearrange("p (c w u) -> p c w u", w=P, u=2),
+                )
+                u2_sorted[i] = srt
 
         def turn_u2(i, b):
             if b == 0:
-                u2_grp[i] = pool.tile([P, 8, P, 4], BF16, name="u2_grp", bufs=3, align_bytes=64)
+                u2_grp[i] = pool.tile([P, D], BF16, name="u2_grp", bufs=GRP_UNITS, align_bytes=64)
             words = u2_raw[i][:].bitcast(F32)
             ut = psum.tile([P, 2, 2, P], F32, name="turn", bufs=TURN_BANKS)
+            first = 4 - sorted_banks(i)
             for s in range(2):
                 c = 2 * b + s
                 for u in range(2):
-                    if i >= HEAD and b >= 4 - SORTED:
-                        src = u2_sorted[i][:, c - 2 * (4 - SORTED), u, :]
+                    if b >= first:
+                        w = 256 * (c - 2 * first) + P * u
+                        src = u2_sorted[i][:, w : w + P]
                     else:
                         src = words[:, 256 * c + u : 256 * (c + 1) : 2]
                     nc.tensor.transpose(ut[:, s, u, :], src, ident[:])
-            dst = u2_grp[i][:, 2 * b : 2 * b + 2].rearrange("p s n t -> p (s n t)").bitcast(F32)
+            dst = u2_grp[i][:, 1024 * b : 1024 * (b + 1)].bitcast(F32)
             nc.scalar.copy(
                 out=dst.rearrange("p (s n u) -> p s n u", s=2, u=2), in_=ut[:].rearrange("p s u n -> p s n u")
             )
@@ -221,24 +233,17 @@ def tile_skconv2d_pa_kernel(tc, xw_bytes, xw_scale, S1s, U1s, U2s, S2s, bias, ou
                 units_turned.append(i)
                 load_more()
 
-        def turn_half(n):
-            for b in range(2 * (n % 2), 2 * (n % 2) + 2):
-                turn_u2(n // 2, b)
-
         def quant_u2(i, lo=0, hi=8):
             if lo == 0:
-                codes = pool.tile([P, 8, P], U32, name="u2_codes", bufs=3, align_bytes=64)
-                scales = pool.tile([P, 8, P], U8, name="u2_scales", bufs=3, align_bytes=64)
+                codes = pool.tile([P, 8 * P], U32, name="u2_codes", bufs=CODE_UNITS, align_bytes=64)
+                scales = pool.tile([P, 8 * P], U8, name="u2_scales", bufs=CODE_UNITS, align_bytes=64)
                 u2_codes[i] = (codes, scales)
             codes, scales = u2_codes[i]
             nc.vector.quantize_mx(
-                out=codes[:, lo:hi].rearrange("p c n -> p (c n)").bitcast(FP8X4),
-                scales=scales[:, lo:hi].rearrange("p c n -> p (c n)"),
-                in_=u2_grp[i][:, lo:hi].rearrange("p c n t -> p (c n t)"),
+                out=codes[:, lo * P : hi * P].bitcast(FP8X4),
+                scales=scales[:, lo * P : hi * P],
+                in_=u2_grp[i][:, lo * 512 : hi * 512],
             )
-
-        def quant_half(n):
-            quant_u2(n // 2, 4 * (n % 2), 4 * (n % 2) + 4)
 
         w_codes = [keep.tile([P, 512], U32, name="w_codes%d" % c, align_bytes=64) for c in range(CHUNKS)]
         w_scales = [keep.tile([P, 512], U8, name="w_scales%d" % c, align_bytes=64) for c in range(CHUNKS)]
@@ -246,29 +251,30 @@ def tile_skconv2d_pa_kernel(tc, xw_bytes, xw_scale, S1s, U1s, U2s, S2s, bias, ou
 
         def interleave_part(copy, c, lo, hi):
             if lo == 0:
-                w_grp[c] = pool.tile([P, 2048], BF16, name="w_grp", bufs=3, align_bytes=64)
+                w_grp[c] = pool.tile([P, 2048], BF16, name="w_grp", bufs=GRP_CHUNKS, align_bytes=64)
             if c < S1_CHUNKS:
-                dst = w_grp[c][:].rearrange("p (q t m r j) -> p t m q r j", q=4, t=8, r=2, j=4)
-                src = w_raw[c][:].rearrange("p (t j m r q) -> p t m q r j", t=8, j=4, r=2, q=4)
-                for t in range(lo, hi):
-                    copy(out=dst[:, t], in_=src[:, t])
+                dst = w_grp[c][:].rearrange("p (q a i j) -> p a q j i", q=4, i=4, j=4)
+                src = w_raw[c][:].rearrange("p (t j m i) -> p t m j i", t=8, j=4, i=4)
+                copy(out=dst[:, 8 * lo : 8 * hi], in_=src[:, 2 * lo : 2 * hi])
             else:
                 dst = w_grp[c][:].rearrange("p (e m r j) -> p m j r e", e=2, r=2, j=4)
                 src = w_raw[c][:].rearrange("p (j m r e) -> p m j r e", j=4, r=2, e=2)
-                copy(out=dst[:, 16 * lo : 16 * hi], in_=src[:, 16 * lo : 16 * hi])
+                copy(out=dst[:, 32 * lo : 32 * hi], in_=src[:, 32 * lo : 32 * hi])
 
-        def interleave(copy, n):
-            n = min(n, 8 * CHUNKS - len(eighths_done))
+        def interleave(copy, n, step=2 * UNITS):
+            landed = sum(1 for u in behind if u + CLAG <= step)
+            n = max(0, min(n, 4 * landed - len(quarters_done)))
             while n:
-                c, lo = divmod(len(eighths_done), 8)
-                hi = min(lo + n, 8)
-                interleave_part(copy, c, lo, hi)
-                eighths_done.extend(range(lo, hi))
+                c, lo = divmod(len(quarters_done), 4)
+                hi = min(lo + n, 4)
+                interleave_part(copy, order[c], lo, hi)
+                quarters_done.extend(range(lo, hi))
                 n -= hi - lo
                 load_more()
 
         def quant_chunks():
-            for c in range(len(chunks_quantised), len(eighths_done) // 8):
+            for n in range(len(chunks_quantised), len(quarters_done) // 4):
+                c = order[n]
                 nc.vector.quantize_mx(out=w_codes[c][:].bitcast(FP8X4), scales=w_scales[c][:], in_=w_grp[c][:])
                 chunks_quantised.append(c)
 
@@ -276,166 +282,160 @@ def tile_skconv2d_pa_kernel(tc, xw_bytes, xw_scale, S1s, U1s, U2s, S2s, bias, ou
         h_grp = {}
         h_codes = [keep.tile([P, N], U32, name="h_codes%d" % g, align_bytes=64) for g in range(5)]
         h_scales = [keep.tile([P, N], U8, name="h_scales%d" % g, align_bytes=64) for g in range(5)]
+        closed = []
+        emptied = []
 
         def multiply(group, t, g, codes, scales, start, stop):
-            if (group, t // 2) not in h_bank:
-                h_bank[group, t // 2] = psum.tile([P, 2, N], F32, name="sums", bufs=8 - TURN_BANKS)
             nc.tensor.matmul_mx(
                 out=h_bank[group, t // 2][:, t % 2, :],
                 lhsT=codes.bitcast(FP8X4),
                 lhsT_scale=scales,
-                rhs=x_codes[:, g, :].bitcast(FP8X4),
-                rhs_scale=x_scales[:, g, :],
+                rhs=x_codes[:, g * N : (g + 1) * N].bitcast(FP8X4),
+                rhs_scale=x_scales[:, g * N : (g + 1) * N],
                 start=start,
                 stop=stop,
             )
 
-        def multiply_half(n):
-            i, pair = divmod(n, 2)
-            codes, scales = u2_codes[i]
-            for c in range(4 * pair, 4 * pair + 4):
-                t, s = divmod(c, 2)
-                first = i == 0 and c % 4 == 0
-                last = i == HEAD - 1 and c % 4 == 3
-                multiply(0, t, 2 * i + s, codes[:, c, :], scales[:, c, :], first, last)
-
         def multiply_u2(i):
+            group, t = divmod(i, 4)
+            if t % 2 == 0:
+                h_bank[group, t // 2] = psum.tile([P, 2, N], F32, name="sums", bufs=2)
             codes, scales = u2_codes[i]
             for g in range(PASSES):
-                multiply(i // 4, i % 4, g, codes[:, g, :], scales[:, g, :], g == 0, g == PASSES - 1)
+                cols = slice(g * P, (g + 1) * P)
+                multiply(group, t, g, codes[:, cols], scales[:, cols], g == 0, g == PASSES - 1)
+            if t % 2 == 1:
+                closed.append((group, t // 2))
 
-        def multiply_s1(t):
-            cols = slice(t * P, (t + 1) * P)
-            for g in range(PASSES):
-                multiply(H1_GROUP, t, g, w_codes[g][:, cols], w_scales[g][:, cols], g == 0, g == PASSES - 1)
+        def multiply_s1(g):
+            for t in range(4):
+                if g == 0 and t % 2 == 0:
+                    h_bank[H1_GROUP, t // 2] = psum.tile([P, 2, N], F32, name="long", bufs=2)
+                cols = slice(t * P, (t + 1) * P)
+                first = g == 0 and t % 2 == 0
+                last = g == PASSES - 1 and t % 2 == 1
+                multiply(H1_GROUP, t, g, w_codes[g][:, cols], w_scales[g][:, cols], first, last)
 
-        def empty_h(group, pair):
-            if pair == 0:
-                h_grp[group] = pool.tile([P, N, 4], BF16, name="h_grp", bufs=2, align_bytes=64)
-            nc.scalar.copy(
-                out=h_grp[group][:, :, 2 * pair : 2 * pair + 2],
-                in_=h_bank[group, pair][:].rearrange("p t n -> p n t"),
-            )
+        def empty_h():
+            while closed:
+                group, pair = closed.pop(0)
+                if pair == 0:
+                    h_grp[group] = pool.tile([P, N * 4], BF16, name="h_grp", bufs=2, align_bytes=64)
+                nc.scalar.copy(
+                    out=h_grp[group][:].rearrange("p (n t) -> p n t", t=4)[:, :, 2 * pair : 2 * pair + 2],
+                    in_=h_bank[group, pair][:].rearrange("p t n -> p n t"),
+                )
+                if pair == 1:
+                    emptied.append(group)
 
-        def quant_h(group):
-            nc.vector.quantize_mx(
-                out=h_codes[group][:].bitcast(FP8X4),
-                scales=h_scales[group][:],
-                in_=h_grp[group][:].rearrange("p n t -> p (n t)"),
-            )
+        def quant_h():
+            while emptied:
+                group = emptied.pop(0)
+                nc.vector.quantize_mx(
+                    out=h_codes[group][:].bitcast(FP8X4), scales=h_scales[group][:], in_=h_grp[group][:]
+                )
 
-        load_x(0)
+        acc = []
+
+        def project(group, pairs=(0, 1)):
+            c = S1_CHUNKS + group
+            for a in pairs:
+                for e in range(2):
+                    if group == 0:
+                        acc.append(psum.tile([P, 512], F32, name="turn", bufs=TURN_BANKS))
+                    cols = slice(256 * e + P * a, 256 * e + P * (a + 1))
+                    nc.tensor.matmul_mx(
+                        out=acc[2 * a + e][:, :N],
+                        lhsT=w_codes[c][:, cols].bitcast(FP8X4),
+                        lhsT_scale=w_scales[c][:, cols],
+                        rhs=h_codes[group][:].bitcast(FP8X4),
+                        rhs_scale=h_scales[group][:],
+                        start=group == 0,
+                        stop=group == 3,
+                    )
+
+        load_x(0, 1)
         nc.scalar.dma_start(out=x_scale[:], in_=xw_scale.rearrange("o (g p t) -> p (o g) t", p=P, t=4))
-        load_x(1)
-        load_x(2)
-        load_u2(0)
-        load_u2(1)
-        load_x(3)
+        load_x(1, 2)
+        load_u2(0, 0, 2)
+        load_x(2, 4)
+        load_u2(0, 2, 4)
+        load_x(4, 6)
+        load_u2(1, 0, 2)
+        load_x(6, 8)
+        load_u2(1, 2, 4)
         load_more()
 
-        for b in range(HEAD - 1):
-            for h in range(2):
-                widen_x(b, h)
-        for g in range(2):
-            turn_x(g)
-            scale_x(g)
-        turn_half(0)
-        turn_x(2)
-        scale_x(2)
-        turn_half(1)
-        quant_x(0)
-        quant_half(0)
-        x_steps = PASSES - 3
-        next_half = 2
-        for j in range(2 * HEAD):
-            quant_half(j + 1)
-            if j % 2 == 1 and j <= x_steps:
-                quant_x((j + 1) // 2)
-            if j < x_steps:
-                turn_x(j + 3)
-            for n in range(2 if j in (x_steps, x_steps + 1) else 1):
-                turn_half(next_half)
-                next_half += 1
-            if j < 2:
-                widen_x(HEAD - 1, j)
-            if j < x_steps:
-                scale_x(j + 3)
-            quant_chunks()
-            if 2 <= j < x_steps:
-                interleave(nc.scalar.copy, SCALAR_HEAD_SHARE)
-            if j in (HEAD, HEAD + 1):
-                sort_u2(j)
-            elif j == 2 * HEAD - 1:
-                sort_u2(HEAD + 2)
-            multiply_half(j)
-        quant_half(2 * HEAD + 1)
-        interleave(nc.vector.tensor_copy, VECTOR_GAP_SHARE)
+        for a in range(3):
+            widen_x(a)
+        turn_x(0)
+        for a in range(PIECES):
+            if a + 1 < PIECES:
+                turn_x(a + 1)
+            if a + 3 < PIECES:
+                widen_x(a + 3)
+            if a == PIECES - 1:
+                sort_u2(HEAD)
+            if a >= 4:
+                quant_x(a - 4)
+            if Q0 <= a < Q0 + 2:
+                quant_u2(0, 4 * (a - Q0), 4 * (a - Q0 + 1))
+            for b in range(2 * (a % 2), 2 * (a % 2) + 2):
+                turn_u2(a // 2, b)
+        multiply_u2(0)
+        quant_u2(1)
 
+        quantised = 2
+        multiplied = 1
+        s1_done = 0
+        interleave(nc.scalar.copy, S_GAP, HEAD)
         for i in range(HEAD, UNITS):
-            turning = i + 2 < UNITS
-            sorting = i + 3 < UNITS
-            pair_closed = i % 2 == 0 and i > HEAD
-            if turning:
-                for b in range(4):
-                    turn_u2(i + 2, b)
-                    if i == HEAD and b % 2 == 1:
-                        empty_h(0, b // 2)
-                    if pair_closed and b == 1:
-                        empty_h((i - 1) // 4, (i - 1) % 4 // 2)
-            elif pair_closed:
-                empty_h((i - 1) // 4, (i - 1) % 4 // 2)
+            ready = min(len(chunks_quantised), S1_CHUNKS)
+            empty_h()
+            for b in range(4):
+                turn_u2(i, b)
+            if i - HEAD < DOUBLE:
+                quant_u2(quantised)
+                quantised += 1
+            interleave(nc.vector.tensor_copy, -len(quarters_done) % 4 or 4, i - 1)
+            if quantised < i:
+                quant_u2(quantised)
+                quantised += 1
             quant_chunks()
-            if sorting:
-                interleave(nc.vector.tensor_copy, VECTOR_SHARE)
-                sort_u2(i + 3)
+            quant_h()
             if i + 1 < UNITS:
-                quant_u2(i + 1)
-            if i % 4 == 1:
-                quant_h(i // 4 - 1)
-            if not sorting:
-                interleave(nc.vector.tensor_copy, VECTOR_END_SHARE)
-            if not turning:
-                interleave(nc.scalar.copy, SCALAR_END_SHARE)
-            elif i % 2 == 1:
-                interleave(nc.scalar.copy, SCALAR_SHARE)
-            if i == UNITS - 1:
-                multiply_s1(0)
-                multiply_s1(1)
-                empty_h(H1_GROUP, 0)
-            multiply_u2(i)
+                sort_u2(i + 1)
+            interleave(nc.scalar.copy, 0 if i >= S_STOP else S_ODD if i % 2 else S_EVEN, i)
+            for n in range(2 if i - HEAD < DOUBLE else 1):
+                multiply_u2(multiplied)
+                multiplied += 1
+            for g in range(s1_done, ready):
+                multiply_s1(g)
+                s1_done += 1
         nc.sync.dma_start(
             out=bias_in[:].rearrange("p (a e) -> p a e", a=2), in_=bias.rearrange("(a p e) -> p a e", a=2, e=2)
         )
+        interleave(nc.vector.tensor_copy, V_END)
+        quant_u2(UNITS - 1, 0, 4)
+        interleave(nc.vector.tensor_copy, V_END2)
+        quant_u2(UNITS - 1, 4, 8)
+        closed[:] = [(H1_GROUP, 0), (3, 0), (H1_GROUP, 1)]
+        empty_h()
+        multiply_u2(UNITS - 2)
+        multiply_u2(UNITS - 1)
+        interleave(nc.vector.tensor_copy, 4 * CHUNKS)
         quant_chunks()
+        quant_h()
+        empty_h()
+        quant_h()
         bias2 = const.tile([P, 4], F32, name="bias2", align_bytes=64)
         nc.vector.tensor_scalar(out=bias2[:], in0=bias_in[:], scalar1=2.0, scalar2=None, op0=MULT)
-        empty_h(3, 1)
-        multiply_s1(2)
-        multiply_s1(3)
-        quant_h(3)
-        empty_h(H1_GROUP, 1)
-        quant_h(H1_GROUP)
-
-        acc = [psum.tile([P, 512], F32, name="turn", bufs=TURN_BANKS) for m in range(4)]
-        for groups in (range(0, 3), range(3, 5)):
-            for a in range(2):
-                for group in groups:
-                    c = S1_CHUNKS + group
-                    for e in range(2):
-                        cols = slice(256 * e + P * a, 256 * e + P * (a + 1))
-                        nc.tensor.matmul_mx(
-                            out=acc[2 * a + e][:, :N],
-                            lhsT=w_codes[c][:, cols].bitcast(FP8X4),
-                            lhsT_scale=w_scales[c][:, cols],
-                            rhs=h_codes[group][:].bitcast(FP8X4),
-                            rhs_scale=h_scales[group][:],
-                            start=(group == 0),
-                            stop=(group == H1_GROUP),
-                        )
-
+        for group in (0, 1, 2, H1_GROUP):
+            project(group)
         result = [keep.tile([P, 4, 2, 64], F32, name="result%d" % a, align_bytes=64) for a in range(2)]
         out_view = out.rearrange("b (a p e) i j -> a p b (e i j)", a=2, e=2)
         for a in range(2):
+            project(3, (a,))
             even, odd = (acc[2 * a + e][:, :N].rearrange("p (b s) -> p b s", b=4) for e in range(2))
             nc.scalar.activation(
                 out=result[a][:, :, 0, :], in_=even, func=IDENTITY, bias=bias2[:, 2 * a : 2 * a + 1], scale=0.125

@@ -21,7 +21,7 @@ K1 = 512
 K2 = 2048
 PASSES = D // 512
 UNITS = 16
-HEAD = 4
+HEAD = 3
 PIECES = 8
 S1_CHUNKS = 8
 CHUNKS = 13
@@ -34,15 +34,15 @@ GRP_UNITS = 5
 CODE_UNITS = 4
 TURN_BANKS = 4
 
-V_EVERY = 4
-SORT_EVEN = 3
+V_WIDEN = 2
+SORT_EVEN = 2
 SORT_ODD = 3
 SORT_FROM = 4
 SORT_LATE = 15
 SORT_END = 2
 DOUBLE = 1
 H1_STEP = 13
-FIRST = 4
+FIRST = 3
 LAST = 15
 G_EARLY = 1
 CLAG = 0
@@ -58,7 +58,7 @@ S_GAP = 0
 S_STOP = 15
 V_LATE = 4
 V_END = 0
-V_END2 = 4
+V_END2 = 0
 S_END = 2
 
 FLOPS = 2 * N * D * (K1 + K2) + 2 * N * (K1 + K2) * O
@@ -150,7 +150,7 @@ def tile_skconv2d_pa_kernel(tc, xw_bytes, xw_scale, S1s, U1s, U2s, S2s, bias, ou
                 x_bf[a // 2] = pool.tile([P, 2048], BF16, name="w_grp", bufs=GRP_CHUNKS, align_bytes=64)
             wide = x_bf[a // 2][:, a % 2 * 1024 : (a % 2 + 1) * 1024]
             src = x_in[a].bitcast(FP8)
-            if a % V_EVERY == 0:
+            if a < V_WIDEN:
                 nc.vector.tensor_scalar(
                     out=wide.rearrange("p (s t m) -> p s m t", s=2, t=4),
                     in0=src.rearrange("p (s m t) -> p s m t", s=2, t=4),
@@ -166,7 +166,7 @@ def tile_skconv2d_pa_kernel(tc, xw_bytes, xw_scale, S1s, U1s, U2s, S2s, bias, ou
             for s in range(2):
                 xt = psum.tile([P, 4, P], F32, name="long" if s else "sums", bufs=2)
                 for t in range(4):
-                    if a % V_EVERY == 0:
+                    if a < V_WIDEN:
                         src = wide[:, (4 * s + t) * P : (4 * s + t + 1) * P]
                     else:
                         src = wide[:, 512 * s + t : 512 * (s + 1) : 4]
@@ -296,12 +296,12 @@ def tile_skconv2d_pa_kernel(tc, xw_bytes, xw_scale, S1s, U1s, U2s, S2s, bias, ou
                 stop=stop,
             )
 
-        def multiply_u2(i):
+        def multiply_u2(i, lo=0, hi=PASSES):
             group, t = divmod(i, 4)
-            if t % 2 == 0:
+            if t % 2 == 0 and lo == 0:
                 h_bank[group, t // 2] = psum.tile([P, 2, N], F32, name="sums", bufs=2)
             codes, scales = u2_codes[i]
-            for g in range(PASSES):
+            for g in range(lo, hi):
                 cols = slice(g * P, (g + 1) * P)
                 multiply(group, t, g, codes[:, cols], scales[:, cols], g == 0, g == PASSES - 1)
             if t % 2 == 1:
@@ -357,44 +357,43 @@ def tile_skconv2d_pa_kernel(tc, xw_bytes, xw_scale, S1s, U1s, U2s, S2s, bias, ou
         load_x(0, 1)
         nc.scalar.dma_start(out=x_scale[:], in_=xw_scale.rearrange("o (g p t) -> p (o g) t", p=P, t=4))
         load_x(1, 2)
-        load_u2(0, 0, 2)
         load_x(2, 4)
-        load_u2(0, 2, 4)
+        load_u2(0, 0, 2)
         load_x(4, 6)
-        load_u2(1, 0, 2)
+        load_u2(0, 2, 4)
         load_x(6, 8)
+        load_u2(1, 0, 2)
         load_u2(1, 2, 4)
         load_more()
 
-        for a in range(3):
+        for a in range(4):
             widen_x(a)
         turn_x(0)
-        for a in range(PIECES):
-            if a + 1 < PIECES:
-                turn_x(a + 1)
-            if a + 3 < PIECES:
-                widen_x(a + 3)
-            if a == PIECES - 1:
+        turn_x(1)
+        for n in range(2 * HEAD):
+            turn_x(n + 2)
+            if n + 4 < PIECES:
+                widen_x(n + 4)
+            if n == Q0:
+                quant_u2(0, 0, 4)
+            if n == 2 * HEAD - 1:
                 sort_u2(HEAD)
-            if a >= 4:
-                quant_x(a - 4)
-            if Q0 <= a < Q0 + 2:
-                quant_u2(0, 4 * (a - Q0), 4 * (a - Q0 + 1))
-            for b in range(2 * (a % 2), 2 * (a % 2) + 2):
-                turn_u2(a // 2, b)
-        multiply_u2(0)
-        quant_u2(1)
+            if n >= 3:
+                quant_x(n - 3)
+            for b in range(2 * (n % 2), 2 * (n % 2) + 2):
+                turn_u2(n // 2, b)
+        multiply_u2(0, 0, 4)
+        quant_x(3)
+        quant_u2(0, 4, 8)
 
-        quantised = 2
-        multiplied = 1
+        quantised = 1
         s1_done = 0
-        interleave(nc.scalar.copy, S_GAP, HEAD)
         for i in range(HEAD, UNITS):
             ready = min(len(chunks_quantised), S1_CHUNKS)
             empty_h()
             for b in range(4):
                 turn_u2(i, b)
-            if i - HEAD < DOUBLE:
+            if i == HEAD:
                 quant_u2(quantised)
                 quantised += 1
             interleave(nc.vector.tensor_copy, -len(quarters_done) % 4 or 4, i - 1)
@@ -406,9 +405,9 @@ def tile_skconv2d_pa_kernel(tc, xw_bytes, xw_scale, S1s, U1s, U2s, S2s, bias, ou
             if i + 1 < UNITS:
                 sort_u2(i + 1)
             interleave(nc.scalar.copy, 0 if i >= S_STOP else S_ODD if i % 2 else S_EVEN, i)
-            for n in range(2 if i - HEAD < DOUBLE else 1):
-                multiply_u2(multiplied)
-                multiplied += 1
+            if i == HEAD:
+                multiply_u2(0, 4, 8)
+            multiply_u2(i - 2)
             for g in range(s1_done, ready):
                 multiply_s1(g)
                 s1_done += 1

@@ -37,13 +37,16 @@ TURN_BANKS = 4
 V_WIDEN = 2
 SORT_EVEN = 2
 SORT_ODD = 3
-SORT_FROM = 4
+SORT_HEAD = 0
+SORT_HI = 4
 SORT_LATE = 15
 SORT_END = 2
 DOUBLE = 1
 H1_STEP = 13
 FIRST = 3
-LAST = 15
+TRAIL = 2
+H1_AT = 14
+V_BANK = 9
 G_EARLY = 1
 CLAG = 0
 Q0 = 2
@@ -57,9 +60,11 @@ S_EXTRA = 2
 S_GAP = 0
 S_STOP = 15
 V_LATE = 4
-V_END = 0
+V_END = 4
+V_PRE = 0
 V_END2 = 0
-S_END = 2
+V_END3 = 0
+S_END = 1
 
 FLOPS = 2 * N * D * (K1 + K2) + 2 * N * (K1 + K2) * O
 
@@ -118,7 +123,7 @@ def tile_skconv2d_pa_kernel(tc, xw_bytes, xw_scale, S1s, U1s, U2s, S2s, bias, ou
             w_raw[c] = raw
 
         order = list(range(S1_CHUNKS)) + [8, 9, 10, U1_CHUNK, 11]
-        behind = [min(FIRST + n, LAST) for n in range(CHUNKS)]
+        behind = [FIRST + n if n < CHUNKS - TRAIL else UNITS - 1 for n in range(CHUNKS)]
         queue = []
         for i in range(2, UNITS):
             queue.append(("unit", i))
@@ -193,10 +198,14 @@ def tile_skconv2d_pa_kernel(tc, xw_bytes, xw_scale, S1s, U1s, U2s, S2s, bias, ou
         u2_codes = {}
 
         def sorted_banks(i):
-            if i < SORT_FROM:
+            if i < HEAD:
                 return 0
-            if i >= SORT_LATE:
+            if i == HEAD:
+                return SORT_HEAD
+            if i == UNITS - 1:
                 return SORT_END
+            if i >= SORT_LATE:
+                return SORT_HI
             return SORT_ODD if i % 2 else SORT_EVEN
 
         def sort_u2(i):
@@ -226,9 +235,8 @@ def tile_skconv2d_pa_kernel(tc, xw_bytes, xw_scale, S1s, U1s, U2s, S2s, bias, ou
                         src = words[:, 256 * c + u : 256 * (c + 1) : 2]
                     nc.tensor.transpose(ut[:, s, u, :], src, ident[:])
             dst = u2_grp[i][:, 1024 * b : 1024 * (b + 1)].bitcast(F32)
-            nc.scalar.copy(
-                out=dst.rearrange("p (s n u) -> p s n u", s=2, u=2), in_=ut[:].rearrange("p s u n -> p s n u")
-            )
+            copy = nc.vector.tensor_copy if i == UNITS - 1 and b == V_BANK else nc.scalar.copy
+            copy(out=dst.rearrange("p (s n u) -> p s n u", s=2, u=2), in_=ut[:].rearrange("p s u n -> p s n u"))
             if b == 3:
                 units_turned.append(i)
                 load_more()
@@ -359,11 +367,9 @@ def tile_skconv2d_pa_kernel(tc, xw_bytes, xw_scale, S1s, U1s, U2s, S2s, bias, ou
         load_x(1, 2)
         load_x(2, 4)
         load_u2(0, 0, 2)
-        load_x(4, 6)
+        load_x(4, 8)
         load_u2(0, 2, 4)
-        load_x(6, 8)
-        load_u2(1, 0, 2)
-        load_u2(1, 2, 4)
+        load_u2(1)
         load_more()
 
         for a in range(4):
@@ -390,7 +396,13 @@ def tile_skconv2d_pa_kernel(tc, xw_bytes, xw_scale, S1s, U1s, U2s, S2s, bias, ou
         s1_done = 0
         for i in range(HEAD, UNITS):
             ready = min(len(chunks_quantised), S1_CHUNKS)
-            empty_h()
+            last = i == UNITS - 1
+            if not last:
+                empty_h()
+            if last:
+                quant_u2(quantised)
+                quantised += 1
+                interleave(nc.vector.tensor_copy, V_PRE)
             for b in range(4):
                 turn_u2(i, b)
             if i == HEAD:
@@ -402,12 +414,20 @@ def tile_skconv2d_pa_kernel(tc, xw_bytes, xw_scale, S1s, U1s, U2s, S2s, bias, ou
                 quantised += 1
             quant_chunks()
             quant_h()
-            if i + 1 < UNITS:
+            if not last:
                 sort_u2(i + 1)
-            interleave(nc.scalar.copy, 0 if i >= S_STOP else S_ODD if i % 2 else S_EVEN, i)
+            if H1_AT <= i < H1_AT + 2 or last:
+                if i < H1_AT + 2:
+                    closed.append((H1_GROUP, i - H1_AT))
+                empty_h()
+            elif i < S_STOP:
+                interleave(nc.scalar.copy, S_ODD if i % 2 else S_EVEN, i)
             if i == HEAD:
                 multiply_u2(0, 4, 8)
-            multiply_u2(i - 2)
+            if not last:
+                multiply_u2(i - 2)
+            if i >= UNITS - 2:
+                multiply_u2(i - 1)
             for g in range(s1_done, ready):
                 multiply_s1(g)
                 s1_done += 1
@@ -418,13 +438,14 @@ def tile_skconv2d_pa_kernel(tc, xw_bytes, xw_scale, S1s, U1s, U2s, S2s, bias, ou
         quant_u2(UNITS - 1, 0, 4)
         interleave(nc.vector.tensor_copy, V_END2)
         quant_u2(UNITS - 1, 4, 8)
-        closed[:] = [(H1_GROUP, 0), (3, 0), (H1_GROUP, 1)]
-        empty_h()
-        multiply_u2(UNITS - 2)
-        multiply_u2(UNITS - 1)
-        interleave(nc.vector.tensor_copy, 4 * CHUNKS)
         quant_chunks()
+        interleave(nc.scalar.copy, S_END)
+        multiply_u2(UNITS - 1)
+        interleave(nc.vector.tensor_copy, V_END3)
+        quant_chunks()
+        interleave(nc.vector.tensor_copy, 4 * CHUNKS)
         quant_h()
+        quant_chunks()
         empty_h()
         quant_h()
         bias2 = const.tile([P, 4], F32, name="bias2", align_bytes=64)

@@ -35,9 +35,13 @@ CODE_UNITS = 4
 TURN_BANKS = 4
 
 V_WIDEN = 2
+WARM = 0
+S_FIRST = 2
+S_SORT = 1
+Q14 = 1
 SORT_EVEN = 2
 SORT_ODD = 3
-SORT_HEAD = 0
+SORT_HEAD = 1
 SORT_HI = 4
 SORT_LATE = 15
 SORT_END = 2
@@ -45,11 +49,20 @@ DOUBLE = 1
 H1_STEP = 13
 FIRST = 3
 TRAIL = 2
+RING2 = 0
+AHEAD = 1
+RP = 0
+LEAD = 2
+LO = 0
+TRAIL2 = 2
+B10 = 0
+B9 = 0
 H1_AT = 14
 V_BANK = 9
 G_EARLY = 1
 CLAG = 0
-Q0 = 2
+Q0 = 1
+NH = 2
 Q1 = 5
 S2_EARLY = 2
 V_EVEN = 3
@@ -82,8 +95,8 @@ def tile_skconv2d_pa_kernel(tc, xw_bytes, xw_scale, S1s, U1s, U2s, S2s, bias, ou
         u2_rows = U2s.rearrange("t r d -> (t r) d").rearrange("(g p t) d -> g p t d", p=P, t=4)
         s1_rows = S1s.rearrange("t (g p j) r -> g p t (j r)", p=P, j=4)
         s2_rows = S2s.rearrange("t r o -> (t r) o").rearrange("(g p j) o -> g p (j o)", p=P, j=4)
-        u1_rows = U1s.rearrange("t r o -> (t r) o").rearrange("(a q i) o -> i a q o", q=4, i=4)
-        x_rows = xw_bytes.rearrange("(h p) d -> h p d", p=P)
+        u1_rows = U1s.rearrange("t r o -> (t r) o").rearrange("(a q i) o -> q a i o", q=4, i=4)
+        x_rows = xw_bytes.rearrange("(h p) d -> p h d", p=P)
 
         ident_bf = const.tile([P, P], BF16, name="ident_bf", align_bytes=64)
         make_identity(nc, ident_bf[:])
@@ -91,6 +104,12 @@ def tile_skconv2d_pa_kernel(tc, xw_bytes, xw_scale, S1s, U1s, U2s, S2s, bias, ou
         make_identity(nc, ident[:])
         ones = const.tile([P, 1], F32, name="ones", align_bytes=64)
         nc.vector.memset(ones[:], 1.0)
+        if WARM:
+            zeros = const.tile([P, 512], BF16, name="zeros", align_bytes=64)
+            nc.vector.memset(zeros[:], 0.0)
+            warm = psum.tile([P, 512], F32, name="long", bufs=2)
+            for n in range(WARM):
+                nc.tensor.matmul(warm[:], zeros[:, :P], zeros[:], start=True, stop=True)
         x_scale = const.tile([P, PASSES, 4], F32, name="x_scale", align_bytes=64)
         bias_in = const.tile([P, 4], BF16, name="bias_in", align_bytes=64)
 
@@ -99,11 +118,16 @@ def tile_skconv2d_pa_kernel(tc, xw_bytes, xw_scale, S1s, U1s, U2s, S2s, bias, ou
         w_raw = {}
 
         def load_x(lo, hi):
+            hs = slice(lo % 2, lo % 2 + 1) if hi - lo == 1 else slice(0, 2)
+            nb = max(1, (hi - lo) // 2)
             t = keep.tile([P, (hi - lo) * 1024], U8, name="x_in%d" % lo, align_bytes=64)
-            c = lo % 4 * 1024
-            nc.sync.dma_start(out=t[:], in_=x_rows[lo // 4][:, c : c + (hi - lo) * 1024])
+            c = lo // 2 * 1024
+            nc.sync.dma_start(
+                out=t[:].rearrange("p (h d) -> p h d", d=nb * 1024), in_=x_rows[:, hs, c : c + nb * 1024]
+            )
             for a in range(lo, hi):
-                x_in[a] = t[:, (a - lo) * 1024 : (a - lo + 1) * 1024]
+                at = (a - lo) % 2 * nb * 1024 + (a - lo) // 2 * 1024
+                x_in[a] = t[:, at : at + 1024]
 
         def load_u2(i, lo=0, hi=4):
             if lo == 0:
@@ -114,20 +138,26 @@ def tile_skconv2d_pa_kernel(tc, xw_bytes, xw_scale, S1s, U1s, U2s, S2s, bias, ou
         def load_w(c):
             raw = pool.tile([P, 2048], BF16, name="w_raw", bufs=RAW_CHUNKS, align_bytes=64)
             if c < S1_CHUNKS:
-                nc.sync.dma_start(out=raw[:].rearrange("p (t x) -> p t x", t=8), in_=s1_rows[c])
+                eng = nc.scalar if RING2 else nc.sync
+                eng.dma_start(out=raw[:].rearrange("p (t x) -> p t x", t=8), in_=s1_rows[c])
             elif c < U1_CHUNK:
                 nc.sync.dma_start(out=raw[:], in_=s2_rows[c - S1_CHUNKS])
             else:
-                for i in range(4):
-                    nc.sync.dma_start(out=raw[i:P:4, :].rearrange("p (q o) -> p q o", q=4), in_=u1_rows[i])
+                for q in range(4):
+                    nc.sync.dma_start(out=raw[:, q * O : (q + 1) * O], in_=u1_rows[q])
             w_raw[c] = raw
 
         order = list(range(S1_CHUNKS)) + [8, 9, 10, U1_CHUNK, 11]
         behind = [FIRST + n if n < CHUNKS - TRAIL else UNITS - 1 for n in range(CHUNKS)]
+        taken = [FIRST + n if n < CHUNKS - TRAIL2 else UNITS - 1 for n in range(CHUNKS)]
+        if B10:
+            behind[10] = B10
+        if B9:
+            behind[9] = B9
         queue = []
         for i in range(2, UNITS):
             queue.append(("unit", i))
-            queue.extend(("chunk", n) for n in range(CHUNKS) if behind[n] == i)
+            queue.extend(("chunk", n) for n in range(S1_CHUNKS if RING2 else 0, CHUNKS) if behind[n] == i)
         units_turned = []
         quarters_done = []
         chunks_quantised = []
@@ -138,7 +168,7 @@ def tile_skconv2d_pa_kernel(tc, xw_bytes, xw_scale, S1s, U1s, U2s, S2s, bias, ou
                 kind, n = queue[0]
                 if kind == "unit" and n < len(units_turned) + RAW_UNITS:
                     load_u2(n)
-                elif kind == "chunk" and n + 4 < len(x_quantised) + len(quarters_done) // 4 + RAW_CHUNKS:
+                elif kind == "chunk" and n == len(w_raw) and n + 4 < len(x_quantised) + len(quarters_done) // 4 + RAW_CHUNKS:
                     load_w(order[n])
                 else:
                     return
@@ -177,7 +207,7 @@ def tile_skconv2d_pa_kernel(tc, xw_bytes, xw_scale, S1s, U1s, U2s, S2s, bias, ou
                         src = wide[:, 512 * s + t : 512 * (s + 1) : 4]
                     nc.tensor.matmul(xt[:, t, :], src, ident_bf[:], start=True, stop=True)
                 x_bank[a, s] = xt
-                h, b = divmod(a, 4)
+                b, h = divmod(a, 2)
                 g = 2 * b + s
                 c = s * 1024 + h * 512
                 nc.vector.tensor_tensor(
@@ -213,7 +243,8 @@ def tile_skconv2d_pa_kernel(tc, xw_bytes, xw_scale, S1s, U1s, U2s, S2s, bias, ou
             if k:
                 srt = pool.tile([P, 512 * k], F32, name="u2_sorted", bufs=2, align_bytes=64)
                 words = u2_raw[i][:].bitcast(F32)[:, (4 - k) * 512 :]
-                nc.vector.tensor_copy(
+                copy = nc.scalar.copy if i == HEAD and S_SORT else nc.vector.tensor_copy
+                copy(
                     out=srt[:].rearrange("p (c u w) -> p c w u", u=2, w=P),
                     in_=words.rearrange("p (c w u) -> p c w u", w=P, u=2),
                 )
@@ -270,7 +301,7 @@ def tile_skconv2d_pa_kernel(tc, xw_bytes, xw_scale, S1s, U1s, U2s, S2s, bias, ou
                 copy(out=dst[:, 32 * lo : 32 * hi], in_=src[:, 32 * lo : 32 * hi])
 
         def interleave(copy, n, step=2 * UNITS):
-            landed = sum(1 for u in behind if u + CLAG <= step)
+            landed = sum(1 for u in taken if u + CLAG <= step)
             n = max(0, min(n, 4 * landed - len(quarters_done)))
             while n:
                 c, lo = divmod(len(quarters_done), 4)
@@ -366,37 +397,61 @@ def tile_skconv2d_pa_kernel(tc, xw_bytes, xw_scale, S1s, U1s, U2s, S2s, bias, ou
         nc.scalar.dma_start(out=x_scale[:], in_=xw_scale.rearrange("o (g p t) -> p (o g) t", p=P, t=4))
         load_x(1, 2)
         load_x(2, 4)
-        load_u2(0, 0, 2)
-        load_x(4, 8)
-        load_u2(0, 2, 4)
+        if LO == 0:
+            load_u2(0, 0, 2)
+            load_x(4, 8)
+            load_u2(0, 2, 4)
+        elif LO == 1:
+            load_x(4, 8)
+            load_u2(0, 0, 2)
+            load_u2(0, 2, 4)
+        elif LO == 2:
+            load_x(4, 6)
+            load_u2(0, 0, 2)
+            load_x(6, 8)
+            load_u2(0, 2, 4)
         load_u2(1)
         load_more()
 
-        for a in range(4):
+        for a in range(LEAD + 2):
             widen_x(a)
-        turn_x(0)
-        turn_x(1)
+        for a in range(LEAD):
+            turn_x(a)
+        halves = 0
         for n in range(2 * HEAD):
-            turn_x(n + 2)
-            if n + 4 < PIECES:
-                widen_x(n + 4)
-            if n == Q0:
-                quant_u2(0, 0, 4)
-            if n == 2 * HEAD - 1:
+            if n + LEAD < PIECES:
+                turn_x(n + LEAD)
+            if n + LEAD + 2 < PIECES:
+                widen_x(n + LEAD + 2)
+            if n == 2 * HEAD - 1 and not S_SORT:
                 sort_u2(HEAD)
-            if n >= 3:
-                quant_x(n - 3)
+            if (n + LEAD) % 2 == 0 and len(x_quantised) < 4:
+                quant_x(len(x_quantised))
+            elif n >= Q0 and halves < NH:
+                quant_u2(halves // 2, 4 * (halves % 2), 4 * (halves % 2) + 4)
+                halves += 1
+            if RING2 and n % 2 == RP and n // 2 + AHEAD >= FIRST:
+                load_w(n // 2 + AHEAD - FIRST)
             for b in range(2 * (n % 2), 2 * (n % 2) + 2):
                 turn_u2(n // 2, b)
+        if S_SORT:
+            sort_u2(HEAD)
         multiply_u2(0, 0, 4)
-        quant_x(3)
-        quant_u2(0, 4, 8)
+        if halves < 2:
+            quant_u2(0, 4, 8)
+        elif halves == 2:
+            quant_u2(1, 0, 4)
+        if len(x_quantised) < 4:
+            quant_x(3)
 
         quantised = 1
         s1_done = 0
         for i in range(HEAD, UNITS):
             ready = min(len(chunks_quantised), S1_CHUNKS)
             last = i == UNITS - 1
+            if RING2 and i + AHEAD - FIRST < S1_CHUNKS:
+                load_w(i + AHEAD - FIRST)
+                load_more()
             if not last:
                 empty_h()
             if last:
@@ -405,8 +460,8 @@ def tile_skconv2d_pa_kernel(tc, xw_bytes, xw_scale, S1s, U1s, U2s, S2s, bias, ou
                 interleave(nc.vector.tensor_copy, V_PRE)
             for b in range(4):
                 turn_u2(i, b)
-            if i == HEAD:
-                quant_u2(quantised)
+            if i == HEAD or (i == UNITS - 2 and Q14):
+                quant_u2(quantised, 4 if i == HEAD and halves == 2 else 0, 8)
                 quantised += 1
             interleave(nc.vector.tensor_copy, -len(quarters_done) % 4 or 4, i - 1)
             if quantised < i:
@@ -421,7 +476,7 @@ def tile_skconv2d_pa_kernel(tc, xw_bytes, xw_scale, S1s, U1s, U2s, S2s, bias, ou
                     closed.append((H1_GROUP, i - H1_AT))
                 empty_h()
             elif i < S_STOP:
-                interleave(nc.scalar.copy, S_ODD if i % 2 else S_EVEN, i)
+                interleave(nc.scalar.copy, S_FIRST if i == HEAD else S_ODD if i % 2 else S_EVEN, i)
             if i == HEAD:
                 multiply_u2(0, 4, 8)
             if not last:

@@ -74,6 +74,12 @@ S_GAP = 0
 S_STOP = 15
 V_LATE = 4
 V_END = 4
+SPLIT = 1
+S12 = 1
+X_SPLIT = 0
+S14 = 0
+BIAS_AT = 9
+S13 = 1
 V_PRE = 0
 V_END2 = 0
 V_END3 = 0
@@ -112,6 +118,7 @@ def tile_skconv2d_pa_kernel(tc, xw_bytes, xw_scale, S1s, U1s, U2s, S2s, bias, ou
                 nc.tensor.matmul(warm[:], zeros[:, :P], zeros[:], start=True, stop=True)
         x_scale = const.tile([P, PASSES, 4], F32, name="x_scale", align_bytes=64)
         bias_in = const.tile([P, 4], BF16, name="bias_in", align_bytes=64)
+        bias2 = const.tile([P, 4], F32, name="bias2", align_bytes=64)
 
         u2_raw = {}
         x_in = {}
@@ -198,22 +205,23 @@ def tile_skconv2d_pa_kernel(tc, xw_bytes, xw_scale, S1s, U1s, U2s, S2s, bias, ou
 
         def turn_x(a):
             wide = x_bf[a // 2][:, a % 2 * 1024 : (a % 2 + 1) * 1024]
+            xt = psum.tile([P, 2, 4, P], BF16, name="long" if a % 2 else "sums", bufs=2)
             for s in range(2):
-                xt = psum.tile([P, 4, P], F32, name="long" if s else "sums", bufs=2)
                 for t in range(4):
                     if a < V_WIDEN:
                         src = wide[:, (4 * s + t) * P : (4 * s + t + 1) * P]
                     else:
                         src = wide[:, 512 * s + t : 512 * (s + 1) : 4]
-                    nc.tensor.matmul(xt[:, t, :], src, ident_bf[:], start=True, stop=True)
-                x_bank[a, s] = xt
-                b, h = divmod(a, 2)
-                g = 2 * b + s
-                c = s * 1024 + h * 512
+                    nc.tensor.matmul(xt[:, s, t, :], src, ident_bf[:], start=True, stop=True)
+            b, h = divmod(a, 2)
+            dst = x_grp[b][:].rearrange("p (s h n t) -> p h s n t", s=2, h=2, t=4)[:, h]
+            scale = x_scale[:, 2 * b : 2 * b + 2, :].rearrange("p s (o t) -> p s o t", o=1)
+            parts = [slice(0, 1), slice(1, 2)] if a < X_SPLIT else [slice(0, 2)]
+            for part in parts:
                 nc.vector.tensor_tensor(
-                    out=x_grp[b][:, c : c + 512].rearrange("p (n t) -> p n t", t=4),
-                    in0=xt[:].rearrange("p t n -> p n t"),
-                    in1=x_scale[:, g : g + 1, :].to_broadcast([P, P, 4]),
+                    out=dst[:, part],
+                    in0=xt[:].rearrange("p s t n -> p s n t")[:, part],
+                    in1=scale[:, part].to_broadcast([P, part.stop - part.start, P, 4]),
                     op=MULT,
                 )
 
@@ -449,34 +457,43 @@ def tile_skconv2d_pa_kernel(tc, xw_bytes, xw_scale, S1s, U1s, U2s, S2s, bias, ou
         for i in range(HEAD, UNITS):
             ready = min(len(chunks_quantised), S1_CHUNKS)
             last = i == UNITS - 1
+            if i == BIAS_AT:
+                nc.sync.dma_start(
+                    out=bias_in[:].rearrange("p (a e) -> p a e", a=2),
+                    in_=bias.rearrange("(a p e) -> p a e", a=2, e=2),
+                )
             if RING2 and i + AHEAD - FIRST < S1_CHUNKS:
                 load_w(i + AHEAD - FIRST)
                 load_more()
             if not last:
                 empty_h()
-            if last:
-                quant_u2(quantised)
-                quantised += 1
-                interleave(nc.vector.tensor_copy, V_PRE)
             for b in range(4):
                 turn_u2(i, b)
-            if i == HEAD or (i == UNITS - 2 and Q14):
-                quant_u2(quantised, 4 if i == HEAD and halves == 2 else 0, 8)
-                quantised += 1
-            interleave(nc.vector.tensor_copy, -len(quarters_done) % 4 or 4, i - 1)
-            if quantised < i:
-                quant_u2(quantised)
-                quantised += 1
-            quant_chunks()
-            quant_h()
+            if i == HEAD:
+                quant_u2(1, 4, 8)
+            if i == UNITS - 2:
+                quant_u2(i - 1)
             if not last:
+                interleave(nc.vector.tensor_copy, -len(quarters_done) % 4 or 4, i - 1)
+            if i < UNITS - 2:
+                quant_u2(i - 1)
+                quant_chunks()
+                quant_h()
                 sort_u2(i + 1)
+            elif not last:
+                sort_u2(i + 1)
+                quant_h()
+                quant_chunks()
+                quant_u2(i)
             if H1_AT <= i < H1_AT + 2 or last:
                 if i < H1_AT + 2:
                     closed.append((H1_GROUP, i - H1_AT))
                 empty_h()
+                if i == UNITS - 2:
+                    nc.scalar.activation(out=bias2[:], in_=bias_in[:], func=IDENTITY, scale=2.0)
+                    interleave(nc.scalar.copy, S14)
             elif i < S_STOP:
-                interleave(nc.scalar.copy, S_FIRST if i == HEAD else S_ODD if i % 2 else S_EVEN, i)
+                interleave(nc.scalar.copy, S_FIRST if i == HEAD else S12 if i == 12 else S13 if i == 13 else S_ODD if i % 2 else S_EVEN, i)
             if i == HEAD:
                 multiply_u2(0, 4, 8)
             if not last:
@@ -486,25 +503,23 @@ def tile_skconv2d_pa_kernel(tc, xw_bytes, xw_scale, S1s, U1s, U2s, S2s, bias, ou
             for g in range(s1_done, ready):
                 multiply_s1(g)
                 s1_done += 1
-        nc.sync.dma_start(
-            out=bias_in[:].rearrange("p (a e) -> p a e", a=2), in_=bias.rearrange("(a p e) -> p a e", a=2, e=2)
-        )
         interleave(nc.vector.tensor_copy, V_END)
         quant_u2(UNITS - 1, 0, 4)
         interleave(nc.vector.tensor_copy, V_END2)
-        quant_u2(UNITS - 1, 4, 8)
+        if SPLIT:
+            quant_u2(UNITS - 1, 4, 6)
+            quant_u2(UNITS - 1, 6, 8)
+        else:
+            quant_u2(UNITS - 1, 4, 8)
+        interleave(nc.vector.tensor_copy, -len(quarters_done) % 4)
         quant_chunks()
         interleave(nc.scalar.copy, S_END)
         multiply_u2(UNITS - 1)
-        interleave(nc.vector.tensor_copy, V_END3)
-        quant_chunks()
         interleave(nc.vector.tensor_copy, 4 * CHUNKS)
         quant_h()
         quant_chunks()
         empty_h()
         quant_h()
-        bias2 = const.tile([P, 4], F32, name="bias2", align_bytes=64)
-        nc.vector.tensor_scalar(out=bias2[:], in0=bias_in[:], scalar1=2.0, scalar2=None, op0=MULT)
         for group in (0, 1, 2, H1_GROUP):
             project(group)
         result = [keep.tile([P, 4, 2, 64], F32, name="result%d" % a, align_bytes=64) for a in range(2)]

@@ -20,70 +20,24 @@ O = 512
 K1 = 512
 K2 = 2048
 PASSES = D // 512
-UNITS = 16
-HEAD = 3
+UNITS = K2 // P
+LAST = UNITS - 1
 PIECES = 8
-S1_CHUNKS = 8
+S1_CHUNKS = PASSES
+U1_CHUNK = 12
 CHUNKS = 13
 H1_GROUP = 4
-U1_CHUNK = 12
+
+HEAD = 3
+VECTOR_PIECES = 2
+TRAILING_CHUNKS = 2
 RAW_UNITS = 7
 RAW_CHUNKS = 6
 GRP_CHUNKS = 4
 GRP_UNITS = 5
 CODE_UNITS = 4
 TURN_BANKS = 4
-
-V_WIDEN = 2
-WARM = 0
-S_FIRST = 2
-S_SORT = 1
-Q14 = 1
-SORT_EVEN = 2
-SORT_ODD = 3
-SORT_HEAD = 1
-SORT_HI = 4
-SORT_LATE = 15
-SORT_END = 2
-DOUBLE = 1
-H1_STEP = 13
-FIRST = 3
-TRAIL = 2
-RING2 = 0
-AHEAD = 1
-RP = 0
-LEAD = 2
-LO = 0
-TRAIL2 = 2
-B10 = 0
-B9 = 0
-H1_AT = 14
-V_BANK = 9
-G_EARLY = 1
-CLAG = 0
-Q0 = 1
-NH = 2
-Q1 = 5
-S2_EARLY = 2
-V_EVEN = 3
-V_ODD = 3
-S_EVEN = 1
-S_ODD = 1
-S_EXTRA = 2
-S_GAP = 0
-S_STOP = 15
-V_LATE = 4
-V_END = 4
-SPLIT = 1
-S12 = 1
-X_SPLIT = 0
-S14 = 0
-BIAS_AT = 9
-S13 = 1
-V_PRE = 0
-V_END2 = 0
-V_END3 = 0
-S_END = 1
+BIAS_STEP = 9
 
 FLOPS = 2 * N * D * (K1 + K2) + 2 * N * (K1 + K2) * O
 
@@ -110,12 +64,6 @@ def tile_skconv2d_pa_kernel(tc, xw_bytes, xw_scale, S1s, U1s, U2s, S2s, bias, ou
         make_identity(nc, ident[:])
         ones = const.tile([P, 1], F32, name="ones", align_bytes=64)
         nc.vector.memset(ones[:], 1.0)
-        if WARM:
-            zeros = const.tile([P, 512], BF16, name="zeros", align_bytes=64)
-            nc.vector.memset(zeros[:], 0.0)
-            warm = psum.tile([P, 512], F32, name="long", bufs=2)
-            for n in range(WARM):
-                nc.tensor.matmul(warm[:], zeros[:, :P], zeros[:], start=True, stop=True)
         x_scale = const.tile([P, PASSES, 4], F32, name="x_scale", align_bytes=64)
         bias_in = const.tile([P, 4], BF16, name="bias_in", align_bytes=64)
         bias2 = const.tile([P, 4], F32, name="bias2", align_bytes=64)
@@ -125,28 +73,24 @@ def tile_skconv2d_pa_kernel(tc, xw_bytes, xw_scale, S1s, U1s, U2s, S2s, bias, ou
         w_raw = {}
 
         def load_x(lo, hi):
-            hs = slice(lo % 2, lo % 2 + 1) if hi - lo == 1 else slice(0, 2)
-            nb = max(1, (hi - lo) // 2)
+            halves = slice(lo % 2, lo % 2 + 1) if hi - lo == 1 else slice(0, 2)
+            width = max(1, (hi - lo) // 2) * 1024
             t = keep.tile([P, (hi - lo) * 1024], U8, name="x_in%d" % lo, align_bytes=64)
             c = lo // 2 * 1024
-            nc.sync.dma_start(
-                out=t[:].rearrange("p (h d) -> p h d", d=nb * 1024), in_=x_rows[:, hs, c : c + nb * 1024]
-            )
+            nc.sync.dma_start(out=t[:].rearrange("p (h d) -> p h d", d=width), in_=x_rows[:, halves, c : c + width])
             for a in range(lo, hi):
-                at = (a - lo) % 2 * nb * 1024 + (a - lo) // 2 * 1024
+                at = (a - lo) % 2 * width + (a - lo) // 2 * 1024
                 x_in[a] = t[:, at : at + 1024]
 
-        def load_u2(i, lo=0, hi=4):
+        def load_u2(i, lo=0, hi=D):
             if lo == 0:
                 u2_raw[i] = pool.tile([P, D], BF16, name="u2_raw", bufs=RAW_UNITS, align_bytes=64)
-            cols = slice(lo * 1024, hi * 1024)
-            nc.sync.dma_start(out=u2_raw[i][:, cols], in_=u2_rows[i // 4][:, i % 4, cols])
+            nc.sync.dma_start(out=u2_raw[i][:, lo:hi], in_=u2_rows[i // 4][:, i % 4, lo:hi])
 
         def load_w(c):
             raw = pool.tile([P, 2048], BF16, name="w_raw", bufs=RAW_CHUNKS, align_bytes=64)
             if c < S1_CHUNKS:
-                eng = nc.scalar if RING2 else nc.sync
-                eng.dma_start(out=raw[:].rearrange("p (t x) -> p t x", t=8), in_=s1_rows[c])
+                nc.sync.dma_start(out=raw[:].rearrange("p (t x) -> p t x", t=8), in_=s1_rows[c])
             elif c < U1_CHUNK:
                 nc.sync.dma_start(out=raw[:], in_=s2_rows[c - S1_CHUNKS])
             else:
@@ -154,17 +98,12 @@ def tile_skconv2d_pa_kernel(tc, xw_bytes, xw_scale, S1s, U1s, U2s, S2s, bias, ou
                     nc.sync.dma_start(out=raw[:, q * O : (q + 1) * O], in_=u1_rows[q])
             w_raw[c] = raw
 
-        order = list(range(S1_CHUNKS)) + [8, 9, 10, U1_CHUNK, 11]
-        behind = [FIRST + n if n < CHUNKS - TRAIL else UNITS - 1 for n in range(CHUNKS)]
-        taken = [FIRST + n if n < CHUNKS - TRAIL2 else UNITS - 1 for n in range(CHUNKS)]
-        if B10:
-            behind[10] = B10
-        if B9:
-            behind[9] = B9
+        order = list(range(U1_CHUNK - 1)) + [U1_CHUNK, U1_CHUNK - 1]
+        behind = [HEAD + n if n < CHUNKS - TRAILING_CHUNKS else LAST for n in range(CHUNKS)]
         queue = []
         for i in range(2, UNITS):
             queue.append(("unit", i))
-            queue.extend(("chunk", n) for n in range(S1_CHUNKS if RING2 else 0, CHUNKS) if behind[n] == i)
+            queue.extend(("chunk", n) for n in range(CHUNKS) if behind[n] == i)
         units_turned = []
         quarters_done = []
         chunks_quantised = []
@@ -175,7 +114,7 @@ def tile_skconv2d_pa_kernel(tc, xw_bytes, xw_scale, S1s, U1s, U2s, S2s, bias, ou
                 kind, n = queue[0]
                 if kind == "unit" and n < len(units_turned) + RAW_UNITS:
                     load_u2(n)
-                elif kind == "chunk" and n == len(w_raw) and n + 4 < len(x_quantised) + len(quarters_done) // 4 + RAW_CHUNKS:
+                elif kind == "chunk" and n + 4 < len(x_quantised) + len(quarters_done) // 4 + RAW_CHUNKS:
                     load_w(order[n])
                 else:
                     return
@@ -184,7 +123,6 @@ def tile_skconv2d_pa_kernel(tc, xw_bytes, xw_scale, S1s, U1s, U2s, S2s, bias, ou
         x_codes = keep.tile([P, PASSES * N], U32, name="x_codes", align_bytes=64)
         x_scales = keep.tile([P, PASSES * N], U8, name="x_scales", align_bytes=64)
         x_bf = {}
-        x_bank = {}
         x_grp = [pool.tile([P, 2048], BF16, name="w_raw", bufs=RAW_CHUNKS, align_bytes=64) for b in range(4)]
 
         def widen_x(a):
@@ -192,7 +130,7 @@ def tile_skconv2d_pa_kernel(tc, xw_bytes, xw_scale, S1s, U1s, U2s, S2s, bias, ou
                 x_bf[a // 2] = pool.tile([P, 2048], BF16, name="w_grp", bufs=GRP_CHUNKS, align_bytes=64)
             wide = x_bf[a // 2][:, a % 2 * 1024 : (a % 2 + 1) * 1024]
             src = x_in[a].bitcast(FP8)
-            if a < V_WIDEN:
+            if a < VECTOR_PIECES:
                 nc.vector.tensor_scalar(
                     out=wide.rearrange("p (s t m) -> p s m t", s=2, t=4),
                     in0=src.rearrange("p (s m t) -> p s m t", s=2, t=4),
@@ -208,22 +146,19 @@ def tile_skconv2d_pa_kernel(tc, xw_bytes, xw_scale, S1s, U1s, U2s, S2s, bias, ou
             xt = psum.tile([P, 2, 4, P], BF16, name="long" if a % 2 else "sums", bufs=2)
             for s in range(2):
                 for t in range(4):
-                    if a < V_WIDEN:
+                    if a < VECTOR_PIECES:
                         src = wide[:, (4 * s + t) * P : (4 * s + t + 1) * P]
                     else:
                         src = wide[:, 512 * s + t : 512 * (s + 1) : 4]
                     nc.tensor.matmul(xt[:, s, t, :], src, ident_bf[:], start=True, stop=True)
             b, h = divmod(a, 2)
-            dst = x_grp[b][:].rearrange("p (s h n t) -> p h s n t", s=2, h=2, t=4)[:, h]
             scale = x_scale[:, 2 * b : 2 * b + 2, :].rearrange("p s (o t) -> p s o t", o=1)
-            parts = [slice(0, 1), slice(1, 2)] if a < X_SPLIT else [slice(0, 2)]
-            for part in parts:
-                nc.vector.tensor_tensor(
-                    out=dst[:, part],
-                    in0=xt[:].rearrange("p s t n -> p s n t")[:, part],
-                    in1=scale[:, part].to_broadcast([P, part.stop - part.start, P, 4]),
-                    op=MULT,
-                )
+            nc.vector.tensor_tensor(
+                out=x_grp[b][:].rearrange("p (s h n t) -> p h s n t", s=2, h=2, t=4)[:, h],
+                in0=xt[:].rearrange("p s t n -> p s n t"),
+                in1=scale.to_broadcast([P, 2, P, 4]),
+                op=MULT,
+            )
 
         def quant_x(b):
             cols = slice(2 * b * N, (2 * b + 2) * N)
@@ -239,24 +174,20 @@ def tile_skconv2d_pa_kernel(tc, xw_bytes, xw_scale, S1s, U1s, U2s, S2s, bias, ou
             if i < HEAD:
                 return 0
             if i == HEAD:
-                return SORT_HEAD
-            if i == UNITS - 1:
-                return SORT_END
-            if i >= SORT_LATE:
-                return SORT_HI
-            return SORT_ODD if i % 2 else SORT_EVEN
+                return 1
+            if i == LAST:
+                return 1
+            return 3 if i % 2 else 2
 
-        def sort_u2(i):
+        def sort_u2(i, copy):
             k = sorted_banks(i)
-            if k:
-                srt = pool.tile([P, 512 * k], F32, name="u2_sorted", bufs=2, align_bytes=64)
-                words = u2_raw[i][:].bitcast(F32)[:, (4 - k) * 512 :]
-                copy = nc.scalar.copy if i == HEAD and S_SORT else nc.vector.tensor_copy
-                copy(
-                    out=srt[:].rearrange("p (c u w) -> p c w u", u=2, w=P),
-                    in_=words.rearrange("p (c w u) -> p c w u", w=P, u=2),
-                )
-                u2_sorted[i] = srt
+            srt = pool.tile([P, 512 * k], F32, name="u2_sorted", bufs=2, align_bytes=64)
+            words = u2_raw[i][:].bitcast(F32)[:, (4 - k) * 512 :]
+            copy(
+                out=srt[:].rearrange("p (c u w) -> p c w u", u=2, w=P),
+                in_=words.rearrange("p (c w u) -> p c w u", w=P, u=2),
+            )
+            u2_sorted[i] = srt
 
         def turn_u2(i, b):
             if b == 0:
@@ -274,16 +205,17 @@ def tile_skconv2d_pa_kernel(tc, xw_bytes, xw_scale, S1s, U1s, U2s, S2s, bias, ou
                         src = words[:, 256 * c + u : 256 * (c + 1) : 2]
                     nc.tensor.transpose(ut[:, s, u, :], src, ident[:])
             dst = u2_grp[i][:, 1024 * b : 1024 * (b + 1)].bitcast(F32)
-            copy = nc.vector.tensor_copy if i == UNITS - 1 and b == V_BANK else nc.scalar.copy
-            copy(out=dst.rearrange("p (s n u) -> p s n u", s=2, u=2), in_=ut[:].rearrange("p s u n -> p s n u"))
+            nc.scalar.copy(
+                out=dst.rearrange("p (s n u) -> p s n u", s=2, u=2), in_=ut[:].rearrange("p s u n -> p s n u")
+            )
             if b == 3:
                 units_turned.append(i)
                 load_more()
 
-        def quant_u2(i, lo=0, hi=8):
+        def quant_u2(i, lo=0, hi=PASSES):
             if lo == 0:
-                codes = pool.tile([P, 8 * P], U32, name="u2_codes", bufs=CODE_UNITS, align_bytes=64)
-                scales = pool.tile([P, 8 * P], U8, name="u2_scales", bufs=CODE_UNITS, align_bytes=64)
+                codes = pool.tile([P, PASSES * P], U32, name="u2_codes", bufs=CODE_UNITS, align_bytes=64)
+                scales = pool.tile([P, PASSES * P], U8, name="u2_scales", bufs=CODE_UNITS, align_bytes=64)
                 u2_codes[i] = (codes, scales)
             codes, scales = u2_codes[i]
             nc.vector.quantize_mx(
@@ -308,29 +240,24 @@ def tile_skconv2d_pa_kernel(tc, xw_bytes, xw_scale, S1s, U1s, U2s, S2s, bias, ou
                 src = w_raw[c][:].rearrange("p (j m r e) -> p m j r e", j=4, r=2, e=2)
                 copy(out=dst[:, 32 * lo : 32 * hi], in_=src[:, 32 * lo : 32 * hi])
 
-        def interleave(copy, n, step=2 * UNITS):
-            landed = sum(1 for u in taken if u + CLAG <= step)
-            n = max(0, min(n, 4 * landed - len(quarters_done)))
-            while n:
-                c, lo = divmod(len(quarters_done), 4)
-                hi = min(lo + n, 4)
-                interleave_part(copy, order[c], lo, hi)
-                quarters_done.extend(range(lo, hi))
-                n -= hi - lo
-                load_more()
+        def interleave(copy, quarters):
+            n, lo = divmod(len(quarters_done), 4)
+            interleave_part(copy, order[n], lo, lo + quarters)
+            quarters_done.extend(range(quarters))
+            load_more()
 
-        def quant_chunks():
-            for n in range(len(chunks_quantised), len(quarters_done) // 4):
-                c = order[n]
-                nc.vector.quantize_mx(out=w_codes[c][:].bitcast(FP8X4), scales=w_scales[c][:], in_=w_grp[c][:])
-                chunks_quantised.append(c)
+        def finish_chunk():
+            interleave(nc.vector.tensor_copy, 4 - len(quarters_done) % 4)
+
+        def quant_chunk():
+            c = order[len(chunks_quantised)]
+            nc.vector.quantize_mx(out=w_codes[c][:].bitcast(FP8X4), scales=w_scales[c][:], in_=w_grp[c][:])
+            chunks_quantised.append(c)
 
         h_bank = {}
         h_grp = {}
         h_codes = [keep.tile([P, N], U32, name="h_codes%d" % g, align_bytes=64) for g in range(5)]
         h_scales = [keep.tile([P, N], U8, name="h_scales%d" % g, align_bytes=64) for g in range(5)]
-        closed = []
-        emptied = []
 
         def multiply(group, t, g, codes, scales, start, stop):
             nc.tensor.matmul_mx(
@@ -351,36 +278,26 @@ def tile_skconv2d_pa_kernel(tc, xw_bytes, xw_scale, S1s, U1s, U2s, S2s, bias, ou
             for g in range(lo, hi):
                 cols = slice(g * P, (g + 1) * P)
                 multiply(group, t, g, codes[:, cols], scales[:, cols], g == 0, g == PASSES - 1)
-            if t % 2 == 1:
-                closed.append((group, t // 2))
 
         def multiply_s1(g):
             for t in range(4):
-                if g == 0 and t % 2 == 0:
+                first = g == 0 and t % 2 == 0
+                if first:
                     h_bank[H1_GROUP, t // 2] = psum.tile([P, 2, N], F32, name="long", bufs=2)
                 cols = slice(t * P, (t + 1) * P)
-                first = g == 0 and t % 2 == 0
-                last = g == PASSES - 1 and t % 2 == 1
-                multiply(H1_GROUP, t, g, w_codes[g][:, cols], w_scales[g][:, cols], first, last)
+                closing = g == PASSES - 1 and t % 2 == 1
+                multiply(H1_GROUP, t, g, w_codes[g][:, cols], w_scales[g][:, cols], first, closing)
 
-        def empty_h():
-            while closed:
-                group, pair = closed.pop(0)
-                if pair == 0:
-                    h_grp[group] = pool.tile([P, N * 4], BF16, name="h_grp", bufs=2, align_bytes=64)
-                nc.scalar.copy(
-                    out=h_grp[group][:].rearrange("p (n t) -> p n t", t=4)[:, :, 2 * pair : 2 * pair + 2],
-                    in_=h_bank[group, pair][:].rearrange("p t n -> p n t"),
-                )
-                if pair == 1:
-                    emptied.append(group)
+        def empty_h(group, pair):
+            if pair == 0:
+                h_grp[group] = pool.tile([P, N * 4], BF16, name="h_grp", bufs=2, align_bytes=64)
+            nc.scalar.copy(
+                out=h_grp[group][:].rearrange("p (n t) -> p n t", t=4)[:, :, 2 * pair : 2 * pair + 2],
+                in_=h_bank[group, pair][:].rearrange("p t n -> p n t"),
+            )
 
-        def quant_h():
-            while emptied:
-                group = emptied.pop(0)
-                nc.vector.quantize_mx(
-                    out=h_codes[group][:].bitcast(FP8X4), scales=h_scales[group][:], in_=h_grp[group][:]
-                )
+        def quant_h(group):
+            nc.vector.quantize_mx(out=h_codes[group][:].bitcast(FP8X4), scales=h_scales[group][:], in_=h_grp[group][:])
 
         acc = []
 
@@ -405,121 +322,88 @@ def tile_skconv2d_pa_kernel(tc, xw_bytes, xw_scale, S1s, U1s, U2s, S2s, bias, ou
         nc.scalar.dma_start(out=x_scale[:], in_=xw_scale.rearrange("o (g p t) -> p (o g) t", p=P, t=4))
         load_x(1, 2)
         load_x(2, 4)
-        if LO == 0:
-            load_u2(0, 0, 2)
-            load_x(4, 8)
-            load_u2(0, 2, 4)
-        elif LO == 1:
-            load_x(4, 8)
-            load_u2(0, 0, 2)
-            load_u2(0, 2, 4)
-        elif LO == 2:
-            load_x(4, 6)
-            load_u2(0, 0, 2)
-            load_x(6, 8)
-            load_u2(0, 2, 4)
+        load_u2(0, 0, D // 2)
+        load_x(4, 8)
+        load_u2(0, D // 2, D)
         load_u2(1)
         load_more()
 
-        for a in range(LEAD + 2):
+        for a in range(4):
             widen_x(a)
-        for a in range(LEAD):
-            turn_x(a)
-        halves = 0
+        turn_x(0)
+        turn_x(1)
         for n in range(2 * HEAD):
-            if n + LEAD < PIECES:
-                turn_x(n + LEAD)
-            if n + LEAD + 2 < PIECES:
-                widen_x(n + LEAD + 2)
-            if n == 2 * HEAD - 1 and not S_SORT:
-                sort_u2(HEAD)
-            if (n + LEAD) % 2 == 0 and len(x_quantised) < 4:
-                quant_x(len(x_quantised))
-            elif n >= Q0 and halves < NH:
-                quant_u2(halves // 2, 4 * (halves % 2), 4 * (halves % 2) + 4)
-                halves += 1
-            if RING2 and n % 2 == RP and n // 2 + AHEAD >= FIRST:
-                load_w(n // 2 + AHEAD - FIRST)
-            for b in range(2 * (n % 2), 2 * (n % 2) + 2):
-                turn_u2(n // 2, b)
-        if S_SORT:
-            sort_u2(HEAD)
+            turn_x(n + 2)
+            if n + 4 < PIECES:
+                widen_x(n + 4)
+            if n % 2 == 0:
+                quant_x(n // 2)
+            elif n < 4:
+                quant_u2(0, 2 * (n - 1), 2 * (n + 1))
+            turn_u2(n // 2, 2 * (n % 2))
+            turn_u2(n // 2, 2 * (n % 2) + 1)
+        sort_u2(HEAD, nc.scalar.copy)
         multiply_u2(0, 0, 4)
-        if halves < 2:
-            quant_u2(0, 4, 8)
-        elif halves == 2:
-            quant_u2(1, 0, 4)
-        if len(x_quantised) < 4:
-            quant_x(3)
+        quant_u2(1, 0, 4)
+        quant_x(3)
 
-        quantised = 1
-        s1_done = 0
-        for i in range(HEAD, UNITS):
-            ready = min(len(chunks_quantised), S1_CHUNKS)
-            last = i == UNITS - 1
-            if i == BIAS_AT:
+        for i in range(HEAD, LAST):
+            if i == BIAS_STEP:
                 nc.sync.dma_start(
                     out=bias_in[:].rearrange("p (a e) -> p a e", a=2),
                     in_=bias.rearrange("(a p e) -> p a e", a=2, e=2),
                 )
-            if RING2 and i + AHEAD - FIRST < S1_CHUNKS:
-                load_w(i + AHEAD - FIRST)
-                load_more()
-            if not last:
-                empty_h()
+            group, pair = divmod((i - 3) // 2, 2)
+            if i % 2 == 0:
+                empty_h(group, pair)
             for b in range(4):
                 turn_u2(i, b)
             if i == HEAD:
-                quant_u2(1, 4, 8)
-            if i == UNITS - 2:
+                quant_u2(1, 4, PASSES)
+                quant_u2(2)
+                sort_u2(i + 1, nc.vector.tensor_copy)
+            elif i < LAST - 1:
+                finish_chunk()
                 quant_u2(i - 1)
-            if not last:
-                interleave(nc.vector.tensor_copy, -len(quarters_done) % 4 or 4, i - 1)
-            if i < UNITS - 2:
+                quant_chunk()
+                if i % 4 == 2:
+                    quant_h(group)
+                sort_u2(i + 1, nc.vector.tensor_copy)
+            else:
                 quant_u2(i - 1)
-                quant_chunks()
-                quant_h()
-                sort_u2(i + 1)
-            elif not last:
-                sort_u2(i + 1)
-                quant_h()
-                quant_chunks()
+                finish_chunk()
+                sort_u2(i + 1, nc.vector.tensor_copy)
+                quant_h(group)
+                quant_chunk()
                 quant_u2(i)
-            if H1_AT <= i < H1_AT + 2 or last:
-                if i < H1_AT + 2:
-                    closed.append((H1_GROUP, i - H1_AT))
-                empty_h()
-                if i == UNITS - 2:
-                    nc.scalar.activation(out=bias2[:], in_=bias_in[:], func=IDENTITY, scale=2.0)
-                    interleave(nc.scalar.copy, S14)
-            elif i < S_STOP:
-                interleave(nc.scalar.copy, S_FIRST if i == HEAD else S12 if i == 12 else S13 if i == 13 else S_ODD if i % 2 else S_EVEN, i)
+            if i < LAST - 1:
+                interleave(nc.scalar.copy, 2 if i == HEAD or i % 4 == 2 else 1)
+            else:
+                empty_h(H1_GROUP, 0)
+                nc.scalar.activation(out=bias2[:], in_=bias_in[:], func=IDENTITY, scale=2.0)
             if i == HEAD:
-                multiply_u2(0, 4, 8)
-            if not last:
-                multiply_u2(i - 2)
-            if i >= UNITS - 2:
-                multiply_u2(i - 1)
-            for g in range(s1_done, ready):
-                multiply_s1(g)
-                s1_done += 1
-        interleave(nc.vector.tensor_copy, V_END)
-        quant_u2(UNITS - 1, 0, 4)
-        interleave(nc.vector.tensor_copy, V_END2)
-        if SPLIT:
-            quant_u2(UNITS - 1, 4, 6)
-            quant_u2(UNITS - 1, 6, 8)
-        else:
-            quant_u2(UNITS - 1, 4, 8)
-        interleave(nc.vector.tensor_copy, -len(quarters_done) % 4)
-        quant_chunks()
-        interleave(nc.scalar.copy, S_END)
-        multiply_u2(UNITS - 1)
-        interleave(nc.vector.tensor_copy, 4 * CHUNKS)
-        quant_h()
-        quant_chunks()
-        empty_h()
-        quant_h()
+                multiply_u2(0, 4, PASSES)
+            multiply_u2(i - 2)
+            if 0 <= i - HEAD - 2 < S1_CHUNKS:
+                multiply_s1(i - HEAD - 2)
+
+        for b in range(4):
+            turn_u2(LAST, b)
+        empty_h(H1_GROUP, 1)
+        multiply_u2(LAST - 2)
+        empty_h(3, 0)
+        multiply_u2(LAST - 1)
+        finish_chunk()
+        quant_u2(LAST, 0, 4)
+        quant_u2(LAST, 4, PASSES)
+        quant_chunk()
+        interleave(nc.scalar.copy, 1)
+        multiply_u2(LAST)
+        finish_chunk()
+        quant_h(H1_GROUP)
+        quant_chunk()
+        empty_h(3, 1)
+        quant_h(3)
         for group in (0, 1, 2, H1_GROUP):
             project(group)
         result = [keep.tile([P, 4, 2, 64], F32, name="result%d" % a, align_bytes=64) for a in range(2)]

@@ -176,7 +176,7 @@ def tile_skconv2d_pa_kernel(tc, xw_bytes, xw_scale, S1s, U1s, U2s, S2s, bias, ou
             if i == HEAD:
                 return 1
             if i == LAST:
-                return 1
+                return 2
             return 3 if i % 2 else 2
 
         def sort_u2(i, copy):

@@ -59,9 +59,9 @@ def tile_skconv2d_pa_kernel(tc, xw_bytes, xw_scale, S1s, U1s, U2s, S2s, bias, ou
         x_rows = xw_bytes.rearrange("(h p) d -> p h d", p=P)
 
         ident_bf = const.tile([P, P], BF16, name="ident_bf", align_bytes=64)
-        make_identity(nc, ident_bf[:])
+        nc.vector.memset(ident_bf[:], 0.0)
+        make_identity(nc, ident_bf[:], nomemset=True)
         ident = const.tile([P, P], F32, name="ident", align_bytes=64)
-        make_identity(nc, ident[:])
         ones = const.tile([P, 1], F32, name="ones", align_bytes=64)
         nc.vector.memset(ones[:], 1.0)
         x_scale = const.tile([P, PASSES, 4], F32, name="x_scale", align_bytes=64)
@@ -330,6 +330,7 @@ def tile_skconv2d_pa_kernel(tc, xw_bytes, xw_scale, S1s, U1s, U2s, S2s, bias, ou
 
         for a in range(4):
             widen_x(a)
+        nc.vector.tensor_copy(out=ident[:], in_=ident_bf[:])
         turn_x(0)
         turn_x(1)
         for n in range(2 * HEAD):

@@ -75,7 +75,7 @@ def tile_skconv2d_pa_kernel(tc, xw_bytes, xw_scale, S1s, U1s, U2s, S2s, bias, ou
         def load_x(lo, hi):
             halves = slice(lo % 2, lo % 2 + 1) if hi - lo == 1 else slice(0, 2)
             width = max(1, (hi - lo) // 2) * 1024
-            t = keep.tile([P, (hi - lo) * 1024], U8, name="x_in%d" % lo, align_bytes=64)
+            t = keep.tile([P, (hi - lo) * 1024], U8, name="x_in%d" % lo, align_bytes=256)
             c = lo // 2 * 1024
             nc.sync.dma_start(out=t[:].rearrange("p (h d) -> p h d", d=width), in_=x_rows[:, halves, c : c + width])
             for a in range(lo, hi):
@@ -84,11 +84,11 @@ def tile_skconv2d_pa_kernel(tc, xw_bytes, xw_scale, S1s, U1s, U2s, S2s, bias, ou
 
         def load_u2(i, lo=0, hi=D):
             if lo == 0:
-                u2_raw[i] = pool.tile([P, D], BF16, name="u2_raw", bufs=RAW_UNITS, align_bytes=64)
+                u2_raw[i] = pool.tile([P, D], BF16, name="u2_raw", bufs=RAW_UNITS, align_bytes=256)
             nc.sync.dma_start(out=u2_raw[i][:, lo:hi], in_=u2_rows[i // 4][:, i % 4, lo:hi])
 
         def load_w(c):
-            raw = pool.tile([P, 2048], BF16, name="w_raw", bufs=RAW_CHUNKS, align_bytes=64)
+            raw = pool.tile([P, 2048], BF16, name="w_raw", bufs=RAW_CHUNKS, align_bytes=256)
             if c < S1_CHUNKS:
                 nc.sync.dma_start(out=raw[:].rearrange("p (t x) -> p t x", t=8), in_=s1_rows[c])
             elif c < U1_CHUNK:
@@ -123,7 +123,7 @@ def tile_skconv2d_pa_kernel(tc, xw_bytes, xw_scale, S1s, U1s, U2s, S2s, bias, ou
         x_codes = keep.tile([P, PASSES * N], U32, name="x_codes", align_bytes=64)
         x_scales = keep.tile([P, PASSES * N], U8, name="x_scales", align_bytes=64)
         x_bf = {}
-        x_grp = [pool.tile([P, 2048], BF16, name="w_raw", bufs=RAW_CHUNKS, align_bytes=64) for b in range(4)]
+        x_grp = [pool.tile([P, 2048], BF16, name="w_raw", bufs=RAW_CHUNKS, align_bytes=256) for b in range(4)]
 
         def widen_x(a):
             if a % 2 == 0:
@@ -407,7 +407,7 @@ def tile_skconv2d_pa_kernel(tc, xw_bytes, xw_scale, S1s, U1s, U2s, S2s, bias, ou
         quant_h(3)
         for group in (0, 1, 2, H1_GROUP):
             project(group)
-        result = [keep.tile([P, 4, 2, 64], F32, name="result%d" % a, align_bytes=64) for a in range(2)]
+        result = [keep.tile([P, 4, 2, 64], F32, name="result%d" % a, align_bytes=256) for a in range(2)]
         out_view = out.rearrange("b (a p e) i j -> a p b (e i j)", a=2, e=2)
         for a in range(2):
             project(3, (a,))

@@ -30,6 +30,7 @@ H1_GROUP = 4
 
 HEAD = 3
 VECTOR_PIECES = 2
+EARLY_PASSES = 4
 TRAILING_CHUNKS = 2
 RAW_UNITS = 7
 RAW_CHUNKS = 6
@@ -58,12 +59,9 @@ def tile_skconv2d_pa_kernel(tc, xw_bytes, xw_scale, S1s, U1s, U2s, S2s, bias, ou
         u1_rows = U1s.rearrange("t r o -> (t r) o").rearrange("(a q i) o -> q a i o", q=4, i=4)
         x_rows = xw_bytes.rearrange("(h p) d -> p h d", p=P)
 
-        ident_bf = const.tile([P, P], BF16, name="ident_bf", align_bytes=64)
-        nc.vector.memset(ident_bf[:], 0.0)
-        make_identity(nc, ident_bf[:], nomemset=True)
         ident = const.tile([P, P], F32, name="ident", align_bytes=64)
-        ones = const.tile([P, 1], F32, name="ones", align_bytes=64)
-        nc.vector.memset(ones[:], 1.0)
+        nc.vector.memset(ident[:], 0.0)
+        make_identity(nc, ident[:], nomemset=True)
         x_scale = const.tile([P, PASSES, 4], F32, name="x_scale", align_bytes=64)
         bias_in = const.tile([P, 4], BF16, name="bias_in", align_bytes=64)
         bias2 = const.tile([P, 4], F32, name="bias2", align_bytes=64)
@@ -73,11 +71,11 @@ def tile_skconv2d_pa_kernel(tc, xw_bytes, xw_scale, S1s, U1s, U2s, S2s, bias, ou
         w_raw = {}
 
         def load_x(lo, hi):
-            halves = slice(lo % 2, lo % 2 + 1) if hi - lo == 1 else slice(0, 2)
-            width = max(1, (hi - lo) // 2) * 1024
-            t = keep.tile([P, (hi - lo) * 1024], U8, name="x_in%d" % lo, align_bytes=256)
-            c = lo // 2 * 1024
-            nc.sync.dma_start(out=t[:].rearrange("p (h d) -> p h d", d=width), in_=x_rows[:, halves, c : c + width])
+            width = (hi - lo) * 512
+            t = keep.tile([P, 2 * width], U8, name="x_in%d" % lo, align_bytes=256)
+            nc.sync.dma_start(
+                out=t[:].rearrange("p (h d) -> p h d", d=width), in_=x_rows[:, :, 512 * lo : 512 * hi]
+            )
             for a in range(lo, hi):
                 at = (a - lo) % 2 * width + (a - lo) // 2 * 1024
                 x_in[a] = t[:, at : at + 1024]
@@ -128,35 +126,22 @@ def tile_skconv2d_pa_kernel(tc, xw_bytes, xw_scale, S1s, U1s, U2s, S2s, bias, ou
         def widen_x(a):
             if a % 2 == 0:
                 x_bf[a // 2] = pool.tile([P, 2048], BF16, name="w_grp", bufs=GRP_CHUNKS, align_bytes=64)
-            wide = x_bf[a // 2][:, a % 2 * 1024 : (a % 2 + 1) * 1024]
-            src = x_in[a].bitcast(FP8)
-            if a < VECTOR_PIECES:
-                nc.vector.tensor_scalar(
-                    out=wide.rearrange("p (s t m) -> p s m t", s=2, t=4),
-                    in0=src.rearrange("p (s m t) -> p s m t", s=2, t=4),
-                    scalar1=ones[:],
-                    scalar2=None,
-                    op0=MULT,
-                )
-            else:
-                nc.scalar.copy(out=wide, in_=src)
+            copy = nc.vector.tensor_copy if a < VECTOR_PIECES else nc.scalar.copy
+            copy(out=x_bf[a // 2][:, a % 2 * 1024 : (a % 2 + 1) * 1024], in_=x_in[a].bitcast(FP8))
 
-        def turn_x(a):
-            wide = x_bf[a // 2][:, a % 2 * 1024 : (a % 2 + 1) * 1024]
-            xt = psum.tile([P, 2, 4, P], BF16, name="long" if a % 2 else "sums", bufs=2)
-            for s in range(2):
-                for t in range(4):
-                    if a < VECTOR_PIECES:
-                        src = wide[:, (4 * s + t) * P : (4 * s + t + 1) * P]
-                    else:
-                        src = wide[:, 512 * s + t : 512 * (s + 1) : 4]
-                    nc.tensor.matmul(xt[:, s, t, :], src, ident_bf[:], start=True, stop=True)
-            b, h = divmod(a, 2)
-            scale = x_scale[:, 2 * b : 2 * b + 2, :].rearrange("p s (o t) -> p s o t", o=1)
+        def turn_x(g):
+            b, s = divmod(g, 2)
+            words = x_bf[b][:].bitcast(F32)
+            xt = psum.tile([P, 2 * N], F32, name="long" if s else "sums", bufs=2)
+            for h in range(2):
+                for u in range(2):
+                    at = 512 * s + 256 * h if g < VECTOR_PIECES else 512 * h + 256 * s
+                    nc.tensor.transpose(xt[:, N * u + P * h : N * u + P * (h + 1)], words[:, at + u : at + 256 : 2], ident[:])
+            scale = x_scale[:, g, :].rearrange("p (o u e) -> p o u e", o=1, u=2)
             nc.vector.tensor_tensor(
-                out=x_grp[b][:].rearrange("p (s h n t) -> p h s n t", s=2, h=2, t=4)[:, h],
-                in0=xt[:].rearrange("p s t n -> p s n t"),
-                in1=scale.to_broadcast([P, 2, P, 4]),
+                out=x_grp[b][:, 1024 * s : 1024 * (s + 1)].rearrange("p (n u e) -> p n u e", u=2, e=2),
+                in0=xt[:].bitcast(BF16).rearrange("p (u n e) -> p n u e", u=2, e=2),
+                in1=scale.to_broadcast([P, N, 2, 2]),
                 op=MULT,
             )
 
@@ -211,6 +196,10 @@ def tile_skconv2d_pa_kernel(tc, xw_bytes, xw_scale, S1s, U1s, U2s, S2s, bias, ou
             if b == 3:
                 units_turned.append(i)
                 load_more()
+
+        def turn_half(n):
+            turn_u2(n // 2, 2 * (n % 2))
+            turn_u2(n // 2, 2 * (n % 2) + 1)
 
         def quant_u2(i, lo=0, hi=PASSES):
             if lo == 0:
@@ -328,25 +317,37 @@ def tile_skconv2d_pa_kernel(tc, xw_bytes, xw_scale, S1s, U1s, U2s, S2s, bias, ou
         load_u2(1)
         load_more()
 
-        for a in range(4):
-            widen_x(a)
-        nc.vector.tensor_copy(out=ident[:], in_=ident_bf[:])
+        widen_x(0)
+        widen_x(1)
+        widen_x(2)
+        widen_x(3)
         turn_x(0)
         turn_x(1)
-        for n in range(2 * HEAD):
-            turn_x(n + 2)
-            if n + 4 < PIECES:
-                widen_x(n + 4)
-            if n % 2 == 0:
-                quant_x(n // 2)
-            elif n < 4:
-                quant_u2(0, 2 * (n - 1), 2 * (n + 1))
-            turn_u2(n // 2, 2 * (n % 2))
-            turn_u2(n // 2, 2 * (n % 2) + 1)
-        sort_u2(HEAD, nc.scalar.copy)
-        multiply_u2(0, 0, 4)
-        quant_u2(1, 0, 4)
+        turn_x(2)
+        quant_x(0)
+        turn_x(3)
+        widen_x(4)
+        widen_x(5)
+        turn_half(0)
+        turn_x(4)
+        quant_x(1)
+        widen_x(6)
+        turn_half(1)
+        turn_x(5)
+        widen_x(7)
+        quant_u2(0, 0, 4)
+        turn_half(2)
+        turn_x(6)
+        quant_x(2)
+        turn_half(3)
+        turn_x(7)
+        quant_u2(0, 4, PASSES)
         quant_x(3)
+        turn_half(4)
+        turn_half(5)
+        sort_u2(HEAD, nc.scalar.copy)
+        multiply_u2(0, 0, EARLY_PASSES)
+        quant_u2(1, 0, 4)
 
         for i in range(HEAD, LAST):
             if i == BIAS_STEP:
@@ -383,7 +384,7 @@ def tile_skconv2d_pa_kernel(tc, xw_bytes, xw_scale, S1s, U1s, U2s, S2s, bias, ou
                 empty_h(H1_GROUP, 0)
                 nc.scalar.activation(out=bias2[:], in_=bias_in[:], func=IDENTITY, scale=2.0)
             if i == HEAD:
-                multiply_u2(0, 4, PASSES)
+                multiply_u2(0, EARLY_PASSES, PASSES)
             multiply_u2(i - 2)
             if 0 <= i - HEAD - 2 < S1_CHUNKS:
                 multiply_s1(i - HEAD - 2)

@@ -126,7 +126,7 @@ def tile_skconv2d_pa_kernel(tc, xw_bytes, xw_scale, S1s, U1s, U2s, S2s, bias, ou
         def widen_x(a):
             if a % 2 == 0:
                 x_bf[a // 2] = pool.tile([P, 2048], BF16, name="w_grp", bufs=GRP_CHUNKS, align_bytes=64)
-            copy = nc.vector.tensor_copy if a < VECTOR_PIECES else nc.scalar.copy
+            copy = nc.vector.tensor_copy if a < VECTOR_PIECES else nc.gpsimd.tensor_copy if a % 2 else nc.scalar.copy
             copy(out=x_bf[a // 2][:, a % 2 * 1024 : (a % 2 + 1) * 1024], in_=x_in[a].bitcast(FP8))
 
         def turn_x(g):
@@ -324,8 +324,8 @@ def tile_skconv2d_pa_kernel(tc, xw_bytes, xw_scale, S1s, U1s, U2s, S2s, bias, ou
         turn_x(0)
         turn_x(1)
         turn_x(2)
-        quant_x(0)
         turn_x(3)
+        quant_x(0)
         widen_x(4)
         widen_x(5)
         turn_half(0)

@@ -308,8 +308,10 @@ def tile_skconv2d_pa_kernel(tc, xw_bytes, xw_scale, S1s, U1s, U2s, S2s, bias, ou
                     )
 
         load_x(0, 1)
-        nc.scalar.dma_start(out=x_scale[:], in_=xw_scale.rearrange("o (g p t) -> p (o g) t", p=P, t=4))
+        scale_rows = xw_scale.rearrange("o (g p t) -> p (o g) t", p=P, t=4)
+        nc.scalar.dma_start(out=x_scale[:, :2], in_=scale_rows[:, :2])
         load_x(1, 2)
+        nc.scalar.dma_start(out=x_scale[:, 2:], in_=scale_rows[:, 2:])
         load_x(2, 4)
         load_u2(0, 0, D // 2)
         load_x(4, 8)
@@ -346,6 +348,7 @@ def tile_skconv2d_pa_kernel(tc, xw_bytes, xw_scale, S1s, U1s, U2s, S2s, bias, ou
         turn_half(4)
         turn_half(5)
         sort_u2(HEAD, nc.scalar.copy)
+        interleave(nc.scalar.copy, 1)
         multiply_u2(0, 0, EARLY_PASSES)
         quant_u2(1, 0, 4)
 

@@ -162,7 +162,7 @@ def tile_skconv2d_pa_kernel(tc, xw_bytes, xw_scale, S1s, U1s, U2s, S2s, bias, ou
                 return 1
             if i == LAST:
                 return 2
-            return 3 if i % 2 else 2
+            return 2
 
         def sort_u2(i, copy):
             k = sorted_banks(i)
@@ -382,7 +382,7 @@ def tile_skconv2d_pa_kernel(tc, xw_bytes, xw_scale, S1s, U1s, U2s, S2s, bias, ou
                 quant_chunk()
                 quant_u2(i)
             if i < LAST - 1:
-                interleave(nc.scalar.copy, 2 if i == HEAD or i % 4 == 2 else 1)
+                interleave(nc.scalar.copy, 2 if i == HEAD else 1)
             else:
                 empty_h(H1_GROUP, 0)
                 nc.scalar.activation(out=bias2[:], in_=bias_in[:], func=IDENTITY, scale=2.0)

@@ -31,6 +31,7 @@ H1_GROUP = 4
 HEAD = 3
 VECTOR_PIECES = 2
 EARLY_PASSES = 4
+LONE_PASSES = 4
 TRAILING_CHUNKS = 2
 RAW_UNITS = 7
 RAW_CHUNKS = 6
@@ -135,7 +136,7 @@ def tile_skconv2d_pa_kernel(tc, xw_bytes, xw_scale, S1s, U1s, U2s, S2s, bias, ou
             xt = psum.tile([P, 2 * N], F32, name="long" if s else "sums", bufs=2)
             for h in range(2):
                 for u in range(2):
-                    at = 512 * s + 256 * h if g < VECTOR_PIECES else 512 * h + 256 * s
+                    at = 512 * s + 256 * h if g < LONE_PASSES else 512 * h + 256 * s
                     nc.tensor.transpose(xt[:, N * u + P * h : N * u + P * (h + 1)], words[:, at + u : at + 256 : 2], ident[:])
             scale = x_scale[:, g, :].rearrange("p (o u e) -> p o u e", o=1, u=2)
             nc.vector.tensor_tensor(
@@ -159,7 +160,7 @@ def tile_skconv2d_pa_kernel(tc, xw_bytes, xw_scale, S1s, U1s, U2s, S2s, bias, ou
             if i < HEAD:
                 return 0
             if i == HEAD:
-                return 1
+                return 2
             if i == LAST:
                 return 2
             return 2
@@ -308,11 +309,10 @@ def tile_skconv2d_pa_kernel(tc, xw_bytes, xw_scale, S1s, U1s, U2s, S2s, bias, ou
                     )
 
         load_x(0, 1)
-        scale_rows = xw_scale.rearrange("o (g p t) -> p (o g) t", p=P, t=4)
-        nc.scalar.dma_start(out=x_scale[:, :2], in_=scale_rows[:, :2])
+        nc.scalar.dma_start(out=x_scale[:], in_=xw_scale.rearrange("o (g p t) -> p (o g) t", p=P, t=4))
         load_x(1, 2)
-        nc.scalar.dma_start(out=x_scale[:, 2:], in_=scale_rows[:, 2:])
-        load_x(2, 4)
+        load_x(2, 3)
+        load_x(3, 4)
         load_u2(0, 0, D // 2)
         load_x(4, 8)
         load_u2(0, D // 2, D)
@@ -326,17 +326,17 @@ def tile_skconv2d_pa_kernel(tc, xw_bytes, xw_scale, S1s, U1s, U2s, S2s, bias, ou
         turn_x(0)
         turn_x(1)
         turn_x(2)
-        turn_x(3)
-        quant_x(0)
         widen_x(4)
         widen_x(5)
         turn_half(0)
+        turn_x(3)
+        quant_x(0)
+        turn_half(1)
         turn_x(4)
         quant_x(1)
         widen_x(6)
-        turn_half(1)
-        turn_x(5)
         widen_x(7)
+        turn_x(5)
         quant_u2(0, 0, 4)
         turn_half(2)
         turn_x(6)
@@ -348,7 +348,6 @@ def tile_skconv2d_pa_kernel(tc, xw_bytes, xw_scale, S1s, U1s, U2s, S2s, bias, ou
         turn_half(4)
         turn_half(5)
         sort_u2(HEAD, nc.scalar.copy)
-        interleave(nc.scalar.copy, 1)
         multiply_u2(0, 0, EARLY_PASSES)
         quant_u2(1, 0, 4)
 

from contextlib import ExitStack

import concourse.mybir as mybir
from concourse.masks import make_identity

F32 = mybir.dt.float32
BF16 = mybir.dt.bfloat16
U32 = mybir.dt.uint32
U8 = mybir.dt.uint8
FP8 = mybir.dt.float8_e4m3fn
FP8X4 = mybir.dt.float8_e4m3fn_x4
MULT = mybir.AluOpType.mult
ADD = mybir.AluOpType.add
IDENTITY = mybir.ActivationFunctionType.Identity

P = 128
N = 256
D = 4096
O = 512
K1 = 512
K2 = 2048
PASSES = D // 512
UNITS = K2 // P
LAST = UNITS - 1
PIECES = 8
S1_CHUNKS = PASSES
U1_CHUNK = 12
CHUNKS = 13
H1_GROUP = 4

HEAD = 3
VECTOR_PIECES = 2
EARLY_PASSES = 4
LONE_PASSES = 4
TRAILING_CHUNKS = 2
RAW_UNITS = 7
RAW_CHUNKS = 6
GRP_CHUNKS = 4
GRP_UNITS = 5
CODE_UNITS = 4
TURN_BANKS = 4
BIAS_STEP = 9

FLOPS = 2 * N * D * (K1 + K2) + 2 * N * (K1 + K2) * O


def tile_skconv2d_pa_kernel(tc, xw_bytes, xw_scale, S1s, U1s, U2s, S2s, bias, out):
    nc = tc.nc

    with ExitStack() as ctx:
        const = ctx.enter_context(tc.tile_pool(name="const", bufs=1))
        keep = ctx.enter_context(tc.tile_pool(name="keep", bufs=1))
        pool = ctx.enter_context(tc.tile_pool(name="pool", bufs=2))
        psum = ctx.enter_context(tc.psum_pool(name="psum", bufs=2))
        ctx.enter_context(tc.manual_schedule())

        u2_rows = U2s.rearrange("t r d -> (t r) d").rearrange("(g p t) d -> g p t d", p=P, t=4)
        s1_rows = S1s.rearrange("t (g p j) r -> g p t (j r)", p=P, j=4)
        s2_rows = S2s.rearrange("t r o -> (t r) o").rearrange("(g p j) o -> g p (j o)", p=P, j=4)
        u1_rows = U1s.rearrange("t r o -> (t r) o").rearrange("(a q i) o -> q a i o", q=4, i=4)
        x_rows = xw_bytes.rearrange("(h p) d -> p h d", p=P)

        ident = const.tile([P, P], F32, name="ident", align_bytes=64)
        nc.vector.memset(ident[:], 0.0)
        make_identity(nc, ident[:], nomemset=True)
        x_scale = const.tile([P, PASSES, 4], F32, name="x_scale", align_bytes=64)
        bias_in = const.tile([P, 4], BF16, name="bias_in", align_bytes=64)
        bias2 = const.tile([P, 4], F32, name="bias2", align_bytes=64)

        u2_raw = {}
        x_in = {}
        w_raw = {}

        def load_x(lo, hi):
            width = (hi - lo) * 512
            t = keep.tile([P, 2 * width], U8, name="x_in%d" % lo, align_bytes=256)
            nc.sync.dma_start(
                out=t[:].rearrange("p (h d) -> p h d", d=width), in_=x_rows[:, :, 512 * lo : 512 * hi]
            )
            for a in range(lo, hi):
                at = (a - lo) % 2 * width + (a - lo) // 2 * 1024
                x_in[a] = t[:, at : at + 1024]

        def load_u2(i, lo=0, hi=D):
            if lo == 0:
                u2_raw[i] = pool.tile([P, D], BF16, name="u2_raw", bufs=RAW_UNITS, align_bytes=256)
            nc.sync.dma_start(out=u2_raw[i][:, lo:hi], in_=u2_rows[i // 4][:, i % 4, lo:hi])

        def load_w(c):
            raw = pool.tile([P, 2048], BF16, name="w_raw", bufs=RAW_CHUNKS, align_bytes=256)
            if c < S1_CHUNKS:
                nc.sync.dma_start(out=raw[:].rearrange("p (t x) -> p t x", t=8), in_=s1_rows[c])
            elif c < U1_CHUNK:
                nc.sync.dma_start(out=raw[:], in_=s2_rows[c - S1_CHUNKS])
            else:
                for q in range(4):
                    nc.sync.dma_start(out=raw[:, q * O : (q + 1) * O], in_=u1_rows[q])
            w_raw[c] = raw

        order = list(range(U1_CHUNK - 1)) + [U1_CHUNK, U1_CHUNK - 1]
        behind = [HEAD + n if n < CHUNKS - TRAILING_CHUNKS else LAST for n in range(CHUNKS)]
        queue = []
        for i in range(2, UNITS):
            queue.append(("unit", i))
            queue.extend(("chunk", n) for n in range(CHUNKS) if behind[n] == i)
        units_turned = []
        quarters_done = []
        chunks_quantised = []
        x_quantised = []

        def load_more():
            while queue:
                kind, n = queue[0]
                if kind == "unit" and n < len(units_turned) + RAW_UNITS:
                    load_u2(n)
                elif kind == "chunk" and n + 4 < len(x_quantised) + len(quarters_done) // 4 + RAW_CHUNKS:
                    load_w(order[n])
                else:
                    return
                queue.pop(0)

        x_codes = keep.tile([P, PASSES * N], U32, name="x_codes", align_bytes=64)
        x_scales = keep.tile([P, PASSES * N], U8, name="x_scales", align_bytes=64)
        x_bf = {}
        x_grp = [pool.tile([P, 2048], BF16, name="w_raw", bufs=RAW_CHUNKS, align_bytes=256) for b in range(4)]

        def widen_x(a):
            if a % 2 == 0:
                x_bf[a // 2] = pool.tile([P, 2048], BF16, name="w_grp", bufs=GRP_CHUNKS, align_bytes=64)
            copy = nc.vector.tensor_copy if a < VECTOR_PIECES else nc.gpsimd.tensor_copy if a % 2 else nc.scalar.copy
            copy(out=x_bf[a // 2][:, a % 2 * 1024 : (a % 2 + 1) * 1024], in_=x_in[a].bitcast(FP8))

        def turn_x(g):
            b, s = divmod(g, 2)
            words = x_bf[b][:].bitcast(F32)
            xt = psum.tile([P, 2 * N], F32, name="long" if s else "sums", bufs=2)
            for h in range(2):
                for u in range(2):
                    at = 512 * s + 256 * h if g < LONE_PASSES else 512 * h + 256 * s
                    nc.tensor.transpose(xt[:, N * u + P * h : N * u + P * (h + 1)], words[:, at + u : at + 256 : 2], ident[:])
            scale = x_scale[:, g, :].rearrange("p (o u e) -> p o u e", o=1, u=2)
            nc.vector.tensor_tensor(
                out=x_grp[b][:, 1024 * s : 1024 * (s + 1)].rearrange("p (n u e) -> p n u e", u=2, e=2),
                in0=xt[:].bitcast(BF16).rearrange("p (u n e) -> p n u e", u=2, e=2),
                in1=scale.to_broadcast([P, N, 2, 2]),
                op=MULT,
            )

        def quant_x(b):
            cols = slice(2 * b * N, (2 * b + 2) * N)
            nc.vector.quantize_mx(out=x_codes[:, cols].bitcast(FP8X4), scales=x_scales[:, cols], in_=x_grp[b][:])
            x_quantised.append(b)
            load_more()

        u2_sorted = {}
        u2_grp = {}
        u2_codes = {}

        def sorted_banks(i):
            if i < HEAD:
                return 0
            if i == HEAD:
                return 2
            if i == LAST:
                return 2
            return 2

        def sort_u2(i, copy):
            k = sorted_banks(i)
            srt = pool.tile([P, 512 * k], F32, name="u2_sorted", bufs=2, align_bytes=64)
            words = u2_raw[i][:].bitcast(F32)[:, (4 - k) * 512 :]
            copy(
                out=srt[:].rearrange("p (c u w) -> p c w u", u=2, w=P),
                in_=words.rearrange("p (c w u) -> p c w u", w=P, u=2),
            )
            u2_sorted[i] = srt

        def turn_u2(i, b):
            if b == 0:
                u2_grp[i] = pool.tile([P, D], BF16, name="u2_grp", bufs=GRP_UNITS, align_bytes=64)
            words = u2_raw[i][:].bitcast(F32)
            ut = psum.tile([P, 2, 2, P], F32, name="turn", bufs=TURN_BANKS)
            first = 4 - sorted_banks(i)
            for s in range(2):
                c = 2 * b + s
                for u in range(2):
                    if b >= first:
                        w = 256 * (c - 2 * first) + P * u
                        src = u2_sorted[i][:, w : w + P]
                    else:
                        src = words[:, 256 * c + u : 256 * (c + 1) : 2]
                    nc.tensor.transpose(ut[:, s, u, :], src, ident[:])
            dst = u2_grp[i][:, 1024 * b : 1024 * (b + 1)].bitcast(F32)
            nc.scalar.copy(
                out=dst.rearrange("p (s n u) -> p s n u", s=2, u=2), in_=ut[:].rearrange("p s u n -> p s n u")
            )
            if b == 3:
                units_turned.append(i)
                load_more()

        def turn_half(n):
            turn_u2(n // 2, 2 * (n % 2))
            turn_u2(n // 2, 2 * (n % 2) + 1)

        def quant_u2(i, lo=0, hi=PASSES):
            if lo == 0:
                codes = pool.tile([P, PASSES * P], U32, name="u2_codes", bufs=CODE_UNITS, align_bytes=64)
                scales = pool.tile([P, PASSES * P], U8, name="u2_scales", bufs=CODE_UNITS, align_bytes=64)
                u2_codes[i] = (codes, scales)
            codes, scales = u2_codes[i]
            nc.vector.quantize_mx(
                out=codes[:, lo * P : hi * P].bitcast(FP8X4),
                scales=scales[:, lo * P : hi * P],
                in_=u2_grp[i][:, lo * 512 : hi * 512],
            )

        w_codes = [keep.tile([P, 512], U32, name="w_codes%d" % c, align_bytes=64) for c in range(CHUNKS)]
        w_scales = [keep.tile([P, 512], U8, name="w_scales%d" % c, align_bytes=64) for c in range(CHUNKS)]
        w_grp = {}

        def interleave_part(copy, c, lo, hi):
            if lo == 0:
                w_grp[c] = pool.tile([P, 2048], BF16, name="w_grp", bufs=GRP_CHUNKS, align_bytes=64)
            if c < S1_CHUNKS:
                dst = w_grp[c][:].rearrange("p (q a i j) -> p a q j i", q=4, i=4, j=4)
                src = w_raw[c][:].rearrange("p (t j m i) -> p t m j i", t=8, j=4, i=4)
                copy(out=dst[:, 8 * lo : 8 * hi], in_=src[:, 2 * lo : 2 * hi])
            else:
                dst = w_grp[c][:].rearrange("p (e m r j) -> p m j r e", e=2, r=2, j=4)
                src = w_raw[c][:].rearrange("p (j m r e) -> p m j r e", j=4, r=2, e=2)
                copy(out=dst[:, 32 * lo : 32 * hi], in_=src[:, 32 * lo : 32 * hi])

        def interleave(copy, quarters):
            n, lo = divmod(len(quarters_done), 4)
            interleave_part(copy, order[n], lo, lo + quarters)
            quarters_done.extend(range(quarters))
            load_more()

        def finish_chunk():
            interleave(nc.vector.tensor_copy, 4 - len(quarters_done) % 4)

        def quant_chunk():
            c = order[len(chunks_quantised)]
            nc.vector.quantize_mx(out=w_codes[c][:].bitcast(FP8X4), scales=w_scales[c][:], in_=w_grp[c][:])
            chunks_quantised.append(c)

        h_bank = {}
        h_grp = {}
        h_codes = [keep.tile([P, N], U32, name="h_codes%d" % g, align_bytes=64) for g in range(5)]
        h_scales = [keep.tile([P, N], U8, name="h_scales%d" % g, align_bytes=64) for g in range(5)]

        def multiply(group, t, g, codes, scales, start, stop):
            nc.tensor.matmul_mx(
                out=h_bank[group, t // 2][:, t % 2, :],
                lhsT=codes.bitcast(FP8X4),
                lhsT_scale=scales,
                rhs=x_codes[:, g * N : (g + 1) * N].bitcast(FP8X4),
                rhs_scale=x_scales[:, g * N : (g + 1) * N],
                start=start,
                stop=stop,
            )

        def multiply_u2(i, lo=0, hi=PASSES):
            group, t = divmod(i, 4)
            if t % 2 == 0 and lo == 0:
                h_bank[group, t // 2] = psum.tile([P, 2, N], F32, name="sums", bufs=2)
            codes, scales = u2_codes[i]
            for g in range(lo, hi):
                cols = slice(g * P, (g + 1) * P)
                multiply(group, t, g, codes[:, cols], scales[:, cols], g == 0, g == PASSES - 1)

        def multiply_s1(g):
            for t in range(4):
                first = g == 0 and t % 2 == 0
                if first:
                    h_bank[H1_GROUP, t // 2] = psum.tile([P, 2, N], F32, name="long", bufs=2)
                cols = slice(t * P, (t + 1) * P)
                closing = g == PASSES - 1 and t % 2 == 1
                multiply(H1_GROUP, t, g, w_codes[g][:, cols], w_scales[g][:, cols], first, closing)

        def empty_h(group, pair):
            if pair == 0:
                h_grp[group] = pool.tile([P, N * 4], BF16, name="h_grp", bufs=2, align_bytes=64)
            nc.scalar.copy(
                out=h_grp[group][:].rearrange("p (n t) -> p n t", t=4)[:, :, 2 * pair : 2 * pair + 2],
                in_=h_bank[group, pair][:].rearrange("p t n -> p n t"),
            )

        def quant_h(group):
            nc.vector.quantize_mx(out=h_codes[group][:].bitcast(FP8X4), scales=h_scales[group][:], in_=h_grp[group][:])

        acc = []

        def project(group, pairs=(0, 1)):
            c = S1_CHUNKS + group
            for a in pairs:
                for e in range(2):
                    if group == 0:
                        acc.append(psum.tile([P, 512], F32, name="turn", bufs=TURN_BANKS))
                    cols = slice(256 * e + P * a, 256 * e + P * (a + 1))
                    nc.tensor.matmul_mx(
                        out=acc[2 * a + e][:, :N],
                        lhsT=w_codes[c][:, cols].bitcast(FP8X4),
                        lhsT_scale=w_scales[c][:, cols],
                        rhs=h_codes[group][:].bitcast(FP8X4),
                        rhs_scale=h_scales[group][:],
                        start=group == 0,
                        stop=group == 3,
                    )

        load_x(0, 1)
        nc.scalar.dma_start(out=x_scale[:], in_=xw_scale.rearrange("o (g p t) -> p (o g) t", p=P, t=4))
        load_x(1, 2)
        load_x(2, 3)
        load_x(3, 4)
        load_u2(0, 0, D // 2)
        load_x(4, 8)
        load_u2(0, D // 2, D)
        load_u2(1)
        load_more()

        widen_x(0)
        widen_x(1)
        widen_x(2)
        widen_x(3)
        turn_x(0)
        turn_x(1)
        turn_x(2)
        widen_x(4)
        widen_x(5)
        turn_half(0)
        turn_x(3)
        quant_x(0)
        turn_half(1)
        turn_x(4)
        quant_x(1)
        widen_x(6)
        widen_x(7)
        turn_x(5)
        quant_u2(0, 0, 4)
        turn_half(2)
        turn_x(6)
        quant_x(2)
        turn_half(3)
        turn_x(7)
        quant_u2(0, 4, PASSES)
        quant_x(3)
        turn_half(4)
        turn_half(5)
        sort_u2(HEAD, nc.scalar.copy)
        multiply_u2(0, 0, EARLY_PASSES)
        quant_u2(1, 0, 4)

        for i in range(HEAD, LAST):
            if i == BIAS_STEP:
                nc.sync.dma_start(
                    out=bias_in[:].rearrange("p (a e) -> p a e", a=2),
                    in_=bias.rearrange("(a p e) -> p a e", a=2, e=2),
                )
            group, pair = divmod((i - 3) // 2, 2)
            if i % 2 == 0:
                empty_h(group, pair)
            for b in range(4):
                turn_u2(i, b)
            if i == HEAD:
                quant_u2(1, 4, PASSES)
                quant_u2(2)
                sort_u2(i + 1, nc.vector.tensor_copy)
            elif i < LAST - 1:
                finish_chunk()
                quant_u2(i - 1)
                quant_chunk()
                if i % 4 == 2:
                    quant_h(group)
                sort_u2(i + 1, nc.vector.tensor_copy)
            else:
                quant_u2(i - 1)
                finish_chunk()
                sort_u2(i + 1, nc.vector.tensor_copy)
                quant_h(group)
                quant_chunk()
                quant_u2(i)
            if i < LAST - 1:
                interleave(nc.scalar.copy, 2 if i == HEAD else 1)
            else:
                empty_h(H1_GROUP, 0)
                nc.scalar.activation(out=bias2[:], in_=bias_in[:], func=IDENTITY, scale=2.0)
            if i == HEAD:
                multiply_u2(0, EARLY_PASSES, PASSES)
            multiply_u2(i - 2)
            if 0 <= i - HEAD - 2 < S1_CHUNKS:
                multiply_s1(i - HEAD - 2)

        for b in range(4):
            turn_u2(LAST, b)
        empty_h(H1_GROUP, 1)
        multiply_u2(LAST - 2)
        empty_h(3, 0)
        multiply_u2(LAST - 1)
        finish_chunk()
        quant_u2(LAST, 0, 4)
        quant_u2(LAST, 4, PASSES)
        quant_chunk()
        interleave(nc.scalar.copy, 1)
        multiply_u2(LAST)
        finish_chunk()
        quant_h(H1_GROUP)
        quant_chunk()
        empty_h(3, 1)
        quant_h(3)
        for group in (0, 1, 2, H1_GROUP):
            project(group)
        result = [keep.tile([P, 4, 2, 64], F32, name="result%d" % a, align_bytes=256) for a in range(2)]
        out_view = out.rearrange("b (a p e) i j -> a p b (e i j)", a=2, e=2)
        for a in range(2):
            project(3, (a,))
            even, odd = (acc[2 * a + e][:, :N].rearrange("p (b s) -> p b s", b=4) for e in range(2))
            nc.scalar.activation(
                out=result[a][:, :, 0, :], in_=even, func=IDENTITY, bias=bias2[:, 2 * a : 2 * a + 1], scale=0.125
            )
            nc.vector.tensor_scalar(
                out=result[a][:, :, 1, :],
                in0=odd,
                scalar1=0.125,
                scalar2=bias2[:, 2 * a + 1 : 2 * a + 2],
                op0=MULT,
                op1=ADD,
            )
            nc.sync.dma_start(out=out_view[a], in_=result[a][:].rearrange("p b e s -> p b (e s)"))
